import numpy as np
import ml_dtypes


def mxq(x, axis, fmt="e4m3"):
    dtype, down = {"e4m3": (ml_dtypes.float8_e4m3fn, 7), "e5m2": (ml_dtypes.float8_e5m2, 14)}[fmt]
    v = np.moveaxis(np.asarray(x, np.float32).astype(ml_dtypes.bfloat16).astype(np.float64), axis, -1)
    blocks = v.reshape(v.shape[:-1] + (-1, 32))
    amax = np.abs(blocks).max(-1, keepdims=True)
    byte = np.maximum(np.where(amax > 0, np.frexp(amax)[1] - 1 + 127, 0) - down, 1)
    scale = np.exp2(byte - 127.0)
    codes = (blocks / scale).astype(np.float32).astype(dtype).astype(np.float64)
    return np.moveaxis((codes * scale).reshape(v.shape), -1, axis)


WIDE = False


def mx_kscale(k):
    if not WIDE:
        return np.ones(k)
    levels = np.array([10, -10, 5, -5, 0])
    a = np.random.permutation(np.resize(levels, k // 512 * 4)).reshape(k // 512, 4)
    idx = np.arange(k)
    return np.exp2(a[idx // 512, idx % 128 // 32])


BF16 = ml_dtypes.bfloat16


def bf(x):
    return np.asarray(x, np.float32).astype(BF16)


def f64(x):
    return np.asarray(x).astype(np.float64)


E2M1 = np.array([0.0, 0.5, 1.0, 1.5, 2.0, 3.0, 4.0, 6.0, -0.0, -0.5, -1.0, -1.5, -2.0, -3.0, -4.0, -6.0])


def pack_weight(w, fmt):
    k, n = w.shape
    w = f64(bf(w)).reshape(k // 32, 32, n)
    amax = np.abs(w).max(1)
    if fmt == "e4m3":
        byte = np.frexp(amax)[1] - 1 + 127 - 7
    else:
        mant, ex = np.frexp(amax / 6.0)
        byte = np.where(mant > 0.5, ex, ex - 1) + 127
    byte = np.clip(np.where(amax > 0, byte, 1), 1, 254)
    scaled = (w * np.exp2(127.0 - byte)[:, None, :]).reshape(k, n).astype(np.float32)
    by_word = np.ascontiguousarray(scaled.reshape(k // 512, 128, 4, n).transpose(0, 1, 3, 2))
    if fmt == "e4m3":
        words = by_word.astype(ml_dtypes.float8_e4m3fn).view(np.uint8)
    else:
        c = by_word.astype(ml_dtypes.float4_e2m1fn).view(np.uint8) & 0xF
        words = c[..., 0::2] | (c[..., 1::2] << 4)
    return np.ascontiguousarray(words), np.ascontiguousarray(byte.astype(np.uint8).reshape(k // 512, 16, n))


def unpack_weight(words, scales, fmt):
    g, p, n, _ = words.shape
    if fmt == "e4m3":
        vals = np.ascontiguousarray(words).view(ml_dtypes.float8_e4m3fn).astype(np.float64)
    else:
        nib = np.empty((g, p, n, 4), np.uint8)
        nib[..., 0::2] = words & 0xF
        nib[..., 1::2] = words >> 4
        vals = E2M1[nib]
    vals = vals * np.repeat(np.exp2(scales.astype(np.float64) - 127.0), 8, axis=1)[..., None]
    return vals.transpose(0, 1, 3, 2).reshape(g * 512, n)


B, K, N, T = 256, 2048, 2048, 8
EPS = 1e-7
MAX_NORM = 1.0 - 1e-5


def _n(x):
    return np.maximum(np.sqrt(np.sum(x * x, axis=-1, keepdims=True)), EPS)


def _artanh(x):
    c = np.clip(x, -1.0 + 1e-5, 1.0 - 1e-5)
    return 0.5 * np.log((1.0 + c) / (1.0 - c))


def _project(x):
    n = _n(x)
    return x * np.where(n > MAX_NORM, MAX_NORM / n, 1.0)


def _mobius_add(x, y):
    x2 = np.sum(x * x, axis=-1, keepdims=True)
    y2 = np.sum(y * y, axis=-1, keepdims=True)
    xy = np.sum(x * y, axis=-1, keepdims=True)
    num = (1.0 + 2.0 * xy + y2) * x + (1.0 - x2) * y
    den = np.maximum(1.0 + 2.0 * xy + x2 * y2, EPS)
    return num / den


def setup_inputs():
    s = mx_kscale(K)
    g = np.sqrt(np.mean(s * s))
    m = np.random.standard_normal(K)
    w0 = np.random.standard_normal((N, K)) * 1.5 / np.sqrt(N)
    u = w0 @ m
    u = u / _n(u)
    v = (np.random.standard_normal((B, K)) + m) * s
    v = 0.7 * v / (1.0 + _n(v))
    z0 = np.random.standard_normal((B, N)) + np.random.standard_normal((B, 1)) * np.sqrt(N) * u
    z0 = 0.5 * z0 / (1.0 + _n(z0))
    b = 0.45 * (0.7 * u + 0.7 * np.random.standard_normal(N) / np.sqrt(N))
    step_sizes = np.log(2.0 / T) + 0.1 * np.random.standard_normal(1)
    W_words, W_scales = pack_weight((w0 * g / s).T, 'e4m3')
    return {'z_0': bf(z0), 'v_init': bf(v), 'W_words': W_words, 'W_scales': W_scales, 'b': bf(b), 'step_sizes': bf(step_sizes)}


def reference(z_0, v_init, W_words, W_scales, b, step_sizes):
    z_0, v_init, b, step_sizes = f64(z_0), f64(v_init), f64(b), f64(step_sizes)
    step = 1.0 / (1.0 + np.exp(-step_sizes))
    mv = mxq(v_init, 1, 'e4m3') @ unpack_weight(W_words, W_scales, 'e4m3')
    vn, mvn = _n(v_init), _n(mv)
    res = np.tanh(mvn / vn * _artanh(vn)) * mv / mvn
    bn = _n(b)
    b_pt = np.tanh(bn) * b / bn
    v0 = _project(_mobius_add(res, b_pt))
    ts = np.arange(1.0, T + 1.0)
    v_t = step * ts[None, :, None] * v0[:, None, :]
    x = z_0[:, None, :]
    lam = 2.0 / np.maximum(1.0 - np.sum(x * x, axis=-1, keepdims=True), EPS)
    vtn = _n(v_t)
    second = np.tanh(0.5 * lam * vtn) * v_t / vtn
    return _project(_mobius_add(x, second))

@@ -1,0 +1,478 @@
+from contextlib import ExitStack
+
+import concourse.mybir as mybir
+from concourse.masks import make_identity
+
+F32 = mybir.dt.float32
+BF16 = mybir.dt.bfloat16
+I32 = mybir.dt.int32
+U32 = mybir.dt.uint32
+U8 = mybir.dt.uint8
+FP8X4 = mybir.dt.float8_e4m3fn_x4
+ALU = mybir.AluOpType
+ACT = mybir.ActivationFunctionType
+AX = mybir.AxisListType
+
+P = 128
+B, K, N, T = 256, 2048, 2048, 8
+ROW_BLOCKS = B // P
+PACK = 4
+K_PASS = P * PACK
+PASSES = K // K_PASS
+N_TILE = 512
+N_TILES = N // N_TILE
+HALF = N // 2
+
+EPS = 1e-7
+EPS_SQ = 1e-14
+TINY = 1e-24
+MAX_NORM = 1.0 - 1e-5
+
+FLOPS = 2 * B * K * N
+
+
+def tile_paralleldirectpoincaredynamics_kernel(
+    tc, z_0, v_init, W_words, W_scales, b, step_sizes, out
+):
+    nc = tc.nc
+    with ExitStack() as ctx:
+        keep = ctx.enter_context(tc.tile_pool(name="keep", bufs=1))
+        small = ctx.enter_context(tc.tile_pool(name="small", bufs=1))
+        stream = ctx.enter_context(tc.tile_pool(name="stream", bufs=6))
+        psum = ctx.enter_context(tc.psum_pool(name="psum", bufs=8))
+        ctx.enter_context(tc.manual_schedule())
+
+        def per_row(name, width=ROW_BLOCKS):
+            return small.tile([P, width], F32, name=name)
+
+        def per_horizon(name):
+            return small.tile([P, ROW_BLOCKS, T], F32, name=name)
+
+        def col(scalars, r):
+            return scalars[:, r : r + 1]
+
+        def tile_cols(j):
+            return slice(j * N_TILE, (j + 1) * N_TILE)
+
+        blocks = range(ROW_BLOCKS)
+        last = N_TILES - 1
+
+        w_planes = keep.tile([P, N], U8, align_bytes=64)
+        b_row = keep.tile([P, N], BF16)
+        ones = keep.tile([P, P], BF16)
+        ones_f32 = keep.tile([P, P], F32)
+        one_col = per_row("one_col", 1)
+        plus_half = per_row("plus_half")
+        minus_half = per_row("minus_half")
+        horizon = per_row("horizon", T)
+        b_sq_part = per_row("b_sq_part")
+        ident = keep.tile([P, P], F32)
+        nc.vector.memset(b_row[:].bitcast(I32), 0)
+        nc.vector.memset(ones[:], 1.0)
+        nc.vector.memset(one_col[:], 1.0)
+        nc.vector.memset(w_planes[:].bitcast(I32), 0)
+        nc.vector.memset(ones_f32[:], 1.0)
+        nc.vector.memset(b_sq_part[:], 0.0)
+        nc.vector.memset(plus_half[:], 0.5)
+        nc.vector.memset(minus_half[:], -0.5)
+        for t in range(T):
+            nc.vector.memset(horizon[:, t : t + 1], float(t + 1))
+        make_identity(nc, ident[:])
+
+        step_raw = small.tile([P, 1], BF16)
+        b_cols = small.tile([P, N // P], BF16)
+        nc.scalar.dma_start(out=b_row[0:1, :], in_=b.rearrange("(o n) -> o n", o=1))
+        nc.scalar.dma_start(out=b_cols[:], in_=b.rearrange("(p c) -> p c", p=P))
+        nc.scalar.dma_start(out=step_raw[:], in_=step_sizes.partition_broadcast(P))
+
+        v_sb = keep.tile([P, ROW_BLOCKS, K], BF16)
+        z_sb = keep.tile([P, ROW_BLOCKS, N], BF16)
+        for r in blocks:
+            nc.sync.dma_start(out=v_sb[:, r, :], in_=v_init[r * P : (r + 1) * P, :])
+            nc.sync.dma_start(out=z_sb[:, r, :], in_=z_0[r * P : (r + 1) * P, :])
+        for quad in range(4):
+            nc.sync.dma_start(
+                out=w_planes[32 * quad : 32 * quad + 16, :].bitcast(I32),
+                in_=W_scales[:, 4 * quad : 4 * quad + 4, :].bitcast(I32),
+            )
+        w_words = keep.tile([P, PASSES, N], I32, align_bytes=64)
+        w_bytes = W_words.rearrange("g p n t -> p g (n t)")
+        for j in range(N_TILES):
+            nc.sync.dma_start(
+                out=w_words[:, :, tile_cols(j)],
+                in_=w_bytes[:, :, j * N_TILE * PACK : (j + 1) * N_TILE * PACK].bitcast(I32),
+            )
+
+        squares = keep.tile([P, N], BF16)
+        products = keep.tile([P, N], F32)
+        b_bc = keep.tile([P, N], BF16)
+        v_sq = per_row("v_sq")
+        z_sq = per_row("z_sq")
+        z_dot_b = per_row("z_dot_b")
+        grouped = keep.tile([P, ROW_BLOCKS, PASSES * P * PACK], BF16, align_bytes=64)
+        v_codes = keep.tile([P, ROW_BLOCKS, PASSES * P], U32, align_bytes=64)
+        v_planes = keep.tile([P, ROW_BLOCKS, PASSES * P], U8, align_bytes=64)
+        mv = [[None] * N_TILES for r in blocks]
+        mv_sq_parts = small.tile([P, ROW_BLOCKS, N_TILES], F32)
+        mv_dot_b_parts = small.tile([P, ROW_BLOCKS, N_TILES], F32)
+        mv_dot_z_parts = small.tile([P, ROW_BLOCKS, N_TILES], F32)
+        u_sb = keep.tile([P, ROW_BLOCKS, N], F32)
+        rho = per_row("rho")
+
+        def square_rows(rows, total):
+            nc.scalar.activation(out=squares[:], in_=rows, func=ACT.Square, accum_out=total)
+
+        def dot_z_b(r):
+            nc.vector.scalar_tensor_tensor(
+                out=products[:], in0=z_sb[:, r, :], scalar=1.0, in1=b_bc[:],
+                op0=ALU.mult, op1=ALU.mult, accum_out=col(z_dot_b, r),
+            )
+
+        def turn_v(r):
+            v_pairs = v_sb[:, r, :].bitcast(F32)
+            for h in range(2):
+                turned = psum.tile([P, 2, 2, P], F32, tag="bank")
+                for i in range(2):
+                    g = 2 * h + i
+                    for u in range(2):
+                        nc.tensor.transpose(
+                            turned[:, i, u, :], v_pairs[:, 256 * g + u : 256 * (g + 1) : 2], ident[:]
+                        )
+                nc.scalar.copy(
+                    out=grouped[:, r, h * 1024 : (h + 1) * 1024]
+                    .bitcast(F32)
+                    .rearrange("p (i b u) -> p i b u", i=2, u=2),
+                    in_=turned[:].rearrange("p i u b -> p i b u"),
+                )
+
+        def quantise_v(r):
+            nc.vector.quantize_mx(
+                out=v_codes[:, r, :].bitcast(FP8X4), scales=v_planes[:, r, :], in_=grouped[:, r, :]
+            )
+
+        def multiply(j, r):
+            acc = psum.tile([P, N_TILE], F32, tag="bank", name="mv_%d_%d" % (r, j))
+            mv[r][j] = acc
+            for g in range(PASSES):
+                rows = slice(g * P, (g + 1) * P)
+                nc.tensor.matmul_mx(
+                    out=acc[:],
+                    lhsT=v_codes[:, r, rows].bitcast(FP8X4),
+                    lhsT_scale=v_planes[:, r, rows],
+                    rhs=w_words[:, g, tile_cols(j)].bitcast(FP8X4),
+                    rhs_scale=w_planes[4 * g : P, tile_cols(j)],
+                    start=(g == 0),
+                    stop=(g == PASSES - 1),
+                )
+
+        def square_mv(j, r):
+            nc.scalar.activation(
+                out=squares[:, tile_cols(j)], in_=mv[r][j][:], func=ACT.Square,
+                accum_out=mv_sq_parts[:, r, j : j + 1],
+            )
+
+        def dot_mv(j, r, other, parts):
+            nc.vector.scalar_tensor_tensor(
+                out=products[:, tile_cols(j)], in0=mv[r][j][:], scalar=1.0, in1=other,
+                op0=ALU.mult, op1=ALU.mult, accum_out=parts[:, r, j : j + 1],
+            )
+
+        def dot_mv_b(j, r):
+            dot_mv(j, r, b_bc[:, tile_cols(j)], mv_dot_b_parts)
+
+        def dot_mv_z(j, r):
+            dot_mv(j, r, z_sb[:, r, tile_cols(j)], mv_dot_z_parts)
+
+        def make_u(r, j):
+            nc.vector.scalar_tensor_tensor(
+                out=u_sb[:, r, tile_cols(j)], in0=b_bc[:, tile_cols(j)], scalar=col(rho, r),
+                in1=mv[r][j][:], op0=ALU.mult, op1=ALU.add,
+            )
+
+        warm = per_row("warm", 1)
+        nc.scalar.activation(out=warm[:], in_=one_col[:], func=ACT.Ln)
+        for h in range(2):
+            spread = psum.tile([P, HALF], BF16, tag="bank")
+            for i in range(HALF // N_TILE):
+                nc.tensor.matmul(
+                    out=spread[:, tile_cols(i)], lhsT=ones[:], rhs=b_row[:, tile_cols(2 * h + i)],
+                    start=True, stop=True,
+                )
+            nc.scalar.copy(out=b_bc[:, h * HALF : (h + 1) * HALF], in_=spread[:])
+        nc.scalar.activation(
+            out=squares[:, 0 : N // P], in_=b_cols[:], func=ACT.Square, accum_out=b_sq_part[:, 0:1]
+        )
+        b_sq_ps = psum.tile([P, ROW_BLOCKS], F32, tag="bank")
+        nc.tensor.matmul(out=b_sq_ps[:], lhsT=ones_f32[:], rhs=b_sq_part[:], start=True, stop=True)
+
+        turn_v(0)
+        square_rows(v_sb[:, 0, :], col(v_sq, 0))
+        turn_v(1)
+        square_rows(v_sb[:, 1, :], col(v_sq, 1))
+        dot_z_b(0)
+        quantise_v(0)
+        dot_z_b(1)
+        quantise_v(1)
+        for j in range(N_TILES):
+            for r in blocks:
+                multiply(j, r)
+
+        b_sq = per_row("b_sq", 1)
+        b_sq_c = per_row("b_sq_c", 1)
+        b_norm = per_row("b_norm", 1)
+        b_tanh = per_row("b_tanh", 1)
+        b_rnorm = per_row("b_rnorm", 1)
+        beta = per_row("beta", 1)
+        minus_beta = per_row("minus_beta", 1)
+        two_beta = per_row("two_beta", 1)
+        y2 = per_row("y2", 1)
+        y2_minus_1 = per_row("y2_minus_1", 1)
+        v_sq_c = per_row("v_sq_c")
+        v_norm = per_row("v_norm")
+        v_clip = per_row("v_clip")
+        ln_plus = per_row("ln_plus")
+        ln_minus = per_row("ln_minus")
+        ln_diff = per_row("ln_diff")
+        v_rnorm = per_row("v_rnorm")
+        gain = per_row("gain")
+        step = per_row("step", 1)
+        tau = per_row("tau", T)
+        nc.vector.tensor_copy(out=b_sq[:], in_=b_sq_ps[:, 0:1])
+        nc.vector.tensor_scalar_max(out=v_sq_c[:], in0=v_sq[:], scalar1=EPS_SQ)
+        nc.vector.tensor_scalar_max(out=b_sq_c[:], in0=b_sq[:], scalar1=EPS_SQ)
+        nc.gpsimd.tensor_tensor(out=v_norm[:], in0=v_sq_c[:], in1=plus_half[:], op=ALU.pow)
+        nc.gpsimd.tensor_tensor(out=b_norm[:], in0=b_sq_c[:], in1=plus_half[:, 0:1], op=ALU.pow)
+
+        for r in blocks:
+            square_mv(0, r)
+            dot_mv_b(0, r)
+        nc.vector.tensor_scalar_min(out=v_clip[:], in0=v_norm[:], scalar1=MAX_NORM)
+        nc.vector.reciprocal(out=v_rnorm[:], in_=v_norm[:])
+        nc.vector.reciprocal(out=b_rnorm[:], in_=b_norm[:])
+        nc.scalar.activation(out=ln_plus[:], in_=v_clip[:], func=ACT.Ln, bias=one_col[:], scale=1.0)
+        nc.scalar.activation(out=ln_minus[:], in_=v_clip[:], func=ACT.Ln, bias=one_col[:], scale=-1.0)
+        nc.scalar.activation(out=step[:], in_=step_raw[:], func=ACT.Sigmoid)
+        nc.scalar.activation(out=b_tanh[:], in_=b_norm[:], func=ACT.Tanh)
+        for r in blocks:
+            dot_mv_z(0, r)
+        for r in blocks:
+            square_mv(1, r)
+            dot_mv_b(1, r)
+        square_rows(z_sb[:, 0, :], col(z_sq, 0))
+        nc.vector.tensor_sub(out=ln_diff[:], in0=ln_plus[:], in1=ln_minus[:])
+        nc.vector.tensor_scalar_mul(out=tau[:], in0=horizon[:], scalar1=step[:])
+        nc.vector.tensor_mul(out=beta[:], in0=b_tanh[:], in1=b_rnorm[:])
+        nc.vector.scalar_tensor_tensor(
+            out=gain[:], in0=ln_diff[:], scalar=0.5, in1=v_rnorm[:], op0=ALU.mult, op1=ALU.mult
+        )
+        nc.vector.tensor_scalar_mul(out=two_beta[:], in0=beta[:], scalar1=2.0)
+        nc.vector.tensor_scalar_mul(out=minus_beta[:], in0=beta[:], scalar1=-1.0)
+        nc.vector.tensor_scalar(
+            out=y2[:], in0=beta[:], scalar1=beta[:], scalar2=b_sq[:], op0=ALU.mult, op1=ALU.mult
+        )
+        nc.vector.tensor_scalar_add(out=y2_minus_1[:], in0=y2[:], scalar1=-1.0)
+        for r in blocks:
+            dot_mv_z(1, r)
+        for r in blocks:
+            square_mv(2, r)
+            dot_mv_b(2, r)
+        mv_sq_head = per_row("mv_sq_head")
+        mv_dot_b_head = per_row("mv_dot_b_head")
+        nc.vector.tensor_reduce(out=mv_sq_head[:], in_=mv_sq_parts[:, :, 0:last], axis=AX.X, op=ALU.add)
+        nc.vector.tensor_reduce(out=mv_dot_b_head[:], in_=mv_dot_b_parts[:, :, 0:last], axis=AX.X, op=ALU.add)
+        for r in blocks:
+            square_mv(last, r)
+            dot_mv_b(last, r)
+
+        mv_sq_c = per_row("mv_sq_c")
+        mv_rnorm = per_row("mv_rnorm")
+        mv_sq_gain = per_row("mv_sq_gain")
+        mv_dot_b = per_row("mv_dot_b")
+        mv_dot_2bpt = per_row("mv_dot_2bpt")
+        two_xy_unit = per_row("two_xy_unit")
+        x_norm = per_row("x_norm")
+        for r in blocks:
+            nc.vector.tensor_scalar(
+                out=col(mv_sq_c, r), in0=mv_sq_parts[:, r, last : last + 1], scalar1=col(mv_sq_head, r),
+                scalar2=EPS_SQ, op0=ALU.add, op1=ALU.max,
+            )
+        nc.gpsimd.tensor_tensor(out=mv_rnorm[:], in0=mv_sq_c[:], in1=minus_half[:], op=ALU.pow)
+        nc.vector.tensor_mul(out=mv_sq_gain[:], in0=mv_sq_c[:], in1=gain[:])
+        nc.vector.tensor_add(out=mv_dot_b[:], in0=mv_dot_b_parts[:, :, last], in1=mv_dot_b_head[:])
+        nc.vector.tensor_scalar_mul(out=mv_dot_2bpt[:], in0=mv_dot_b[:], scalar1=two_beta[:])
+        dot_mv_z(2, 0)
+        for r in blocks:
+            nc.scalar.activation(
+                out=col(x_norm, r), in_=col(mv_rnorm, r), func=ACT.Tanh, scale=col(mv_sq_gain, r)
+            )
+        square_rows(z_sb[:, 1, :], col(z_sq, 1))
+        nc.vector.tensor_mul(out=two_xy_unit[:], in0=mv_rnorm[:], in1=mv_dot_2bpt[:])
+        dot_mv_z(2, 1)
+        one_plus_2xy = per_row("one_plus_2xy")
+        x2 = per_row("x2")
+        den_raw = per_row("den_raw")
+        sum_sq = per_row("sum_sq")
+        num_sq = per_row("num_sq")
+        num_norm = per_row("num_norm")
+        den = per_row("den")
+        rden = per_row("rden")
+        for r in blocks:
+            nc.vector.tensor_scalar(
+                out=col(one_plus_2xy, r), in0=col(x_norm, r), scalar1=col(two_xy_unit, r), scalar2=1.0,
+                op0=ALU.mult, op1=ALU.add,
+            )
+        nc.vector.tensor_mul(out=x2[:], in0=x_norm[:], in1=x_norm[:])
+        nc.vector.scalar_tensor_tensor(
+            out=den_raw[:], in0=x2[:], scalar=y2[:], in1=one_plus_2xy[:], op0=ALU.mult, op1=ALU.add
+        )
+        nc.vector.scalar_tensor_tensor(
+            out=sum_sq[:], in0=x2[:], scalar=y2_minus_1[:], in1=one_plus_2xy[:], op0=ALU.add, op1=ALU.add
+        )
+        nc.vector.scalar_tensor_tensor(
+            out=num_sq[:], in0=sum_sq[:], scalar=TINY, in1=den_raw[:], op0=ALU.max, op1=ALU.mult
+        )
+        nc.gpsimd.tensor_tensor(out=num_norm[:], in0=num_sq[:], in1=plus_half[:], op=ALU.pow)
+        nc.vector.tensor_scalar_max(out=den[:], in0=den_raw[:], scalar1=EPS)
+        x_coef = per_row("x_coef")
+        kappa = per_row("kappa")
+        mv_coef = per_row("mv_coef")
+        b_coef = per_row("b_coef")
+        mv_rcoef = per_row("mv_rcoef")
+        nc.vector.tensor_scalar_add(out=x_coef[:], in0=one_plus_2xy[:], scalar1=y2[:])
+        nc.vector.tensor_mul(out=kappa[:], in0=x_norm[:], in1=mv_rnorm[:])
+        nc.vector.reciprocal(out=rden[:], in_=den[:])
+        nc.vector.tensor_scalar(
+            out=b_coef[:], in0=x2[:], scalar1=minus_beta[:], scalar2=beta[:], op0=ALU.mult, op1=ALU.add
+        )
+        nc.vector.tensor_mul(out=mv_coef[:], in0=x_coef[:], in1=kappa[:])
+        one_minus_z2 = per_row("one_minus_z2")
+        z_gap = per_row("z_gap")
+        half_lambda = per_row("half_lambda")
+        nc.vector.tensor_scalar(
+            out=one_minus_z2[:], in0=z_sq[:], scalar1=-1.0, scalar2=1.0, op0=ALU.mult, op1=ALU.add
+        )
+        nc.vector.reciprocal(out=mv_rcoef[:], in_=mv_coef[:])
+        nc.vector.tensor_scalar_max(out=z_gap[:], in0=one_minus_z2[:], scalar1=EPS)
+        nc.vector.tensor_mul(out=rho[:], in0=b_coef[:], in1=mv_rcoef[:])
+        nc.vector.reciprocal(out=half_lambda[:], in_=z_gap[:])
+
+        v0_norm = per_row("v0_norm")
+        vt_norm = per_horizon("vt_norm")
+        vt_tanh = per_horizon("vt_tanh")
+        for r in blocks:
+            nc.vector.tensor_scalar(
+                out=col(v0_norm, r), in0=col(num_norm, r), scalar1=col(rden, r), scalar2=MAX_NORM,
+                op0=ALU.mult, op1=ALU.min,
+            )
+        for r in blocks:
+            nc.vector.tensor_scalar(
+                out=vt_norm[:, r, :], in0=tau[:], scalar1=col(v0_norm, r), scalar2=EPS,
+                op0=ALU.mult, op1=ALU.max,
+            )
+            nc.scalar.activation(
+                out=vt_tanh[:, r, :], in_=vt_norm[:, r, :], func=ACT.Tanh, scale=col(half_lambda, r)
+            )
+
+        num_rnorm = per_row("num_rnorm")
+        w_factor = per_row("w_factor")
+        u_scale = per_row("u_scale")
+        mv_dot_z = per_row("mv_dot_z")
+        z_dot_u_b = per_row("z_dot_u_b")
+        z_dot_u = per_row("z_dot_u")
+        two_z_dot_v0 = per_row("two_z_dot_v0")
+        v0_sq = per_row("v0_sq")
+        u_gain = per_row("u_gain")
+        vt_rnorm = per_horizon("vt_rnorm")
+        tau_over_norm = per_horizon("tau_over_norm")
+        for r in blocks:
+            dot_mv_z(last, r)
+        nc.vector.reciprocal(out=num_rnorm[:], in_=num_norm[:])
+        nc.vector.tensor_reduce(out=mv_dot_z[:], in_=mv_dot_z_parts[:], axis=AX.X, op=ALU.add)
+        nc.vector.tensor_mul(out=z_dot_u_b[:], in0=rho[:], in1=z_dot_b[:])
+        nc.vector.scalar_tensor_tensor(
+            out=w_factor[:], in0=num_rnorm[:], scalar=MAX_NORM, in1=rden[:], op0=ALU.mult, op1=ALU.min
+        )
+        nc.vector.tensor_add(out=z_dot_u[:], in0=z_dot_u_b[:], in1=mv_dot_z[:])
+        nc.vector.tensor_mul(out=u_scale[:], in0=mv_coef[:], in1=w_factor[:])
+        nc.vector.reciprocal(out=vt_rnorm[:], in_=vt_norm[:])
+        nc.vector.tensor_mul(out=v0_sq[:], in0=v0_norm[:], in1=v0_norm[:])
+        nc.vector.scalar_tensor_tensor(
+            out=two_z_dot_v0[:], in0=z_dot_u[:], scalar=2.0, in1=u_scale[:], op0=ALU.mult, op1=ALU.mult
+        )
+        nc.vector.tensor_mul(
+            out=tau_over_norm[:], in0=vt_rnorm[:],
+            in1=tau[:].unsqueeze(1).to_broadcast([P, ROW_BLOCKS, T]),
+        )
+        nc.vector.tensor_mul(out=u_gain[:], in0=one_minus_z2[:], in1=u_scale[:])
+
+        sigma = per_horizon("sigma")
+        s2 = per_horizon("s2")
+        one_plus_2zs = per_horizon("one_plus_2zs")
+        z2_plus_2zs = per_horizon("z2_plus_2zs")
+        z_coef = per_horizon("z_coef")
+        u_coef = per_horizon("u_coef")
+        den2_raw = per_horizon("den2_raw")
+        sum2_sq = per_horizon("sum2_sq")
+        num2_sq = per_horizon("num2_sq")
+        num2_norm = per_horizon("num2_norm")
+        den2 = per_horizon("den2")
+        rden2 = per_horizon("rden2")
+        nc.vector.tensor_mul(out=sigma[:], in0=vt_tanh[:], in1=tau_over_norm[:])
+        for r in blocks:
+            nc.vector.scalar_tensor_tensor(
+                out=s2[:, r, :], in0=sigma[:, r, :], scalar=col(v0_sq, r), in1=sigma[:, r, :],
+                op0=ALU.mult, op1=ALU.mult,
+            )
+        for r in blocks:
+            nc.vector.tensor_scalar(
+                out=one_plus_2zs[:, r, :], in0=sigma[:, r, :], scalar1=col(two_z_dot_v0, r), scalar2=1.0,
+                op0=ALU.mult, op1=ALU.add,
+            )
+        for r in blocks:
+            nc.vector.tensor_scalar(
+                out=z2_plus_2zs[:, r, :], in0=sigma[:, r, :], scalar1=col(two_z_dot_v0, r),
+                scalar2=col(z_sq, r), op0=ALU.mult, op1=ALU.add,
+            )
+        for r in blocks:
+            nc.vector.scalar_tensor_tensor(
+                out=den2_raw[:, r, :], in0=s2[:, r, :], scalar=col(z_sq, r), in1=one_plus_2zs[:, r, :],
+                op0=ALU.mult, op1=ALU.add,
+            )
+        nc.vector.tensor_add(out=sum2_sq[:], in0=s2[:], in1=z2_plus_2zs[:])
+        nc.vector.tensor_scalar_max(out=den2[:], in0=den2_raw[:], scalar1=EPS)
+        nc.vector.scalar_tensor_tensor(
+            out=num2_sq[:], in0=sum2_sq[:], scalar=TINY, in1=den2_raw[:], op0=ALU.max, op1=ALU.mult
+        )
+        nc.scalar.activation(out=num2_norm[:], in_=num2_sq[:], func=ACT.Sqrt)
+        nc.vector.reciprocal(out=rden2[:], in_=den2[:])
+        nc.vector.tensor_add(out=z_coef[:], in0=s2[:], in1=one_plus_2zs[:])
+        for r in blocks:
+            nc.vector.tensor_scalar_mul(out=u_coef[:, r, :], in0=sigma[:, r, :], scalar1=col(u_gain, r))
+        make_u(0, 0)
+        num2_rnorm = per_horizon("num2_rnorm")
+        o_factor = per_horizon("o_factor")
+        a_fin = per_horizon("a_fin")
+        c_fin = per_horizon("c_fin")
+        nc.vector.reciprocal(out=num2_rnorm[:], in_=num2_norm[:])
+        nc.vector.scalar_tensor_tensor(
+            out=o_factor[:], in0=num2_rnorm[:], scalar=MAX_NORM, in1=rden2[:], op0=ALU.mult, op1=ALU.min
+        )
+        nc.vector.tensor_mul(out=a_fin[:], in0=z_coef[:], in1=o_factor[:])
+        nc.vector.tensor_mul(out=c_fin[:], in0=u_coef[:], in1=o_factor[:])
+
+        for r in blocks:
+            for j in range(N_TILES):
+                if (r, j) != (0, 0):
+                    make_u(r, j)
+            for t in range(T):
+                res = stream.tile([P, N], F32)
+                for h in range(N // HALF):
+                    cols = slice(h * HALF, (h + 1) * HALF)
+                    nc.scalar.activation(
+                        out=res[:, cols], in_=z_sb[:, r, cols], func=ACT.Copy, scale=a_fin[:, r, t : t + 1]
+                    )
+                    nc.vector.scalar_tensor_tensor(
+                        out=res[:, cols], in0=u_sb[:, r, cols], scalar=c_fin[:, r, t : t + 1],
+                        in1=res[:, cols], op0=ALU.mult, op1=ALU.add,
+                    )
+                nc.sync.dma_start(out=out[r * P : (r + 1) * P, t, :], in_=res[:])

@@ -81,8 +81,8 @@ def tile_paralleldirectpoincaredynamics_kernel(
 
         step_raw = small.tile([P, 1], BF16)
         b_cols = small.tile([P, N // P], BF16)
-        nc.scalar.dma_start(out=b_row[0:1, :], in_=b.rearrange("(o n) -> o n", o=1))
-        nc.scalar.dma_start(out=b_cols[:], in_=b.rearrange("(p c) -> p c", p=P))
+        nc.sync.dma_start(out=b_row[0:1, :], in_=b.rearrange("(o n) -> o n", o=1))
+        nc.sync.dma_start(out=b_cols[:], in_=b.rearrange("(p c) -> p c", p=P))
         nc.scalar.dma_start(out=step_raw[:], in_=step_sizes.partition_broadcast(P))
 
         v_sb = keep.tile([P, ROW_BLOCKS, K], BF16)
@@ -138,12 +138,15 @@ def tile_paralleldirectpoincaredynamics_kernel(
                         nc.tensor.transpose(
                             turned[:, i, u, :], v_pairs[:, 256 * g + u : 256 * (g + 1) : 2], ident[:]
                         )
-                nc.scalar.copy(
-                    out=grouped[:, r, h * 1024 : (h + 1) * 1024]
+                side_by_side = (
+                    grouped[:, r, h * 1024 : (h + 1) * 1024]
                     .bitcast(F32)
-                    .rearrange("p (i b u) -> p i b u", i=2, u=2),
-                    in_=turned[:].rearrange("p i u b -> p i b u"),
+                    .rearrange("p (i b u) -> p i b u", i=2, u=2)
                 )
+                if r == 0:
+                    nc.scalar.copy(out=side_by_side, in_=turned[:].rearrange("p i u b -> p i b u"))
+                else:
+                    nc.vector.tensor_copy(out=side_by_side, in_=turned[:].rearrange("p i u b -> p i b u"))
 
         def quantise_v(r):
             nc.vector.quantize_mx(
@@ -204,20 +207,21 @@ def tile_paralleldirectpoincaredynamics_kernel(
         )
         b_sq_ps = psum.tile([P, ROW_BLOCKS], F32, tag="bank")
         nc.tensor.matmul(out=b_sq_ps[:], lhsT=ones_f32[:], rhs=b_sq_part[:], start=True, stop=True)
+        b_sq = per_row("b_sq", 1)
+        nc.vector.tensor_copy(out=b_sq[:], in_=b_sq_ps[:, 0:1])
 
         turn_v(0)
         square_rows(v_sb[:, 0, :], col(v_sq, 0))
-        turn_v(1)
-        square_rows(v_sb[:, 1, :], col(v_sq, 1))
         dot_z_b(0)
         quantise_v(0)
-        dot_z_b(1)
+        turn_v(1)
+        square_rows(v_sb[:, 1, :], col(v_sq, 1))
         quantise_v(1)
+        dot_z_b(1)
         for j in range(N_TILES):
             for r in blocks:
                 multiply(j, r)
 
-        b_sq = per_row("b_sq", 1)
         b_sq_c = per_row("b_sq_c", 1)
         b_norm = per_row("b_norm", 1)
         b_tanh = per_row("b_tanh", 1)
@@ -234,21 +238,23 @@ def tile_paralleldirectpoincaredynamics_kernel(
         ln_minus = per_row("ln_minus")
         ln_diff = per_row("ln_diff")
         v_rnorm = per_row("v_rnorm")
+        two_gain = per_row("two_gain")
         gain = per_row("gain")
+        beta_sq = per_row("beta_sq", 1)
         step = per_row("step", 1)
         tau = per_row("tau", T)
-        nc.vector.tensor_copy(out=b_sq[:], in_=b_sq_ps[:, 0:1])
-        nc.vector.tensor_scalar_max(out=v_sq_c[:], in0=v_sq[:], scalar1=EPS_SQ)
-        nc.vector.tensor_scalar_max(out=b_sq_c[:], in0=b_sq[:], scalar1=EPS_SQ)
-        nc.gpsimd.tensor_tensor(out=v_norm[:], in0=v_sq_c[:], in1=plus_half[:], op=ALU.pow)
+        nc.gpsimd.tensor_scalar_max(out=b_sq_c[:], in0=b_sq[:], scalar1=EPS_SQ)
         nc.gpsimd.tensor_tensor(out=b_norm[:], in0=b_sq_c[:], in1=plus_half[:, 0:1], op=ALU.pow)
+        nc.gpsimd.tensor_tensor(out=b_rnorm[:], in0=b_sq_c[:], in1=minus_half[:, 0:1], op=ALU.pow)
+        nc.gpsimd.tensor_scalar_max(out=v_sq_c[:], in0=v_sq[:], scalar1=EPS_SQ)
+        nc.gpsimd.tensor_tensor(out=v_norm[:], in0=v_sq_c[:], in1=plus_half[:], op=ALU.pow)
+        nc.gpsimd.tensor_scalar_min(out=v_clip[:], in0=v_norm[:], scalar1=MAX_NORM)
+        nc.gpsimd.tensor_tensor(out=v_rnorm[:], in0=v_sq_c[:], in1=minus_half[:], op=ALU.pow)
 
         for r in blocks:
             square_mv(0, r)
             dot_mv_b(0, r)
-        nc.vector.tensor_scalar_min(out=v_clip[:], in0=v_norm[:], scalar1=MAX_NORM)
-        nc.vector.reciprocal(out=v_rnorm[:], in_=v_norm[:])
-        nc.vector.reciprocal(out=b_rnorm[:], in_=b_norm[:])
+        square_rows(z_sb[:, 0, :], col(z_sq, 0))
         nc.scalar.activation(out=ln_plus[:], in_=v_clip[:], func=ACT.Ln, bias=one_col[:], scale=1.0)
         nc.scalar.activation(out=ln_minus[:], in_=v_clip[:], func=ACT.Ln, bias=one_col[:], scale=-1.0)
         nc.scalar.activation(out=step[:], in_=step_raw[:], func=ACT.Sigmoid)
@@ -258,19 +264,16 @@ def tile_paralleldirectpoincaredynamics_kernel(
         for r in blocks:
             square_mv(1, r)
             dot_mv_b(1, r)
-        square_rows(z_sb[:, 0, :], col(z_sq, 0))
-        nc.vector.tensor_sub(out=ln_diff[:], in0=ln_plus[:], in1=ln_minus[:])
-        nc.vector.tensor_scalar_mul(out=tau[:], in0=horizon[:], scalar1=step[:])
-        nc.vector.tensor_mul(out=beta[:], in0=b_tanh[:], in1=b_rnorm[:])
-        nc.vector.scalar_tensor_tensor(
-            out=gain[:], in0=ln_diff[:], scalar=0.5, in1=v_rnorm[:], op0=ALU.mult, op1=ALU.mult
-        )
-        nc.vector.tensor_scalar_mul(out=two_beta[:], in0=beta[:], scalar1=2.0)
-        nc.vector.tensor_scalar_mul(out=minus_beta[:], in0=beta[:], scalar1=-1.0)
-        nc.vector.tensor_scalar(
-            out=y2[:], in0=beta[:], scalar1=beta[:], scalar2=b_sq[:], op0=ALU.mult, op1=ALU.mult
-        )
-        nc.vector.tensor_scalar_add(out=y2_minus_1[:], in0=y2[:], scalar1=-1.0)
+        nc.gpsimd.tensor_sub(out=ln_diff[:], in0=ln_plus[:], in1=ln_minus[:])
+        nc.gpsimd.tensor_mul(out=two_gain[:], in0=ln_diff[:], in1=v_rnorm[:])
+        nc.gpsimd.tensor_scalar_mul(out=gain[:], in0=two_gain[:], scalar1=0.5)
+        nc.gpsimd.tensor_mul(out=beta[:], in0=b_tanh[:], in1=b_rnorm[:])
+        nc.gpsimd.tensor_scalar_mul(out=two_beta[:], in0=beta[:], scalar1=2.0)
+        nc.gpsimd.tensor_mul(out=beta_sq[:], in0=beta[:], in1=beta[:])
+        nc.gpsimd.tensor_mul(out=y2[:], in0=beta_sq[:], in1=b_sq[:])
+        nc.gpsimd.tensor_scalar_add(out=y2_minus_1[:], in0=y2[:], scalar1=-1.0)
+        nc.gpsimd.tensor_scalar_mul(out=minus_beta[:], in0=beta[:], scalar1=-1.0)
+        nc.gpsimd.tensor_scalar_mul(out=tau[:], in0=horizon[:], scalar1=step[:])
         for r in blocks:
             dot_mv_z(1, r)
         for r in blocks:

@@ -68,21 +68,21 @@ def tile_paralleldirectpoincaredynamics_kernel(
         b_sq_part = per_row("b_sq_part")
         ident = keep.tile([P, P], F32)
         nc.vector.memset(b_row[:].bitcast(I32), 0)
-        nc.vector.memset(ones[:], 1.0)
-        nc.vector.memset(one_col[:], 1.0)
         nc.vector.memset(w_planes[:].bitcast(I32), 0)
+        nc.vector.memset(ones[:], 1.0)
         nc.vector.memset(ones_f32[:], 1.0)
-        nc.vector.memset(b_sq_part[:], 0.0)
-        nc.vector.memset(plus_half[:], 0.5)
-        nc.vector.memset(minus_half[:], -0.5)
-        for t in range(T):
-            nc.vector.memset(horizon[:, t : t + 1], float(t + 1))
+        nc.gpsimd.memset(one_col[:], 1.0)
         make_identity(nc, ident[:])
+        nc.gpsimd.memset(b_sq_part[:], 0.0)
+        nc.gpsimd.memset(plus_half[:], 0.5)
+        nc.gpsimd.memset(minus_half[:], -0.5)
+        for t in range(T):
+            nc.gpsimd.memset(horizon[:, t : t + 1], float(t + 1))
 
         step_raw = small.tile([P, 1], BF16)
         b_cols = small.tile([P, N // P], BF16)
-        nc.sync.dma_start(out=b_row[0:1, :], in_=b.rearrange("(o n) -> o n", o=1))
-        nc.sync.dma_start(out=b_cols[:], in_=b.rearrange("(p c) -> p c", p=P))
+        nc.scalar.dma_start(out=b_row[0:1, :], in_=b.rearrange("(o n) -> o n", o=1))
+        nc.scalar.dma_start(out=b_cols[:], in_=b.rearrange("(p c) -> p c", p=P))
         nc.scalar.dma_start(out=step_raw[:], in_=step_sizes.partition_broadcast(P))
 
         v_sb = keep.tile([P, ROW_BLOCKS, K], BF16)
@@ -103,8 +103,16 @@ def tile_paralleldirectpoincaredynamics_kernel(
                 in_=w_bytes[:, :, j * N_TILE * PACK : (j + 1) * N_TILE * PACK].bitcast(I32),
             )
 
-        squares = keep.tile([P, N], BF16)
-        products = keep.tile([P, N], F32)
+        squares = keep.tile([P, 2, N], BF16)
+        products = keep.tile([P, 2, N], F32)
+        turns = {"scalar": 0, "vector": 0}
+
+        def scrap(engine, width):
+            tile_of = {"scalar": squares, "vector": products}[engine]
+            places = 2 * N // width
+            turns[engine] = (turns[engine] + 1) % places
+            at = turns[engine] * width
+            return tile_of[:].rearrange("p a n -> p (a n)")[:, at : at + width]
         b_bc = keep.tile([P, N], BF16)
         v_sq = per_row("v_sq")
         z_sq = per_row("z_sq")
@@ -120,15 +128,15 @@ def tile_paralleldirectpoincaredynamics_kernel(
         rho = per_row("rho")
 
         def square_rows(rows, total):
-            nc.scalar.activation(out=squares[:], in_=rows, func=ACT.Square, accum_out=total)
+            nc.scalar.activation(out=scrap("scalar", N), in_=rows, func=ACT.Square, accum_out=total)
 
         def dot_z_b(r):
             nc.vector.scalar_tensor_tensor(
-                out=products[:], in0=z_sb[:, r, :], scalar=1.0, in1=b_bc[:],
+                out=scrap("vector", N), in0=z_sb[:, r, :], scalar=1.0, in1=b_bc[:],
                 op0=ALU.mult, op1=ALU.mult, accum_out=col(z_dot_b, r),
             )
 
-        def turn_v(r):
+        def turn_v(r, copiers):
             v_pairs = v_sb[:, r, :].bitcast(F32)
             for h in range(2):
                 turned = psum.tile([P, 2, 2, P], F32, tag="bank")
@@ -143,7 +151,7 @@ def tile_paralleldirectpoincaredynamics_kernel(
                     .bitcast(F32)
                     .rearrange("p (i b u) -> p i b u", i=2, u=2)
                 )
-                if r == 0:
+                if copiers[h] == "scalar":
                     nc.scalar.copy(out=side_by_side, in_=turned[:].rearrange("p i u b -> p i b u"))
                 else:
                     nc.vector.tensor_copy(out=side_by_side, in_=turned[:].rearrange("p i u b -> p i b u"))
@@ -170,13 +178,13 @@ def tile_paralleldirectpoincaredynamics_kernel(
 
         def square_mv(j, r):
             nc.scalar.activation(
-                out=squares[:, tile_cols(j)], in_=mv[r][j][:], func=ACT.Square,
+                out=scrap("scalar", N_TILE), in_=mv[r][j][:], func=ACT.Square,
                 accum_out=mv_sq_parts[:, r, j : j + 1],
             )
 
         def dot_mv(j, r, other, parts):
             nc.vector.scalar_tensor_tensor(
-                out=products[:, tile_cols(j)], in0=mv[r][j][:], scalar=1.0, in1=other,
+                out=scrap("vector", N_TILE), in0=mv[r][j][:], scalar=1.0, in1=other,
                 op0=ALU.mult, op1=ALU.mult, accum_out=parts[:, r, j : j + 1],
             )
 
@@ -201,23 +209,22 @@ def tile_paralleldirectpoincaredynamics_kernel(
                     out=spread[:, tile_cols(i)], lhsT=ones[:], rhs=b_row[:, tile_cols(2 * h + i)],
                     start=True, stop=True,
                 )
-            nc.scalar.copy(out=b_bc[:, h * HALF : (h + 1) * HALF], in_=spread[:])
+            nc.vector.tensor_copy(out=b_bc[:, h * HALF : (h + 1) * HALF], in_=spread[:])
         nc.scalar.activation(
-            out=squares[:, 0 : N // P], in_=b_cols[:], func=ACT.Square, accum_out=b_sq_part[:, 0:1]
+            out=scrap("scalar", N // P), in_=b_cols[:], func=ACT.Square, accum_out=b_sq_part[:, 0:1]
         )
+        turn_v(0, ("scalar", "scalar"))
+        turn_v(1, ("scalar", "scalar"))
         b_sq_ps = psum.tile([P, ROW_BLOCKS], F32, tag="bank")
         nc.tensor.matmul(out=b_sq_ps[:], lhsT=ones_f32[:], rhs=b_sq_part[:], start=True, stop=True)
         b_sq = per_row("b_sq", 1)
-        nc.vector.tensor_copy(out=b_sq[:], in_=b_sq_ps[:, 0:1])
-
-        turn_v(0)
-        square_rows(v_sb[:, 0, :], col(v_sq, 0))
         dot_z_b(0)
         quantise_v(0)
-        turn_v(1)
-        square_rows(v_sb[:, 1, :], col(v_sq, 1))
         quantise_v(1)
+        nc.vector.tensor_copy(out=b_sq[:], in_=b_sq_ps[:, 0:1])
         dot_z_b(1)
+        square_rows(v_sb[:, 0, :], col(v_sq, 0))
+        square_rows(v_sb[:, 1, :], col(v_sq, 1))
         for j in range(N_TILES):
             for r in blocks:
                 multiply(j, r)
@@ -251,19 +258,30 @@ def tile_paralleldirectpoincaredynamics_kernel(
         nc.gpsimd.tensor_scalar_min(out=v_clip[:], in0=v_norm[:], scalar1=MAX_NORM)
         nc.gpsimd.tensor_tensor(out=v_rnorm[:], in0=v_sq_c[:], in1=minus_half[:], op=ALU.pow)
 
-        for r in blocks:
-            square_mv(0, r)
-            dot_mv_b(0, r)
-        square_rows(z_sb[:, 0, :], col(z_sq, 0))
+        later = []
+        issued = {"n": 0}
+
+        def fill(n):
+            for i in range(n):
+                if issued["n"] < len(later):
+                    later[issued["n"]]()
+                    issued["n"] += 1
+
+        def defer(action, *args):
+            later.append(lambda: action(*args))
+
+        for j in range(N_TILES):
+            for r in blocks:
+                defer(dot_mv_z, j, r)
+        sums_deferred = len(later)
+
+        for j, r in ((0, 0), (0, 1), (1, 0)):
+            square_mv(j, r)
+            dot_mv_b(j, r)
         nc.scalar.activation(out=ln_plus[:], in_=v_clip[:], func=ACT.Ln, bias=one_col[:], scale=1.0)
         nc.scalar.activation(out=ln_minus[:], in_=v_clip[:], func=ACT.Ln, bias=one_col[:], scale=-1.0)
         nc.scalar.activation(out=step[:], in_=step_raw[:], func=ACT.Sigmoid)
         nc.scalar.activation(out=b_tanh[:], in_=b_norm[:], func=ACT.Tanh)
-        for r in blocks:
-            dot_mv_z(0, r)
-        for r in blocks:
-            square_mv(1, r)
-            dot_mv_b(1, r)
         nc.gpsimd.tensor_sub(out=ln_diff[:], in0=ln_plus[:], in1=ln_minus[:])
         nc.gpsimd.tensor_mul(out=two_gain[:], in0=ln_diff[:], in1=v_rnorm[:])
         nc.gpsimd.tensor_scalar_mul(out=gain[:], in0=two_gain[:], scalar1=0.5)
@@ -274,90 +292,100 @@ def tile_paralleldirectpoincaredynamics_kernel(
         nc.gpsimd.tensor_scalar_add(out=y2_minus_1[:], in0=y2[:], scalar1=-1.0)
         nc.gpsimd.tensor_scalar_mul(out=minus_beta[:], in0=beta[:], scalar1=-1.0)
         nc.gpsimd.tensor_scalar_mul(out=tau[:], in0=horizon[:], scalar1=step[:])
-        for r in blocks:
-            dot_mv_z(1, r)
-        for r in blocks:
-            square_mv(2, r)
-            dot_mv_b(2, r)
+        for j, r in ((1, 1), (2, 0), (2, 1)):
+            square_mv(j, r)
+            dot_mv_b(j, r)
+            fill(1)
+        mv_sq_pair = per_row("mv_sq_pair")
         mv_sq_head = per_row("mv_sq_head")
         mv_dot_b_head = per_row("mv_dot_b_head")
-        nc.vector.tensor_reduce(out=mv_sq_head[:], in_=mv_sq_parts[:, :, 0:last], axis=AX.X, op=ALU.add)
+        head_2bpt = per_row("head_2bpt")
+        nc.gpsimd.tensor_add(out=mv_sq_pair[:], in0=mv_sq_parts[:, :, 0], in1=mv_sq_parts[:, :, 1])
+        nc.gpsimd.tensor_add(out=mv_sq_head[:], in0=mv_sq_pair[:], in1=mv_sq_parts[:, :, 2])
         nc.vector.tensor_reduce(out=mv_dot_b_head[:], in_=mv_dot_b_parts[:, :, 0:last], axis=AX.X, op=ALU.add)
-        for r in blocks:
-            square_mv(last, r)
-            dot_mv_b(last, r)
+        nc.vector.tensor_scalar_mul(out=head_2bpt[:], in0=mv_dot_b_head[:], scalar1=two_beta[:])
+        square_mv(last, 0)
+        dot_mv_b(last, 0)
+        square_mv(last, 1)
+        dot_mv_b(last, 1)
 
         mv_sq_c = per_row("mv_sq_c")
         mv_rnorm = per_row("mv_rnorm")
         mv_sq_gain = per_row("mv_sq_gain")
-        mv_dot_b = per_row("mv_dot_b")
         mv_dot_2bpt = per_row("mv_dot_2bpt")
         two_xy_unit = per_row("two_xy_unit")
         x_norm = per_row("x_norm")
         for r in blocks:
-            nc.vector.tensor_scalar(
+            nc.gpsimd.tensor_scalar(
                 out=col(mv_sq_c, r), in0=mv_sq_parts[:, r, last : last + 1], scalar1=col(mv_sq_head, r),
                 scalar2=EPS_SQ, op0=ALU.add, op1=ALU.max,
             )
         nc.gpsimd.tensor_tensor(out=mv_rnorm[:], in0=mv_sq_c[:], in1=minus_half[:], op=ALU.pow)
+        square_rows(z_sb[:, 0, :], col(z_sq, 0))
+        fill(2)
+        nc.vector.scalar_tensor_tensor(
+            out=mv_dot_2bpt[:], in0=mv_dot_b_parts[:, :, last], scalar=two_beta[:], in1=head_2bpt[:],
+            op0=ALU.mult, op1=ALU.add,
+        )
         nc.vector.tensor_mul(out=mv_sq_gain[:], in0=mv_sq_c[:], in1=gain[:])
-        nc.vector.tensor_add(out=mv_dot_b[:], in0=mv_dot_b_parts[:, :, last], in1=mv_dot_b_head[:])
-        nc.vector.tensor_scalar_mul(out=mv_dot_2bpt[:], in0=mv_dot_b[:], scalar1=two_beta[:])
-        dot_mv_z(2, 0)
         for r in blocks:
             nc.scalar.activation(
                 out=col(x_norm, r), in_=col(mv_rnorm, r), func=ACT.Tanh, scale=col(mv_sq_gain, r)
             )
         square_rows(z_sb[:, 1, :], col(z_sq, 1))
+        fill(1)
         nc.vector.tensor_mul(out=two_xy_unit[:], in0=mv_rnorm[:], in1=mv_dot_2bpt[:])
-        dot_mv_z(2, 1)
+        fill(1)
         one_plus_2xy = per_row("one_plus_2xy")
         x2 = per_row("x2")
         den_raw = per_row("den_raw")
         sum_sq = per_row("sum_sq")
         num_sq = per_row("num_sq")
         num_norm = per_row("num_norm")
+        num_rnorm = per_row("num_rnorm")
         den = per_row("den")
         rden = per_row("rden")
+        x_coef = per_row("x_coef")
+        kappa = per_row("kappa")
+        mv_coef = per_row("mv_coef")
+        b_coef = per_row("b_coef")
+        mv_rcoef = per_row("mv_rcoef")
+        one_minus_z2 = per_row("one_minus_z2")
+        z_gap = per_row("z_gap")
+        half_lambda = per_row("half_lambda")
+        nc.vector.tensor_mul(out=x2[:], in0=x_norm[:], in1=x_norm[:])
         for r in blocks:
             nc.vector.tensor_scalar(
                 out=col(one_plus_2xy, r), in0=col(x_norm, r), scalar1=col(two_xy_unit, r), scalar2=1.0,
                 op0=ALU.mult, op1=ALU.add,
             )
-        nc.vector.tensor_mul(out=x2[:], in0=x_norm[:], in1=x_norm[:])
+        nc.vector.tensor_mul(out=kappa[:], in0=x_norm[:], in1=mv_rnorm[:])
         nc.vector.scalar_tensor_tensor(
             out=den_raw[:], in0=x2[:], scalar=y2[:], in1=one_plus_2xy[:], op0=ALU.mult, op1=ALU.add
         )
         nc.vector.scalar_tensor_tensor(
             out=sum_sq[:], in0=x2[:], scalar=y2_minus_1[:], in1=one_plus_2xy[:], op0=ALU.add, op1=ALU.add
         )
+        nc.vector.tensor_scalar_add(out=x_coef[:], in0=one_plus_2xy[:], scalar1=y2[:])
+        nc.vector.tensor_scalar(
+            out=b_coef[:], in0=x2[:], scalar1=minus_beta[:], scalar2=beta[:], op0=ALU.mult, op1=ALU.add
+        )
         nc.vector.scalar_tensor_tensor(
             out=num_sq[:], in0=sum_sq[:], scalar=TINY, in1=den_raw[:], op0=ALU.max, op1=ALU.mult
         )
         nc.gpsimd.tensor_tensor(out=num_norm[:], in0=num_sq[:], in1=plus_half[:], op=ALU.pow)
         nc.vector.tensor_scalar_max(out=den[:], in0=den_raw[:], scalar1=EPS)
-        x_coef = per_row("x_coef")
-        kappa = per_row("kappa")
-        mv_coef = per_row("mv_coef")
-        b_coef = per_row("b_coef")
-        mv_rcoef = per_row("mv_rcoef")
-        nc.vector.tensor_scalar_add(out=x_coef[:], in0=one_plus_2xy[:], scalar1=y2[:])
-        nc.vector.tensor_mul(out=kappa[:], in0=x_norm[:], in1=mv_rnorm[:])
-        nc.vector.reciprocal(out=rden[:], in_=den[:])
-        nc.vector.tensor_scalar(
-            out=b_coef[:], in0=x2[:], scalar1=minus_beta[:], scalar2=beta[:], op0=ALU.mult, op1=ALU.add
-        )
         nc.vector.tensor_mul(out=mv_coef[:], in0=x_coef[:], in1=kappa[:])
-        one_minus_z2 = per_row("one_minus_z2")
-        z_gap = per_row("z_gap")
-        half_lambda = per_row("half_lambda")
+        fill(1)
+        nc.vector.reciprocal(out=rden[:], in_=den[:])
+        nc.vector.reciprocal(out=mv_rcoef[:], in_=mv_coef[:])
         nc.vector.tensor_scalar(
             out=one_minus_z2[:], in0=z_sq[:], scalar1=-1.0, scalar2=1.0, op0=ALU.mult, op1=ALU.add
         )
-        nc.vector.reciprocal(out=mv_rcoef[:], in_=mv_coef[:])
-        nc.vector.tensor_scalar_max(out=z_gap[:], in0=one_minus_z2[:], scalar1=EPS)
         nc.vector.tensor_mul(out=rho[:], in0=b_coef[:], in1=mv_rcoef[:])
-        nc.vector.reciprocal(out=half_lambda[:], in_=z_gap[:])
+        nc.vector.tensor_scalar_max(out=z_gap[:], in0=one_minus_z2[:], scalar1=EPS)
+        for j in range(N_TILES):
+            defer(make_u, 0, j)
 
         v0_norm = per_row("v0_norm")
         vt_norm = per_horizon("vt_norm")
@@ -367,6 +395,8 @@ def tile_paralleldirectpoincaredynamics_kernel(
                 out=col(v0_norm, r), in0=col(num_norm, r), scalar1=col(rden, r), scalar2=MAX_NORM,
                 op0=ALU.mult, op1=ALU.min,
             )
+        nc.vector.reciprocal(out=half_lambda[:], in_=z_gap[:])
+        nc.vector.reciprocal(out=num_rnorm[:], in_=num_norm[:])
         for r in blocks:
             nc.vector.tensor_scalar(
                 out=vt_norm[:, r, :], in0=tau[:], scalar1=col(v0_norm, r), scalar2=EPS,
@@ -376,7 +406,6 @@ def tile_paralleldirectpoincaredynamics_kernel(
                 out=vt_tanh[:, r, :], in_=vt_norm[:, r, :], func=ACT.Tanh, scale=col(half_lambda, r)
             )
 
-        num_rnorm = per_row("num_rnorm")
         w_factor = per_row("w_factor")
         u_scale = per_row("u_scale")
         mv_dot_z = per_row("mv_dot_z")
@@ -387,26 +416,24 @@ def tile_paralleldirectpoincaredynamics_kernel(
         u_gain = per_row("u_gain")
         vt_rnorm = per_horizon("vt_rnorm")
         tau_over_norm = per_horizon("tau_over_norm")
-        for r in blocks:
-            dot_mv_z(last, r)
-        nc.vector.reciprocal(out=num_rnorm[:], in_=num_norm[:])
-        nc.vector.tensor_reduce(out=mv_dot_z[:], in_=mv_dot_z_parts[:], axis=AX.X, op=ALU.add)
-        nc.vector.tensor_mul(out=z_dot_u_b[:], in0=rho[:], in1=z_dot_b[:])
         nc.vector.scalar_tensor_tensor(
             out=w_factor[:], in0=num_rnorm[:], scalar=MAX_NORM, in1=rden[:], op0=ALU.mult, op1=ALU.min
         )
-        nc.vector.tensor_add(out=z_dot_u[:], in0=z_dot_u_b[:], in1=mv_dot_z[:])
-        nc.vector.tensor_mul(out=u_scale[:], in0=mv_coef[:], in1=w_factor[:])
+        fill(max(0, sums_deferred - issued["n"]))
+        nc.vector.tensor_reduce(out=mv_dot_z[:], in_=mv_dot_z_parts[:], axis=AX.X, op=ALU.add)
+        nc.vector.tensor_mul(out=z_dot_u_b[:], in0=rho[:], in1=z_dot_b[:])
         nc.vector.reciprocal(out=vt_rnorm[:], in_=vt_norm[:])
         nc.vector.tensor_mul(out=v0_sq[:], in0=v0_norm[:], in1=v0_norm[:])
-        nc.vector.scalar_tensor_tensor(
-            out=two_z_dot_v0[:], in0=z_dot_u[:], scalar=2.0, in1=u_scale[:], op0=ALU.mult, op1=ALU.mult
-        )
+        nc.vector.tensor_mul(out=u_scale[:], in0=mv_coef[:], in1=w_factor[:])
+        nc.vector.tensor_add(out=z_dot_u[:], in0=z_dot_u_b[:], in1=mv_dot_z[:])
         nc.vector.tensor_mul(
             out=tau_over_norm[:], in0=vt_rnorm[:],
             in1=tau[:].unsqueeze(1).to_broadcast([P, ROW_BLOCKS, T]),
         )
         nc.vector.tensor_mul(out=u_gain[:], in0=one_minus_z2[:], in1=u_scale[:])
+        nc.vector.scalar_tensor_tensor(
+            out=two_z_dot_v0[:], in0=z_dot_u[:], scalar=2.0, in1=u_scale[:], op0=ALU.mult, op1=ALU.mult
+        )
 
         sigma = per_horizon("sigma")
         s2 = per_horizon("s2")
@@ -418,9 +445,11 @@ def tile_paralleldirectpoincaredynamics_kernel(
         sum2_sq = per_horizon("sum2_sq")
         num2_sq = per_horizon("num2_sq")
         num2_norm = per_horizon("num2_norm")
+        num2_rnorm = per_horizon("num2_rnorm")
         den2 = per_horizon("den2")
         rden2 = per_horizon("rden2")
         nc.vector.tensor_mul(out=sigma[:], in0=vt_tanh[:], in1=tau_over_norm[:])
+        fill(1)
         for r in blocks:
             nc.vector.scalar_tensor_tensor(
                 out=s2[:, r, :], in0=sigma[:, r, :], scalar=col(v0_sq, r), in1=sigma[:, r, :],
@@ -442,40 +471,54 @@ def tile_paralleldirectpoincaredynamics_kernel(
                 op0=ALU.mult, op1=ALU.add,
             )
         nc.vector.tensor_add(out=sum2_sq[:], in0=s2[:], in1=z2_plus_2zs[:])
-        nc.vector.tensor_scalar_max(out=den2[:], in0=den2_raw[:], scalar1=EPS)
+        for r in blocks:
+            nc.vector.tensor_scalar_mul(out=u_coef[:, r, :], in0=sigma[:, r, :], scalar1=col(u_gain, r))
+        nc.vector.tensor_add(out=z_coef[:], in0=s2[:], in1=one_plus_2zs[:])
         nc.vector.scalar_tensor_tensor(
             out=num2_sq[:], in0=sum2_sq[:], scalar=TINY, in1=den2_raw[:], op0=ALU.max, op1=ALU.mult
         )
         nc.scalar.activation(out=num2_norm[:], in_=num2_sq[:], func=ACT.Sqrt)
+        nc.vector.tensor_scalar_max(out=den2[:], in0=den2_raw[:], scalar1=EPS)
+        fill(1)
         nc.vector.reciprocal(out=rden2[:], in_=den2[:])
-        nc.vector.tensor_add(out=z_coef[:], in0=s2[:], in1=one_plus_2zs[:])
-        for r in blocks:
-            nc.vector.tensor_scalar_mul(out=u_coef[:, r, :], in0=sigma[:, r, :], scalar1=col(u_gain, r))
-        make_u(0, 0)
-        num2_rnorm = per_horizon("num2_rnorm")
         o_factor = per_horizon("o_factor")
         a_fin = per_horizon("a_fin")
         c_fin = per_horizon("c_fin")
         nc.vector.reciprocal(out=num2_rnorm[:], in_=num2_norm[:])
+        fill(1)
         nc.vector.scalar_tensor_tensor(
             out=o_factor[:], in0=num2_rnorm[:], scalar=MAX_NORM, in1=rden2[:], op0=ALU.mult, op1=ALU.min
         )
+        fill(1)
         nc.vector.tensor_mul(out=a_fin[:], in0=z_coef[:], in1=o_factor[:])
         nc.vector.tensor_mul(out=c_fin[:], in0=u_coef[:], in1=o_factor[:])
 
+        def scale_z(res, r, t, cols):
+            nc.scalar.activation(
+                out=res[:, cols], in_=z_sb[:, r, cols], func=ACT.Copy, scale=a_fin[:, r, t : t + 1]
+            )
+
+        def add_u(res, r, t, cols):
+            nc.vector.scalar_tensor_tensor(
+                out=res[:, cols], in0=u_sb[:, r, cols], scalar=c_fin[:, r, t : t + 1],
+                in1=res[:, cols], op0=ALU.mult, op1=ALU.add,
+            )
+            nc.sync.dma_start(out=out[r * P : (r + 1) * P, t, cols], in_=res[:, cols])
+
+        def emit(r, t, pieces):
+            res = stream.tile([P, N], F32, name="res")
+            width = N // pieces
+            for i in range(pieces):
+                scale_z(res, r, t, slice(i * width, (i + 1) * width))
+            if (r, t) == (0, 0):
+                fill(len(later))
+            for i in range(pieces):
+                add_u(res, r, t, slice(i * width, (i + 1) * width))
+
         for r in blocks:
-            for j in range(N_TILES):
-                if (r, j) != (0, 0):
-                    make_u(r, j)
             for t in range(T):
-                res = stream.tile([P, N], F32)
-                for h in range(N // HALF):
-                    cols = slice(h * HALF, (h + 1) * HALF)
-                    nc.scalar.activation(
-                        out=res[:, cols], in_=z_sb[:, r, cols], func=ACT.Copy, scale=a_fin[:, r, t : t + 1]
-                    )
-                    nc.vector.scalar_tensor_tensor(
-                        out=res[:, cols], in0=u_sb[:, r, cols], scalar=c_fin[:, r, t : t + 1],
-                        in1=res[:, cols], op0=ALU.mult, op1=ALU.add,
-                    )
-                nc.sync.dma_start(out=out[r * P : (r + 1) * P, t, :], in_=res[:])
+                first = (r, t) == (0, 0)
+                final = (r, t) == (ROW_BLOCKS - 1, T - 1)
+                emit(r, t, 4 if first or final else 1)
+                if r == 0 and t < N_TILES:
+                    make_u(1, t)

@@ -22,6 +22,7 @@ PASSES = K // K_PASS
 N_TILE = 512
 N_TILES = N // N_TILE
 HALF = N // 2
+W_LOADS = (512, 512, 512, 512)
 
 EPS = 1e-7
 EPS_SQ = 1e-14
@@ -54,6 +55,9 @@ def tile_paralleldirectpoincaredynamics_kernel(
         def tile_cols(j):
             return slice(j * N_TILE, (j + 1) * N_TILE)
 
+        def half_cols(h):
+            return slice(h * HALF, (h + 1) * HALF)
+
         blocks = range(ROW_BLOCKS)
         last = N_TILES - 1
 
@@ -81,42 +85,55 @@ def tile_paralleldirectpoincaredynamics_kernel(
 
         step_raw = small.tile([P, 1], BF16)
         b_cols = small.tile([P, N // P], BF16)
-        nc.scalar.dma_start(out=b_row[0:1, :], in_=b.rearrange("(o n) -> o n", o=1))
-        nc.scalar.dma_start(out=b_cols[:], in_=b.rearrange("(p c) -> p c", p=P))
-        nc.scalar.dma_start(out=step_raw[:], in_=step_sizes.partition_broadcast(P))
-
         v_sb = keep.tile([P, ROW_BLOCKS, K], BF16)
         z_sb = keep.tile([P, ROW_BLOCKS, N], BF16)
-        for r in blocks:
-            nc.sync.dma_start(out=v_sb[:, r, :], in_=v_init[r * P : (r + 1) * P, :])
-            nc.sync.dma_start(out=z_sb[:, r, :], in_=z_0[r * P : (r + 1) * P, :])
-        for quad in range(4):
-            nc.sync.dma_start(
-                out=w_planes[32 * quad : 32 * quad + 16, :].bitcast(I32),
-                in_=W_scales[:, 4 * quad : 4 * quad + 4, :].bitcast(I32),
-            )
         w_words = keep.tile([P, PASSES, N], I32, align_bytes=64)
         w_bytes = W_words.rearrange("g p n t -> p g (n t)")
-        for j in range(N_TILES):
+        w_starts = [sum(W_LOADS[:i]) for i in range(len(W_LOADS))]
+
+        def load_v(r):
+            nc.sync.dma_start(out=v_sb[:, r, :], in_=v_init[r * P : (r + 1) * P, :])
+
+        def load_z(r):
+            nc.sync.dma_start(out=z_sb[:, r, :], in_=z_0[r * P : (r + 1) * P, :])
+
+        def load_scales():
+            for quad in range(4):
+                nc.sync.dma_start(
+                    out=w_planes[32 * quad : 32 * quad + 16, :].bitcast(I32),
+                    in_=W_scales[:, 4 * quad : 4 * quad + 4, :].bitcast(I32),
+                )
+
+        def load_w(i):
+            c0, c1 = w_starts[i], w_starts[i] + W_LOADS[i]
             nc.sync.dma_start(
-                out=w_words[:, :, tile_cols(j)],
-                in_=w_bytes[:, :, j * N_TILE * PACK : (j + 1) * N_TILE * PACK].bitcast(I32),
+                out=w_words[:, :, c0:c1], in_=w_bytes[:, :, c0 * PACK : c1 * PACK].bitcast(I32)
             )
 
-        squares = keep.tile([P, 2, N], BF16)
-        products = keep.tile([P, 2, N], F32)
+        nc.sync.dma_start(out=b_row[0:1, :], in_=b.rearrange("(o n) -> o n", o=1))
+        nc.sync.dma_start(out=b_cols[:], in_=b.rearrange("(p c) -> p c", p=P))
+        nc.scalar.dma_start(out=step_raw[:], in_=step_sizes.partition_broadcast(P))
+        load_v(0)
+        load_z(0)
+        load_v(1)
+        load_z(1)
+        load_scales()
+        for i in range(len(W_LOADS)):
+            load_w(i)
+
+        squares = keep.tile([P, 2 * N], BF16)
+        products = keep.tile([P, 2 * N], F32)
         turns = {"scalar": 0, "vector": 0}
 
         def scrap(engine, width):
-            tile_of = {"scalar": squares, "vector": products}[engine]
-            places = 2 * N // width
-            turns[engine] = (turns[engine] + 1) % places
+            turns[engine] = (turns[engine] + 1) % (2 * N // width)
             at = turns[engine] * width
-            return tile_of[:].rearrange("p a n -> p (a n)")[:, at : at + width]
+            return {"scalar": squares, "vector": products}[engine][:, at : at + width]
+
         b_bc = keep.tile([P, N], BF16)
-        v_sq = per_row("v_sq")
-        z_sq = per_row("z_sq")
-        z_dot_b = per_row("z_dot_b")
+        v_sq_parts = small.tile([P, ROW_BLOCKS, 2], F32)
+        z_sq_parts = small.tile([P, ROW_BLOCKS, N_TILES], F32)
+        z_dot_b_parts = small.tile([P, ROW_BLOCKS, 2], F32)
         grouped = keep.tile([P, ROW_BLOCKS, PASSES * P * PACK], BF16, align_bytes=64)
         v_codes = keep.tile([P, ROW_BLOCKS, PASSES * P], U32, align_bytes=64)
         v_planes = keep.tile([P, ROW_BLOCKS, PASSES * P], U8, align_bytes=64)
@@ -127,16 +144,25 @@ def tile_paralleldirectpoincaredynamics_kernel(
         u_sb = keep.tile([P, ROW_BLOCKS, N], F32)
         rho = per_row("rho")
 
-        def square_rows(rows, total):
-            nc.scalar.activation(out=scrap("scalar", N), in_=rows, func=ACT.Square, accum_out=total)
-
-        def dot_z_b(r):
-            nc.vector.scalar_tensor_tensor(
-                out=scrap("vector", N), in0=z_sb[:, r, :], scalar=1.0, in1=b_bc[:],
-                op0=ALU.mult, op1=ALU.mult, accum_out=col(z_dot_b, r),
+        def square_v(r, h):
+            nc.scalar.activation(
+                out=scrap("scalar", HALF), in_=v_sb[:, r, half_cols(h)], func=ACT.Square,
+                accum_out=v_sq_parts[:, r, h : h + 1],
             )
 
-        def turn_v(r, copiers):
+        def square_z(r, j):
+            nc.scalar.activation(
+                out=scrap("scalar", N_TILE), in_=z_sb[:, r, tile_cols(j)], func=ACT.Square,
+                accum_out=z_sq_parts[:, r, j : j + 1],
+            )
+
+        def dot_z_b(r, h):
+            nc.vector.scalar_tensor_tensor(
+                out=scrap("vector", HALF), in0=z_sb[:, r, half_cols(h)], scalar=1.0, in1=b_bc[:, half_cols(h)],
+                op0=ALU.mult, op1=ALU.mult, accum_out=z_dot_b_parts[:, r, h : h + 1],
+            )
+
+        def turn_v(r):
             v_pairs = v_sb[:, r, :].bitcast(F32)
             for h in range(2):
                 turned = psum.tile([P, 2, 2, P], F32, tag="bank")
@@ -151,27 +177,26 @@ def tile_paralleldirectpoincaredynamics_kernel(
                     .bitcast(F32)
                     .rearrange("p (i b u) -> p i b u", i=2, u=2)
                 )
-                if copiers[h] == "scalar":
-                    nc.scalar.copy(out=side_by_side, in_=turned[:].rearrange("p i u b -> p i b u"))
-                else:
-                    nc.vector.tensor_copy(out=side_by_side, in_=turned[:].rearrange("p i u b -> p i b u"))
+                nc.scalar.copy(out=side_by_side, in_=turned[:].rearrange("p i u b -> p i b u"))
 
         def quantise_v(r):
             nc.vector.quantize_mx(
                 out=v_codes[:, r, :].bitcast(FP8X4), scales=v_planes[:, r, :], in_=grouped[:, r, :]
             )
 
-        def multiply(j, r):
-            acc = psum.tile([P, N_TILE], F32, tag="bank", name="mv_%d_%d" % (r, j))
-            mv[r][j] = acc
+        def multiply(i, r):
+            c0, width = w_starts[i], W_LOADS[i]
+            j, at = c0 // N_TILE, c0 % N_TILE
+            if mv[r][j] is None:
+                mv[r][j] = psum.tile([P, N_TILE], F32, tag="bank", name="mv_%d_%d" % (r, j))
             for g in range(PASSES):
                 rows = slice(g * P, (g + 1) * P)
                 nc.tensor.matmul_mx(
-                    out=acc[:],
+                    out=mv[r][j][:, at : at + width],
                     lhsT=v_codes[:, r, rows].bitcast(FP8X4),
                     lhsT_scale=v_planes[:, r, rows],
-                    rhs=w_words[:, g, tile_cols(j)].bitcast(FP8X4),
-                    rhs_scale=w_planes[4 * g : P, tile_cols(j)],
+                    rhs=w_words[:, g, c0 : c0 + width].bitcast(FP8X4),
+                    rhs_scale=w_planes[4 * g : P, c0 : c0 + width],
                     start=(g == 0),
                     stop=(g == PASSES - 1),
                 )
@@ -200,6 +225,37 @@ def tile_paralleldirectpoincaredynamics_kernel(
                 in1=mv[r][j][:], op0=ALU.mult, op1=ALU.add,
             )
 
+        lines = {"vector": [], "scalar": []}
+        issued = {"vector": 0, "scalar": 0}
+
+        def defer(engine, action, *args):
+            lines[engine].append(lambda: action(*args))
+
+        def fill(engine, n):
+            for i in range(n):
+                if issued[engine] < len(lines[engine]):
+                    lines[engine][issued[engine]]()
+                    issued[engine] += 1
+
+        def fill_up_to(engine, count):
+            fill(engine, max(0, count - issued[engine]))
+
+        for r in blocks:
+            for h in range(2):
+                defer("vector", dot_z_b, r, h)
+        for j in range(N_TILES):
+            for r in blocks:
+                defer("vector", dot_mv_z, j, r)
+        vector_sums = len(lines["vector"])
+        for r in blocks:
+            for h in range(2):
+                defer("scalar", square_v, r, h)
+        scalar_v_sums = len(lines["scalar"])
+        for r in blocks:
+            for j in range(N_TILES):
+                defer("scalar", square_z, r, j)
+        scalar_sums = len(lines["scalar"])
+
         warm = per_row("warm", 1)
         nc.scalar.activation(out=warm[:], in_=one_col[:], func=ACT.Ln)
         for h in range(2):
@@ -209,25 +265,25 @@ def tile_paralleldirectpoincaredynamics_kernel(
                     out=spread[:, tile_cols(i)], lhsT=ones[:], rhs=b_row[:, tile_cols(2 * h + i)],
                     start=True, stop=True,
                 )
-            nc.vector.tensor_copy(out=b_bc[:, h * HALF : (h + 1) * HALF], in_=spread[:])
+            nc.vector.tensor_copy(out=b_bc[:, half_cols(h)], in_=spread[:])
         nc.scalar.activation(
             out=scrap("scalar", N // P), in_=b_cols[:], func=ACT.Square, accum_out=b_sq_part[:, 0:1]
         )
-        turn_v(0, ("scalar", "scalar"))
-        turn_v(1, ("scalar", "scalar"))
+        fill("scalar", 1)
+        turn_v(0)
+        turn_v(1)
         b_sq_ps = psum.tile([P, ROW_BLOCKS], F32, tag="bank")
         nc.tensor.matmul(out=b_sq_ps[:], lhsT=ones_f32[:], rhs=b_sq_part[:], start=True, stop=True)
         b_sq = per_row("b_sq", 1)
-        dot_z_b(0)
+        fill("vector", 2)
         quantise_v(0)
         quantise_v(1)
         nc.vector.tensor_copy(out=b_sq[:], in_=b_sq_ps[:, 0:1])
-        dot_z_b(1)
-        square_rows(v_sb[:, 0, :], col(v_sq, 0))
-        square_rows(v_sb[:, 1, :], col(v_sq, 1))
-        for j in range(N_TILES):
+        fill("vector", 2)
+        fill_up_to("scalar", scalar_v_sums)
+        for i in range(len(W_LOADS)):
             for r in blocks:
-                multiply(j, r)
+                multiply(i, r)
 
         b_sq_c = per_row("b_sq_c", 1)
         b_norm = per_row("b_norm", 1)
@@ -238,6 +294,7 @@ def tile_paralleldirectpoincaredynamics_kernel(
         two_beta = per_row("two_beta", 1)
         y2 = per_row("y2", 1)
         y2_minus_1 = per_row("y2_minus_1", 1)
+        v_sq = per_row("v_sq")
         v_sq_c = per_row("v_sq_c")
         v_norm = per_row("v_norm")
         v_clip = per_row("v_clip")
@@ -253,31 +310,20 @@ def tile_paralleldirectpoincaredynamics_kernel(
         nc.gpsimd.tensor_scalar_max(out=b_sq_c[:], in0=b_sq[:], scalar1=EPS_SQ)
         nc.gpsimd.tensor_tensor(out=b_norm[:], in0=b_sq_c[:], in1=plus_half[:, 0:1], op=ALU.pow)
         nc.gpsimd.tensor_tensor(out=b_rnorm[:], in0=b_sq_c[:], in1=minus_half[:, 0:1], op=ALU.pow)
+        nc.gpsimd.tensor_add(out=v_sq[:], in0=v_sq_parts[:, :, 0], in1=v_sq_parts[:, :, 1])
         nc.gpsimd.tensor_scalar_max(out=v_sq_c[:], in0=v_sq[:], scalar1=EPS_SQ)
         nc.gpsimd.tensor_tensor(out=v_norm[:], in0=v_sq_c[:], in1=plus_half[:], op=ALU.pow)
         nc.gpsimd.tensor_scalar_min(out=v_clip[:], in0=v_norm[:], scalar1=MAX_NORM)
         nc.gpsimd.tensor_tensor(out=v_rnorm[:], in0=v_sq_c[:], in1=minus_half[:], op=ALU.pow)
 
-        later = []
-        issued = {"n": 0}
-
-        def fill(n):
-            for i in range(n):
-                if issued["n"] < len(later):
-                    later[issued["n"]]()
-                    issued["n"] += 1
-
-        def defer(action, *args):
-            later.append(lambda: action(*args))
-
-        for j in range(N_TILES):
-            for r in blocks:
-                defer(dot_mv_z, j, r)
-        sums_deferred = len(later)
+        def bank_sums(j, r, vector_fill, scalar_fill):
+            square_mv(j, r)
+            fill("scalar", scalar_fill)
+            dot_mv_b(j, r)
+            fill("vector", vector_fill)
 
         for j, r in ((0, 0), (0, 1), (1, 0)):
-            square_mv(j, r)
-            dot_mv_b(j, r)
+            bank_sums(j, r, 1, 1)
         nc.scalar.activation(out=ln_plus[:], in_=v_clip[:], func=ACT.Ln, bias=one_col[:], scale=1.0)
         nc.scalar.activation(out=ln_minus[:], in_=v_clip[:], func=ACT.Ln, bias=one_col[:], scale=-1.0)
         nc.scalar.activation(out=step[:], in_=step_raw[:], func=ACT.Sigmoid)
@@ -293,9 +339,7 @@ def tile_paralleldirectpoincaredynamics_kernel(
         nc.gpsimd.tensor_scalar_mul(out=minus_beta[:], in0=beta[:], scalar1=-1.0)
         nc.gpsimd.tensor_scalar_mul(out=tau[:], in0=horizon[:], scalar1=step[:])
         for j, r in ((1, 1), (2, 0), (2, 1)):
-            square_mv(j, r)
-            dot_mv_b(j, r)
-            fill(1)
+            bank_sums(j, r, 0, 0)
         mv_sq_pair = per_row("mv_sq_pair")
         mv_sq_head = per_row("mv_sq_head")
         mv_dot_b_head = per_row("mv_dot_b_head")
@@ -304,10 +348,8 @@ def tile_paralleldirectpoincaredynamics_kernel(
         nc.gpsimd.tensor_add(out=mv_sq_head[:], in0=mv_sq_pair[:], in1=mv_sq_parts[:, :, 2])
         nc.vector.tensor_reduce(out=mv_dot_b_head[:], in_=mv_dot_b_parts[:, :, 0:last], axis=AX.X, op=ALU.add)
         nc.vector.tensor_scalar_mul(out=head_2bpt[:], in0=mv_dot_b_head[:], scalar1=two_beta[:])
-        square_mv(last, 0)
-        dot_mv_b(last, 0)
-        square_mv(last, 1)
-        dot_mv_b(last, 1)
+        bank_sums(last, 0, 2, 0)
+        bank_sums(last, 1, 0, 0)
 
         mv_sq_c = per_row("mv_sq_c")
         mv_rnorm = per_row("mv_rnorm")
@@ -321,8 +363,8 @@ def tile_paralleldirectpoincaredynamics_kernel(
                 scalar2=EPS_SQ, op0=ALU.add, op1=ALU.max,
             )
         nc.gpsimd.tensor_tensor(out=mv_rnorm[:], in0=mv_sq_c[:], in1=minus_half[:], op=ALU.pow)
-        square_rows(z_sb[:, 0, :], col(z_sq, 0))
-        fill(2)
+        fill("scalar", 4)
+        fill("vector", 2)
         nc.vector.scalar_tensor_tensor(
             out=mv_dot_2bpt[:], in0=mv_dot_b_parts[:, :, last], scalar=two_beta[:], in1=head_2bpt[:],
             op0=ALU.mult, op1=ALU.add,
@@ -332,10 +374,9 @@ def tile_paralleldirectpoincaredynamics_kernel(
             nc.scalar.activation(
                 out=col(x_norm, r), in_=col(mv_rnorm, r), func=ACT.Tanh, scale=col(mv_sq_gain, r)
             )
-        square_rows(z_sb[:, 1, :], col(z_sq, 1))
-        fill(1)
+        fill_up_to("scalar", scalar_sums)
+        fill("vector", 1)
         nc.vector.tensor_mul(out=two_xy_unit[:], in0=mv_rnorm[:], in1=mv_dot_2bpt[:])
-        fill(1)
         one_plus_2xy = per_row("one_plus_2xy")
         x2 = per_row("x2")
         den_raw = per_row("den_raw")
@@ -350,6 +391,8 @@ def tile_paralleldirectpoincaredynamics_kernel(
         mv_coef = per_row("mv_coef")
         b_coef = per_row("b_coef")
         mv_rcoef = per_row("mv_rcoef")
+        z_sq = per_row("z_sq")
+        z_dot_b = per_row("z_dot_b")
         one_minus_z2 = per_row("one_minus_z2")
         z_gap = per_row("z_gap")
         half_lambda = per_row("half_lambda")
@@ -376,16 +419,20 @@ def tile_paralleldirectpoincaredynamics_kernel(
         nc.gpsimd.tensor_tensor(out=num_norm[:], in0=num_sq[:], in1=plus_half[:], op=ALU.pow)
         nc.vector.tensor_scalar_max(out=den[:], in0=den_raw[:], scalar1=EPS)
         nc.vector.tensor_mul(out=mv_coef[:], in0=x_coef[:], in1=kappa[:])
-        fill(1)
+        nc.vector.tensor_reduce(out=z_sq[:], in_=z_sq_parts[:], axis=AX.X, op=ALU.add)
+        fill("vector", 1)
         nc.vector.reciprocal(out=rden[:], in_=den[:])
         nc.vector.reciprocal(out=mv_rcoef[:], in_=mv_coef[:])
         nc.vector.tensor_scalar(
             out=one_minus_z2[:], in0=z_sq[:], scalar1=-1.0, scalar2=1.0, op0=ALU.mult, op1=ALU.add
         )
+        fill_up_to("vector", vector_sums)
         nc.vector.tensor_mul(out=rho[:], in0=b_coef[:], in1=mv_rcoef[:])
         nc.vector.tensor_scalar_max(out=z_gap[:], in0=one_minus_z2[:], scalar1=EPS)
-        for j in range(N_TILES):
-            defer(make_u, 0, j)
+        for r in blocks:
+            for j in range(N_TILES):
+                defer("vector", make_u, r, j)
+        fill("vector", 1)
 
         v0_norm = per_row("v0_norm")
         vt_norm = per_horizon("vt_norm")
@@ -397,6 +444,7 @@ def tile_paralleldirectpoincaredynamics_kernel(
             )
         nc.vector.reciprocal(out=half_lambda[:], in_=z_gap[:])
         nc.vector.reciprocal(out=num_rnorm[:], in_=num_norm[:])
+        fill("vector", 1)
         for r in blocks:
             nc.vector.tensor_scalar(
                 out=vt_norm[:, r, :], in0=tau[:], scalar1=col(v0_norm, r), scalar2=EPS,
@@ -419,17 +467,17 @@ def tile_paralleldirectpoincaredynamics_kernel(
         nc.vector.scalar_tensor_tensor(
             out=w_factor[:], in0=num_rnorm[:], scalar=MAX_NORM, in1=rden[:], op0=ALU.mult, op1=ALU.min
         )
-        fill(max(0, sums_deferred - issued["n"]))
+        nc.vector.tensor_reduce(out=z_dot_b[:], in_=z_dot_b_parts[:], axis=AX.X, op=ALU.add)
         nc.vector.tensor_reduce(out=mv_dot_z[:], in_=mv_dot_z_parts[:], axis=AX.X, op=ALU.add)
-        nc.vector.tensor_mul(out=z_dot_u_b[:], in0=rho[:], in1=z_dot_b[:])
         nc.vector.reciprocal(out=vt_rnorm[:], in_=vt_norm[:])
         nc.vector.tensor_mul(out=v0_sq[:], in0=v0_norm[:], in1=v0_norm[:])
+        nc.vector.tensor_mul(out=z_dot_u_b[:], in0=rho[:], in1=z_dot_b[:])
         nc.vector.tensor_mul(out=u_scale[:], in0=mv_coef[:], in1=w_factor[:])
-        nc.vector.tensor_add(out=z_dot_u[:], in0=z_dot_u_b[:], in1=mv_dot_z[:])
         nc.vector.tensor_mul(
             out=tau_over_norm[:], in0=vt_rnorm[:],
             in1=tau[:].unsqueeze(1).to_broadcast([P, ROW_BLOCKS, T]),
         )
+        nc.vector.tensor_add(out=z_dot_u[:], in0=z_dot_u_b[:], in1=mv_dot_z[:])
         nc.vector.tensor_mul(out=u_gain[:], in0=one_minus_z2[:], in1=u_scale[:])
         nc.vector.scalar_tensor_tensor(
             out=two_z_dot_v0[:], in0=z_dot_u[:], scalar=2.0, in1=u_scale[:], op0=ALU.mult, op1=ALU.mult
@@ -449,7 +497,7 @@ def tile_paralleldirectpoincaredynamics_kernel(
         den2 = per_horizon("den2")
         rden2 = per_horizon("rden2")
         nc.vector.tensor_mul(out=sigma[:], in0=vt_tanh[:], in1=tau_over_norm[:])
-        fill(1)
+        fill("vector", 1)
         for r in blocks:
             nc.vector.scalar_tensor_tensor(
                 out=s2[:, r, :], in0=sigma[:, r, :], scalar=col(v0_sq, r), in1=sigma[:, r, :],
@@ -479,46 +527,40 @@ def tile_paralleldirectpoincaredynamics_kernel(
         )
         nc.scalar.activation(out=num2_norm[:], in_=num2_sq[:], func=ACT.Sqrt)
         nc.vector.tensor_scalar_max(out=den2[:], in0=den2_raw[:], scalar1=EPS)
-        fill(1)
+        fill("vector", 1)
         nc.vector.reciprocal(out=rden2[:], in_=den2[:])
         o_factor = per_horizon("o_factor")
         a_fin = per_horizon("a_fin")
         c_fin = per_horizon("c_fin")
         nc.vector.reciprocal(out=num2_rnorm[:], in_=num2_norm[:])
-        fill(1)
         nc.vector.scalar_tensor_tensor(
             out=o_factor[:], in0=num2_rnorm[:], scalar=MAX_NORM, in1=rden2[:], op0=ALU.mult, op1=ALU.min
         )
-        fill(1)
         nc.vector.tensor_mul(out=a_fin[:], in0=z_coef[:], in1=o_factor[:])
         nc.vector.tensor_mul(out=c_fin[:], in0=u_coef[:], in1=o_factor[:])
+        fill("vector", 2)
 
-        def scale_z(res, r, t, cols):
-            nc.scalar.activation(
-                out=res[:, cols], in_=z_sb[:, r, cols], func=ACT.Copy, scale=a_fin[:, r, t : t + 1]
-            )
-
-        def add_u(res, r, t, cols):
-            nc.vector.scalar_tensor_tensor(
-                out=res[:, cols], in0=u_sb[:, r, cols], scalar=c_fin[:, r, t : t + 1],
-                in1=res[:, cols], op0=ALU.mult, op1=ALU.add,
-            )
-            nc.sync.dma_start(out=out[r * P : (r + 1) * P, t, cols], in_=res[:, cols])
-
-        def emit(r, t, pieces):
+        def emit(r, t, pieces, fill_between):
             res = stream.tile([P, N], F32, name="res")
             width = N // pieces
             for i in range(pieces):
-                scale_z(res, r, t, slice(i * width, (i + 1) * width))
-            if (r, t) == (0, 0):
-                fill(len(later))
+                cols = slice(i * width, (i + 1) * width)
+                nc.scalar.activation(
+                    out=res[:, cols], in_=z_sb[:, r, cols], func=ACT.Copy, scale=a_fin[:, r, t : t + 1]
+                )
             for i in range(pieces):
-                add_u(res, r, t, slice(i * width, (i + 1) * width))
+                cols = slice(i * width, (i + 1) * width)
+                if r == 0:
+                    fill_up_to("vector", vector_sums + (i + 1) * N_TILES // pieces)
+                nc.vector.scalar_tensor_tensor(
+                    out=res[:, cols], in0=u_sb[:, r, cols], scalar=c_fin[:, r, t : t + 1],
+                    in1=res[:, cols], op0=ALU.mult, op1=ALU.add,
+                )
+                nc.sync.dma_start(out=out[r * P : (r + 1) * P, t, cols], in_=res[:, cols])
+            fill("vector", fill_between)
 
         for r in blocks:
             for t in range(T):
                 first = (r, t) == (0, 0)
                 final = (r, t) == (ROW_BLOCKS - 1, T - 1)
-                emit(r, t, 4 if first or final else 1)
-                if r == 0 and t < N_TILES:
-                    make_u(1, t)
+                emit(r, t, N_TILES if first or final else 1, 2 if first else 1)

@@ -40,7 +40,8 @@ def tile_paralleldirectpoincaredynamics_kernel(
         keep = ctx.enter_context(tc.tile_pool(name="keep", bufs=1))
         small = ctx.enter_context(tc.tile_pool(name="small", bufs=1))
         stream = ctx.enter_context(tc.tile_pool(name="stream", bufs=6))
-        psum = ctx.enter_context(tc.psum_pool(name="psum", bufs=8))
+        own = ctx.enter_context(tc.tile_pool(name="own", bufs=2))
+        psum = ctx.enter_context(tc.psum_pool(name="psum", bufs=1))
         ctx.enter_context(tc.manual_schedule())
 
         def per_row(name, width=ROW_BLOCKS):
@@ -51,6 +52,9 @@ def tile_paralleldirectpoincaredynamics_kernel(
 
         def col(scalars, r):
             return scalars[:, r : r + 1]
+
+        def bank(index, shape, dtype, name):
+            return psum.tile(shape, dtype, tag="bank%d" % index, name=name)
 
         def tile_cols(j):
             return slice(j * N_TILE, (j + 1) * N_TILE)
@@ -138,6 +142,7 @@ def tile_paralleldirectpoincaredynamics_kernel(
         v_codes = keep.tile([P, ROW_BLOCKS, PASSES * P], U32, align_bytes=64)
         v_planes = keep.tile([P, ROW_BLOCKS, PASSES * P], U8, align_bytes=64)
         mv = [[None] * N_TILES for r in blocks]
+        u_ps = [[None] * N_TILES for r in blocks]
         mv_sq_parts = small.tile([P, ROW_BLOCKS, N_TILES], F32)
         mv_dot_b_parts = small.tile([P, ROW_BLOCKS, N_TILES], F32)
         mv_dot_z_parts = small.tile([P, ROW_BLOCKS, N_TILES], F32)
@@ -165,7 +170,7 @@ def tile_paralleldirectpoincaredynamics_kernel(
         def turn_v(r):
             v_pairs = v_sb[:, r, :].bitcast(F32)
             for h in range(2):
-                turned = psum.tile([P, 2, 2, P], F32, tag="bank")
+                turned = bank(2 + 2 * r + h, [P, 2, 2, P], F32, "turned")
                 for i in range(2):
                     g = 2 * h + i
                     for u in range(2):
@@ -188,7 +193,7 @@ def tile_paralleldirectpoincaredynamics_kernel(
             c0, width = w_starts[i], W_LOADS[i]
             j, at = c0 // N_TILE, c0 % N_TILE
             if mv[r][j] is None:
-                mv[r][j] = psum.tile([P, N_TILE], F32, tag="bank", name="mv_%d_%d" % (r, j))
+                mv[r][j] = bank(ROW_BLOCKS * j + r, [P, N_TILE], F32, "mv_%d_%d" % (r, j))
             for g in range(PASSES):
                 rows = slice(g * P, (g + 1) * P)
                 nc.tensor.matmul_mx(
@@ -224,6 +229,8 @@ def tile_paralleldirectpoincaredynamics_kernel(
                 out=u_sb[:, r, tile_cols(j)], in0=b_bc[:, tile_cols(j)], scalar=col(rho, r),
                 in1=mv[r][j][:], op0=ALU.mult, op1=ALU.add,
             )
+            u_ps[r][j] = bank(ROW_BLOCKS * j + r, [P, N_TILE], F32, "u_%d_%d" % (r, j))
+            nc.tensor.matmul(out=u_ps[r][j][:], lhsT=ident[:], rhs=u_sb[:, r, tile_cols(j)], start=True, stop=True)
 
         lines = {"vector": [], "scalar": []}
         issued = {"vector": 0, "scalar": 0}
@@ -259,7 +266,7 @@ def tile_paralleldirectpoincaredynamics_kernel(
         warm = per_row("warm", 1)
         nc.scalar.activation(out=warm[:], in_=one_col[:], func=ACT.Ln)
         for h in range(2):
-            spread = psum.tile([P, HALF], BF16, tag="bank")
+            spread = bank(h, [P, HALF], BF16, "spread")
             for i in range(HALF // N_TILE):
                 nc.tensor.matmul(
                     out=spread[:, tile_cols(i)], lhsT=ones[:], rhs=b_row[:, tile_cols(2 * h + i)],
@@ -272,7 +279,7 @@ def tile_paralleldirectpoincaredynamics_kernel(
         fill("scalar", 1)
         turn_v(0)
         turn_v(1)
-        b_sq_ps = psum.tile([P, ROW_BLOCKS], F32, tag="bank")
+        b_sq_ps = bank(6, [P, ROW_BLOCKS], F32, "b_sq_ps")
         nc.tensor.matmul(out=b_sq_ps[:], lhsT=ones_f32[:], rhs=b_sq_part[:], start=True, stop=True)
         b_sq = per_row("b_sq", 1)
         fill("vector", 2)
@@ -538,29 +545,50 @@ def tile_paralleldirectpoincaredynamics_kernel(
         )
         nc.vector.tensor_mul(out=a_fin[:], in0=z_coef[:], in1=o_factor[:])
         nc.vector.tensor_mul(out=c_fin[:], in0=u_coef[:], in1=o_factor[:])
-        fill("vector", 2)
+        fill("vector", 4)
 
-        def emit(r, t, pieces, fill_between):
+        def emit(r, t, stores, fill_between):
             res = stream.tile([P, N], F32, name="res")
-            width = N // pieces
-            for i in range(pieces):
+            width = N // stores
+            for i in range(stores):
                 cols = slice(i * width, (i + 1) * width)
                 nc.scalar.activation(
                     out=res[:, cols], in_=z_sb[:, r, cols], func=ACT.Copy, scale=a_fin[:, r, t : t + 1]
                 )
-            for i in range(pieces):
-                cols = slice(i * width, (i + 1) * width)
-                if r == 0:
-                    fill_up_to("vector", vector_sums + (i + 1) * N_TILES // pieces)
+            for j in range(N_TILES):
+                fill_up_to("vector", vector_sums + r * N_TILES + j + 1)
                 nc.vector.scalar_tensor_tensor(
-                    out=res[:, cols], in0=u_sb[:, r, cols], scalar=c_fin[:, r, t : t + 1],
-                    in1=res[:, cols], op0=ALU.mult, op1=ALU.add,
+                    out=res[:, tile_cols(j)], in0=u_ps[r][j][:], scalar=c_fin[:, r, t : t + 1],
+                    in1=res[:, tile_cols(j)], op0=ALU.mult, op1=ALU.add,
                 )
-                nc.sync.dma_start(out=out[r * P : (r + 1) * P, t, cols], in_=res[:, cols])
+                if (j + 1) % (N_TILES // stores) == 0:
+                    cols = slice((j + 1) * N_TILE - width, (j + 1) * N_TILE)
+                    nc.sync.dma_start(out=out[r * P : (r + 1) * P, t, cols], in_=res[:, cols])
             fill("vector", fill_between)
 
-        for r in blocks:
-            for t in range(T):
-                first = (r, t) == (0, 0)
-                final = (r, t) == (ROW_BLOCKS - 1, T - 1)
-                emit(r, t, N_TILES if first or final else 1, 2 if first else 1)
+        def compute_on_gpsimd(r, t):
+            z_part = own.tile([P, N], F32, name="z_part")
+            u_part = own.tile([P, N], F32, name="u_part")
+            nc.gpsimd.tensor_scalar(
+                out=z_part[:], in0=z_sb[:, r, :], scalar1=a_fin[:, r, t : t + 1], scalar2=0.0,
+                op0=ALU.mult, op1=ALU.add,
+            )
+            nc.gpsimd.tensor_scalar(
+                out=u_part[:], in0=u_sb[:, r, :], scalar1=c_fin[:, r, t : t + 1], scalar2=0.0,
+                op0=ALU.mult, op1=ALU.add,
+            )
+            nc.gpsimd.tensor_add(out=z_part[:], in0=z_part[:], in1=u_part[:])
+            return z_part
+
+        for_gpsimd = [(0, T - 2), (0, T - 1), (1, T - 1)]
+        for_vector = [(r, t) for r in blocks for t in range(T) if (r, t) not in for_gpsimd]
+        ratio = 4
+        for k in range(len(for_vector)):
+            r, t = for_vector[k]
+            if k % ratio == 0 and k // ratio < len(for_gpsimd):
+                fill_up_to("vector", vector_sums + (for_gpsimd[k // ratio][0] + 1) * N_TILES)
+                theirs = compute_on_gpsimd(*for_gpsimd[k // ratio])
+            emit(r, t, N_TILES if k < ratio or k == len(for_vector) - 1 else 1, 0)
+            if k % ratio == ratio - 1:
+                rg, tg = for_gpsimd[k // ratio]
+                nc.sync.dma_start(out=out[rg * P : (rg + 1) * P, tg, :], in_=theirs[:])

@@ -22,7 +22,7 @@ PASSES = K // K_PASS
 N_TILE = 512
 N_TILES = N // N_TILE
 HALF = N // 2
-W_LOADS = (512, 512, 512, 512)
+W_LOADS = (512, 512, 512, 256, 256)
 
 EPS = 1e-7
 EPS_SQ = 1e-14
@@ -588,7 +588,7 @@ def tile_paralleldirectpoincaredynamics_kernel(
             if k % ratio == 0 and k // ratio < len(for_gpsimd):
                 fill_up_to("vector", vector_sums + (for_gpsimd[k // ratio][0] + 1) * N_TILES)
                 theirs = compute_on_gpsimd(*for_gpsimd[k // ratio])
-            emit(r, t, N_TILES if k < ratio or k == len(for_vector) - 1 else 1, 0)
+            emit(r, t, N_TILES if k == 0 else 2 if k < ratio else 1, 0)
             if k % ratio == ratio - 1:
                 rg, tg = for_gpsimd[k // ratio]
                 nc.sync.dma_start(out=out[rg * P : (rg + 1) * P, tg, :], in_=theirs[:])

@@ -75,8 +75,8 @@ def tile_paralleldirectpoincaredynamics_kernel(
         horizon = per_row("horizon", T)
         b_sq_part = per_row("b_sq_part")
         ident = keep.tile([P, P], F32)
-        nc.vector.memset(b_row[:].bitcast(I32), 0)
         nc.vector.memset(w_planes[:].bitcast(I32), 0)
+        nc.vector.memset(b_row[:].bitcast(I32), 0)
         nc.vector.memset(ones[:], 1.0)
         nc.vector.memset(ones_f32[:], 1.0)
         nc.gpsimd.memset(one_col[:], 1.0)
@@ -114,16 +114,19 @@ def tile_paralleldirectpoincaredynamics_kernel(
                 out=w_words[:, :, c0:c1], in_=w_bytes[:, :, c0 * PACK : c1 * PACK].bitcast(I32)
             )
 
+        load_scales()
         nc.sync.dma_start(out=b_row[0:1, :], in_=b.rearrange("(o n) -> o n", o=1))
         nc.sync.dma_start(out=b_cols[:], in_=b.rearrange("(p c) -> p c", p=P))
         nc.scalar.dma_start(out=step_raw[:], in_=step_sizes.partition_broadcast(P))
         load_v(0)
         load_z(0)
         load_v(1)
+        load_w(0)
         load_z(1)
-        load_scales()
-        for i in range(len(W_LOADS)):
-            load_w(i)
+        load_w(1)
+        load_w(2)
+        load_w(3)
+        load_w(4)
 
         squares = keep.tile([P, 2 * N], BF16)
         products = keep.tile([P, 2 * N], F32)

@@ -22,7 +22,7 @@ PASSES = K // K_PASS
 N_TILE = 512
 N_TILES = N // N_TILE
 HALF = N // 2
-W_LOADS = (512, 512, 512, 256, 256)
+W_LOADS = ((0, 0, 4), (1, 0, 4), (2, 0, 4), (3, 0, 2), (3, 2, 2))
 
 EPS = 1e-7
 EPS_SQ = 1e-14
@@ -93,7 +93,6 @@ def tile_paralleldirectpoincaredynamics_kernel(
         z_sb = keep.tile([P, ROW_BLOCKS, N], BF16)
         w_words = keep.tile([P, PASSES, N], I32, align_bytes=64)
         w_bytes = W_words.rearrange("g p n t -> p g (n t)")
-        w_starts = [sum(W_LOADS[:i]) for i in range(len(W_LOADS))]
 
         def load_v(r):
             nc.sync.dma_start(out=v_sb[:, r, :], in_=v_init[r * P : (r + 1) * P, :])
@@ -109,9 +108,10 @@ def tile_paralleldirectpoincaredynamics_kernel(
                 )
 
         def load_w(i):
-            c0, c1 = w_starts[i], w_starts[i] + W_LOADS[i]
+            j, g0, count = W_LOADS[i]
             nc.sync.dma_start(
-                out=w_words[:, :, c0:c1], in_=w_bytes[:, :, c0 * PACK : c1 * PACK].bitcast(I32)
+                out=w_words[:, g0 : g0 + count, tile_cols(j)],
+                in_=w_bytes[:, g0 : g0 + count, j * N_TILE * PACK : (j + 1) * N_TILE * PACK].bitcast(I32),
             )
 
         load_scales()
@@ -193,18 +193,17 @@ def tile_paralleldirectpoincaredynamics_kernel(
             )
 
         def multiply(i, r):
-            c0, width = w_starts[i], W_LOADS[i]
-            j, at = c0 // N_TILE, c0 % N_TILE
+            j, g0, count = W_LOADS[i]
             if mv[r][j] is None:
                 mv[r][j] = bank(ROW_BLOCKS * j + r, [P, N_TILE], F32, "mv_%d_%d" % (r, j))
-            for g in range(PASSES):
+            for g in range(g0, g0 + count):
                 rows = slice(g * P, (g + 1) * P)
                 nc.tensor.matmul_mx(
-                    out=mv[r][j][:, at : at + width],
+                    out=mv[r][j][:],
                     lhsT=v_codes[:, r, rows].bitcast(FP8X4),
                     lhsT_scale=v_planes[:, r, rows],
-                    rhs=w_words[:, g, c0 : c0 + width].bitcast(FP8X4),
-                    rhs_scale=w_planes[4 * g : P, c0 : c0 + width],
+                    rhs=w_words[:, g, tile_cols(j)].bitcast(FP8X4),
+                    rhs_scale=w_planes[4 * g : P, tile_cols(j)],
                     start=(g == 0),
                     stop=(g == PASSES - 1),
                 )
@@ -349,7 +348,7 @@ def tile_paralleldirectpoincaredynamics_kernel(
         nc.gpsimd.tensor_scalar_mul(out=minus_beta[:], in0=beta[:], scalar1=-1.0)
         nc.gpsimd.tensor_scalar_mul(out=tau[:], in0=horizon[:], scalar1=step[:])
         for j, r in ((1, 1), (2, 0), (2, 1)):
-            bank_sums(j, r, 0, 0)
+            bank_sums(j, r, 1, 0)
         mv_sq_pair = per_row("mv_sq_pair")
         mv_sq_head = per_row("mv_sq_head")
         mv_dot_b_head = per_row("mv_dot_b_head")
@@ -358,7 +357,7 @@ def tile_paralleldirectpoincaredynamics_kernel(
         nc.gpsimd.tensor_add(out=mv_sq_head[:], in0=mv_sq_pair[:], in1=mv_sq_parts[:, :, 2])
         nc.vector.tensor_reduce(out=mv_dot_b_head[:], in_=mv_dot_b_parts[:, :, 0:last], axis=AX.X, op=ALU.add)
         nc.vector.tensor_scalar_mul(out=head_2bpt[:], in0=mv_dot_b_head[:], scalar1=two_beta[:])
-        bank_sums(last, 0, 2, 0)
+        bank_sums(last, 0, 1, 0)
         bank_sums(last, 1, 0, 0)
 
         mv_sq_c = per_row("mv_sq_c")
@@ -454,7 +453,6 @@ def tile_paralleldirectpoincaredynamics_kernel(
             )
         nc.vector.reciprocal(out=half_lambda[:], in_=z_gap[:])
         nc.vector.reciprocal(out=num_rnorm[:], in_=num_norm[:])
-        fill("vector", 1)
         for r in blocks:
             nc.vector.tensor_scalar(
                 out=vt_norm[:, r, :], in0=tau[:], scalar1=col(v0_norm, r), scalar2=EPS,
@@ -543,9 +541,11 @@ def tile_paralleldirectpoincaredynamics_kernel(
         a_fin = per_horizon("a_fin")
         c_fin = per_horizon("c_fin")
         nc.vector.reciprocal(out=num2_rnorm[:], in_=num2_norm[:])
+        fill("vector", 1)
         nc.vector.scalar_tensor_tensor(
             out=o_factor[:], in0=num2_rnorm[:], scalar=MAX_NORM, in1=rden2[:], op0=ALU.mult, op1=ALU.min
         )
+        fill("vector", 1)
         nc.vector.tensor_mul(out=a_fin[:], in0=z_coef[:], in1=o_factor[:])
         nc.vector.tensor_mul(out=c_fin[:], in0=u_coef[:], in1=o_factor[:])
         fill("vector", 4)

@@ -88,7 +88,7 @@ def tile_paralleldirectpoincaredynamics_kernel(
             nc.gpsimd.memset(horizon[:, t : t + 1], float(t + 1))
 
         step_raw = small.tile([P, 1], BF16)
-        b_cols = small.tile([P, N // P], BF16)
+        b_cols = small.tile([P, N // 16], BF16)
         v_sb = keep.tile([P, ROW_BLOCKS, K], BF16)
         z_sb = keep.tile([P, ROW_BLOCKS, N], BF16)
         w_words = keep.tile([P, PASSES, N], I32, align_bytes=64)
@@ -116,8 +116,8 @@ def tile_paralleldirectpoincaredynamics_kernel(
 
         load_scales()
         nc.sync.dma_start(out=b_row[0:1, :], in_=b.rearrange("(o n) -> o n", o=1))
-        nc.sync.dma_start(out=b_cols[:], in_=b.rearrange("(p c) -> p c", p=P))
-        nc.scalar.dma_start(out=step_raw[:], in_=step_sizes.partition_broadcast(P))
+        nc.sync.dma_start(out=b_cols[0:16, :], in_=b.rearrange("(p c) -> p c", p=16))
+        nc.sync.dma_start(out=step_raw[0:1, :], in_=step_sizes.rearrange("(o n) -> o n", o=1))
         load_v(0)
         load_z(0)
         load_v(1)
@@ -276,18 +276,20 @@ def tile_paralleldirectpoincaredynamics_kernel(
                 )
             nc.vector.tensor_copy(out=b_bc[:, half_cols(h)], in_=spread[:])
         nc.scalar.activation(
-            out=scrap("scalar", N // P), in_=b_cols[:], func=ACT.Square, accum_out=b_sq_part[:, 0:1]
+            out=scrap("scalar", N // 16)[0:16, :], in_=b_cols[0:16, :], func=ACT.Square, accum_out=b_sq_part[0:16, 0:1]
         )
+        nc.scalar.copy(out=b_sq_part[0:1, 1:2], in_=step_raw[0:1, :])
         fill("scalar", 1)
         turn_v(0)
         turn_v(1)
         b_sq_ps = bank(6, [P, ROW_BLOCKS], F32, "b_sq_ps")
         nc.tensor.matmul(out=b_sq_ps[:], lhsT=ones_f32[:], rhs=b_sq_part[:], start=True, stop=True)
-        b_sq = per_row("b_sq", 1)
+        b_sq_and_step = per_row("b_sq_and_step")
+        b_sq = b_sq_and_step[:, 0:1]
         fill("vector", 2)
         quantise_v(0)
         quantise_v(1)
-        nc.vector.tensor_copy(out=b_sq[:], in_=b_sq_ps[:, 0:1])
+        nc.vector.tensor_copy(out=b_sq_and_step[:], in_=b_sq_ps[:])
         fill("vector", 2)
         fill_up_to("scalar", scalar_v_sums)
         for i in range(len(W_LOADS)):
@@ -316,7 +318,7 @@ def tile_paralleldirectpoincaredynamics_kernel(
         beta_sq = per_row("beta_sq", 1)
         step = per_row("step", 1)
         tau = per_row("tau", T)
-        nc.gpsimd.tensor_scalar_max(out=b_sq_c[:], in0=b_sq[:], scalar1=EPS_SQ)
+        nc.gpsimd.tensor_scalar_max(out=b_sq_c[:], in0=b_sq, scalar1=EPS_SQ)
         nc.gpsimd.tensor_tensor(out=b_norm[:], in0=b_sq_c[:], in1=plus_half[:, 0:1], op=ALU.pow)
         nc.gpsimd.tensor_tensor(out=b_rnorm[:], in0=b_sq_c[:], in1=minus_half[:, 0:1], op=ALU.pow)
         nc.gpsimd.tensor_add(out=v_sq[:], in0=v_sq_parts[:, :, 0], in1=v_sq_parts[:, :, 1])
@@ -335,7 +337,7 @@ def tile_paralleldirectpoincaredynamics_kernel(
             bank_sums(j, r, 1, 1)
         nc.scalar.activation(out=ln_plus[:], in_=v_clip[:], func=ACT.Ln, bias=one_col[:], scale=1.0)
         nc.scalar.activation(out=ln_minus[:], in_=v_clip[:], func=ACT.Ln, bias=one_col[:], scale=-1.0)
-        nc.scalar.activation(out=step[:], in_=step_raw[:], func=ACT.Sigmoid)
+        nc.scalar.activation(out=step[:], in_=b_sq_and_step[:, 1:2], func=ACT.Sigmoid)
         nc.scalar.activation(out=b_tanh[:], in_=b_norm[:], func=ACT.Tanh)
         nc.gpsimd.tensor_sub(out=ln_diff[:], in0=ln_plus[:], in1=ln_minus[:])
         nc.gpsimd.tensor_mul(out=two_gain[:], in0=ln_diff[:], in1=v_rnorm[:])
@@ -343,7 +345,7 @@ def tile_paralleldirectpoincaredynamics_kernel(
         nc.gpsimd.tensor_mul(out=beta[:], in0=b_tanh[:], in1=b_rnorm[:])
         nc.gpsimd.tensor_scalar_mul(out=two_beta[:], in0=beta[:], scalar1=2.0)
         nc.gpsimd.tensor_mul(out=beta_sq[:], in0=beta[:], in1=beta[:])
-        nc.gpsimd.tensor_mul(out=y2[:], in0=beta_sq[:], in1=b_sq[:])
+        nc.gpsimd.tensor_mul(out=y2[:], in0=beta_sq[:], in1=b_sq)
         nc.gpsimd.tensor_scalar_add(out=y2_minus_1[:], in0=y2[:], scalar1=-1.0)
         nc.gpsimd.tensor_scalar_mul(out=minus_beta[:], in0=beta[:], scalar1=-1.0)
         nc.gpsimd.tensor_scalar_mul(out=tau[:], in0=horizon[:], scalar1=step[:])

@@ -286,8 +286,9 @@ def tile_paralleldirectpoincaredynamics_kernel(
         nc.tensor.matmul(out=b_sq_ps[:], lhsT=ones_f32[:], rhs=b_sq_part[:], start=True, stop=True)
         b_sq_and_step = per_row("b_sq_and_step")
         b_sq = b_sq_and_step[:, 0:1]
-        fill("vector", 2)
+        fill("vector", 1)
         quantise_v(0)
+        fill("vector", 1)
         quantise_v(1)
         nc.vector.tensor_copy(out=b_sq_and_step[:], in_=b_sq_ps[:])
         fill("vector", 2)

@@ -75,7 +75,7 @@ def tile_paralleldirectpoincaredynamics_kernel(
         horizon = per_row("horizon", T)
         b_sq_part = per_row("b_sq_part")
         ident = keep.tile([P, P], F32)
-        nc.vector.memset(w_planes[:].bitcast(I32), 0)
+        nc.gpsimd.memset(w_planes[:].bitcast(F32), 0.0)
         nc.vector.memset(b_row[:].bitcast(I32), 0)
         nc.vector.memset(ones[:], 1.0)
         nc.vector.memset(ones_f32[:], 1.0)

@@ -28,6 +28,8 @@ EPS = 1e-7
 EPS_SQ = 1e-14
 TINY = 1e-24
 MAX_NORM = 1.0 - 1e-5
+MAX_SQ = MAX_NORM * MAX_NORM
+ROOT_SLOPE = -0.5 / MAX_SQ
 
 FLOPS = 2 * B * K * N
 
@@ -405,9 +407,14 @@ def tile_paralleldirectpoincaredynamics_kernel(
         mv_rcoef = per_row("mv_rcoef")
         z_sq = per_row("z_sq")
         z_dot_b = per_row("z_dot_b")
+        mv_dot_z = per_row("mv_dot_z")
+        z_dot_u_b = per_row("z_dot_u_b")
+        z_dot_u = per_row("z_dot_u")
         one_minus_z2 = per_row("one_minus_z2")
+        z2_minus_1 = per_row("z2_minus_1")
         z_gap = per_row("z_gap")
         half_lambda = per_row("half_lambda")
+        tau_lambda = per_horizon("tau_lambda")
         nc.vector.tensor_mul(out=x2[:], in0=x_norm[:], in1=x_norm[:])
         for r in blocks:
             nc.vector.tensor_scalar(
@@ -416,10 +423,10 @@ def tile_paralleldirectpoincaredynamics_kernel(
             )
         nc.vector.tensor_mul(out=kappa[:], in0=x_norm[:], in1=mv_rnorm[:])
         nc.vector.scalar_tensor_tensor(
-            out=den_raw[:], in0=x2[:], scalar=y2[:], in1=one_plus_2xy[:], op0=ALU.mult, op1=ALU.add
+            out=sum_sq[:], in0=x2[:], scalar=y2_minus_1[:], in1=one_plus_2xy[:], op0=ALU.add, op1=ALU.add
         )
         nc.vector.scalar_tensor_tensor(
-            out=sum_sq[:], in0=x2[:], scalar=y2_minus_1[:], in1=one_plus_2xy[:], op0=ALU.add, op1=ALU.add
+            out=den_raw[:], in0=x2[:], scalar=y2[:], in1=one_plus_2xy[:], op0=ALU.mult, op1=ALU.add
         )
         nc.vector.tensor_scalar_add(out=x_coef[:], in0=one_plus_2xy[:], scalar1=y2[:])
         nc.vector.tensor_scalar(
@@ -429,129 +436,98 @@ def tile_paralleldirectpoincaredynamics_kernel(
             out=num_sq[:], in0=sum_sq[:], scalar=TINY, in1=den_raw[:], op0=ALU.max, op1=ALU.mult
         )
         nc.gpsimd.tensor_tensor(out=num_norm[:], in0=num_sq[:], in1=plus_half[:], op=ALU.pow)
-        nc.vector.tensor_scalar_max(out=den[:], in0=den_raw[:], scalar1=EPS)
         nc.vector.tensor_mul(out=mv_coef[:], in0=x_coef[:], in1=kappa[:])
+        nc.vector.tensor_scalar_max(out=den[:], in0=den_raw[:], scalar1=EPS)
         nc.vector.tensor_reduce(out=z_sq[:], in_=z_sq_parts[:], axis=AX.X, op=ALU.add)
-        fill("vector", 1)
-        nc.vector.reciprocal(out=rden[:], in_=den[:])
         nc.vector.reciprocal(out=mv_rcoef[:], in_=mv_coef[:])
+        nc.vector.reciprocal(out=rden[:], in_=den[:])
         nc.vector.tensor_scalar(
             out=one_minus_z2[:], in0=z_sq[:], scalar1=-1.0, scalar2=1.0, op0=ALU.mult, op1=ALU.add
         )
-        fill_up_to("vector", vector_sums)
         nc.vector.tensor_mul(out=rho[:], in0=b_coef[:], in1=mv_rcoef[:])
         nc.vector.tensor_scalar_max(out=z_gap[:], in0=one_minus_z2[:], scalar1=EPS)
         for r in blocks:
             for j in range(N_TILES):
                 defer("vector", make_u, r, j)
+        fill_up_to("vector", vector_sums)
+        nc.vector.reciprocal(out=half_lambda[:], in_=z_gap[:])
+        nc.vector.tensor_reduce(out=z_dot_b[:], in_=z_dot_b_parts[:], axis=AX.X, op=ALU.add)
+        nc.vector.tensor_reduce(out=mv_dot_z[:], in_=mv_dot_z_parts[:], axis=AX.X, op=ALU.add)
+        for r in blocks:
+            nc.vector.tensor_scalar_mul(out=tau_lambda[:, r, :], in0=tau[:], scalar1=col(half_lambda, r))
+        nc.vector.tensor_mul(out=z_dot_u_b[:], in0=rho[:], in1=z_dot_b[:])
+        nc.vector.tensor_scalar_add(out=z2_minus_1[:], in0=z_sq[:], scalar1=-1.0)
         fill("vector", 1)
+        nc.vector.tensor_add(out=z_dot_u[:], in0=z_dot_u_b[:], in1=mv_dot_z[:])
 
         v0_norm = per_row("v0_norm")
-        vt_norm = per_horizon("vt_norm")
         vt_tanh = per_horizon("vt_tanh")
         for r in blocks:
             nc.vector.tensor_scalar(
                 out=col(v0_norm, r), in0=col(num_norm, r), scalar1=col(rden, r), scalar2=MAX_NORM,
                 op0=ALU.mult, op1=ALU.min,
             )
-        nc.vector.reciprocal(out=half_lambda[:], in_=z_gap[:])
-        nc.vector.reciprocal(out=num_rnorm[:], in_=num_norm[:])
-        for r in blocks:
-            nc.vector.tensor_scalar(
-                out=vt_norm[:, r, :], in0=tau[:], scalar1=col(v0_norm, r), scalar2=EPS,
-                op0=ALU.mult, op1=ALU.max,
-            )
             nc.scalar.activation(
-                out=vt_tanh[:, r, :], in_=vt_norm[:, r, :], func=ACT.Tanh, scale=col(half_lambda, r)
+                out=vt_tanh[:, r, :], in_=tau_lambda[:, r, :], func=ACT.Tanh, scale=col(v0_norm, r)
             )
-
-        w_factor = per_row("w_factor")
-        u_scale = per_row("u_scale")
-        mv_dot_z = per_row("mv_dot_z")
-        z_dot_u_b = per_row("z_dot_u_b")
-        z_dot_u = per_row("z_dot_u")
-        two_z_dot_v0 = per_row("two_z_dot_v0")
-        v0_sq = per_row("v0_sq")
-        u_gain = per_row("u_gain")
-        vt_rnorm = per_horizon("vt_rnorm")
-        tau_over_norm = per_horizon("tau_over_norm")
+        u_unit = per_row("u_unit")
+        two_z_dot_unit = per_row("two_z_dot_unit")
+        unit_gain = per_row("unit_gain")
+        nc.vector.reciprocal(out=num_rnorm[:], in_=num_norm[:])
+        fill("vector", 1)
+        nc.vector.tensor_mul(out=u_unit[:], in0=mv_coef[:], in1=num_rnorm[:])
         nc.vector.scalar_tensor_tensor(
-            out=w_factor[:], in0=num_rnorm[:], scalar=MAX_NORM, in1=rden[:], op0=ALU.mult, op1=ALU.min
+            out=two_z_dot_unit[:], in0=z_dot_u[:], scalar=2.0, in1=u_unit[:], op0=ALU.mult, op1=ALU.mult
         )
-        nc.vector.tensor_reduce(out=z_dot_b[:], in_=z_dot_b_parts[:], axis=AX.X, op=ALU.add)
-        nc.vector.tensor_reduce(out=mv_dot_z[:], in_=mv_dot_z_parts[:], axis=AX.X, op=ALU.add)
-        nc.vector.reciprocal(out=vt_rnorm[:], in_=vt_norm[:])
-        nc.vector.tensor_mul(out=v0_sq[:], in0=v0_norm[:], in1=v0_norm[:])
-        nc.vector.tensor_mul(out=z_dot_u_b[:], in0=rho[:], in1=z_dot_b[:])
-        nc.vector.tensor_mul(out=u_scale[:], in0=mv_coef[:], in1=w_factor[:])
-        nc.vector.tensor_mul(
-            out=tau_over_norm[:], in0=vt_rnorm[:],
-            in1=tau[:].unsqueeze(1).to_broadcast([P, ROW_BLOCKS, T]),
-        )
-        nc.vector.tensor_add(out=z_dot_u[:], in0=z_dot_u_b[:], in1=mv_dot_z[:])
-        nc.vector.tensor_mul(out=u_gain[:], in0=one_minus_z2[:], in1=u_scale[:])
         nc.vector.scalar_tensor_tensor(
-            out=two_z_dot_v0[:], in0=z_dot_u[:], scalar=2.0, in1=u_scale[:], op0=ALU.mult, op1=ALU.mult
+            out=unit_gain[:], in0=u_unit[:], scalar=ROOT_SLOPE, in1=one_minus_z2[:], op0=ALU.mult, op1=ALU.mult
         )
 
-        sigma = per_horizon("sigma")
+        two_zs = per_horizon("two_zs")
         s2 = per_horizon("s2")
-        one_plus_2zs = per_horizon("one_plus_2zs")
-        z2_plus_2zs = per_horizon("z2_plus_2zs")
+        z2_s2 = per_horizon("z2_s2")
         z_coef = per_horizon("z_coef")
-        u_coef = per_horizon("u_coef")
+        z_coef_scaled = per_horizon("z_coef_scaled")
+        u_coef_scaled = per_horizon("u_coef_scaled")
         den2_raw = per_horizon("den2_raw")
         sum2_sq = per_horizon("sum2_sq")
-        num2_sq = per_horizon("num2_sq")
-        num2_norm = per_horizon("num2_norm")
-        num2_rnorm = per_horizon("num2_rnorm")
         den2 = per_horizon("den2")
         rden2 = per_horizon("rden2")
-        nc.vector.tensor_mul(out=sigma[:], in0=vt_tanh[:], in1=tau_over_norm[:])
-        fill("vector", 1)
-        for r in blocks:
-            nc.vector.scalar_tensor_tensor(
-                out=s2[:, r, :], in0=sigma[:, r, :], scalar=col(v0_sq, r), in1=sigma[:, r, :],
-                op0=ALU.mult, op1=ALU.mult,
-            )
-        for r in blocks:
-            nc.vector.tensor_scalar(
-                out=one_plus_2zs[:, r, :], in0=sigma[:, r, :], scalar1=col(two_z_dot_v0, r), scalar2=1.0,
-                op0=ALU.mult, op1=ALU.add,
-            )
-        for r in blocks:
-            nc.vector.tensor_scalar(
-                out=z2_plus_2zs[:, r, :], in0=sigma[:, r, :], scalar1=col(two_z_dot_v0, r),
-                scalar2=col(z_sq, r), op0=ALU.mult, op1=ALU.add,
-            )
-        for r in blocks:
-            nc.vector.scalar_tensor_tensor(
-                out=den2_raw[:, r, :], in0=s2[:, r, :], scalar=col(z_sq, r), in1=one_plus_2zs[:, r, :],
-                op0=ALU.mult, op1=ALU.add,
-            )
-        nc.vector.tensor_add(out=sum2_sq[:], in0=s2[:], in1=z2_plus_2zs[:])
-        for r in blocks:
-            nc.vector.tensor_scalar_mul(out=u_coef[:, r, :], in0=sigma[:, r, :], scalar1=col(u_gain, r))
-        nc.vector.tensor_add(out=z_coef[:], in0=s2[:], in1=one_plus_2zs[:])
-        nc.vector.scalar_tensor_tensor(
-            out=num2_sq[:], in0=sum2_sq[:], scalar=TINY, in1=den2_raw[:], op0=ALU.max, op1=ALU.mult
-        )
-        nc.scalar.activation(out=num2_norm[:], in_=num2_sq[:], func=ACT.Sqrt)
-        nc.vector.tensor_scalar_max(out=den2[:], in0=den2_raw[:], scalar1=EPS)
-        fill("vector", 1)
-        nc.vector.reciprocal(out=rden2[:], in_=den2[:])
+        out_sq = per_horizon("out_sq")
+        newton = per_horizon("newton")
         o_factor = per_horizon("o_factor")
         a_fin = per_horizon("a_fin")
         c_fin = per_horizon("c_fin")
-        nc.vector.reciprocal(out=num2_rnorm[:], in_=num2_norm[:])
-        fill("vector", 1)
+
+        def each_horizon(scalars):
+            return scalars[:].unsqueeze(2).to_broadcast([P, ROW_BLOCKS, T])
+
+        for r in blocks:
+            nc.vector.scalar_tensor_tensor(
+                out=z2_s2[:, r, :], in0=vt_tanh[:, r, :], scalar=col(z_sq, r), in1=vt_tanh[:, r, :],
+                op0=ALU.mult, op1=ALU.mult,
+            )
+        nc.vector.tensor_mul(out=two_zs[:], in0=vt_tanh[:], in1=each_horizon(two_z_dot_unit))
+        nc.vector.tensor_mul(out=s2[:], in0=vt_tanh[:], in1=vt_tanh[:])
+        nc.vector.tensor_mul(out=u_coef_scaled[:], in0=vt_tanh[:], in1=each_horizon(unit_gain))
         nc.vector.scalar_tensor_tensor(
-            out=o_factor[:], in0=num2_rnorm[:], scalar=MAX_NORM, in1=rden2[:], op0=ALU.mult, op1=ALU.min
+            out=den2_raw[:], in0=two_zs[:], scalar=1.0, in1=z2_s2[:], op0=ALU.add, op1=ALU.add
+        )
+        nc.vector.scalar_tensor_tensor(
+            out=z_coef[:], in0=two_zs[:], scalar=1.0, in1=s2[:], op0=ALU.add, op1=ALU.add
+        )
+        nc.vector.tensor_scalar_max(out=den2[:], in0=den2_raw[:], scalar1=EPS)
+        nc.vector.tensor_add(out=sum2_sq[:], in0=z_coef[:], in1=each_horizon(z2_minus_1))
+        nc.vector.reciprocal(out=rden2[:], in_=den2[:])
+        nc.vector.tensor_scalar_mul(out=z_coef_scaled[:], in0=z_coef[:], scalar1=ROOT_SLOPE)
+        nc.vector.tensor_mul(out=out_sq[:], in0=sum2_sq[:], in1=rden2[:])
+        nc.vector.tensor_scalar(
+            out=newton[:], in0=out_sq[:], scalar1=MAX_SQ, scalar2=-3.0 * MAX_SQ, op0=ALU.max, op1=ALU.add
         )
         fill("vector", 1)
-        nc.vector.tensor_mul(out=a_fin[:], in0=z_coef[:], in1=o_factor[:])
-        nc.vector.tensor_mul(out=c_fin[:], in0=u_coef[:], in1=o_factor[:])
-        fill("vector", 4)
+        nc.vector.tensor_mul(out=o_factor[:], in0=newton[:], in1=rden2[:])
+        nc.vector.tensor_mul(out=a_fin[:], in0=z_coef_scaled[:], in1=o_factor[:])
+        nc.vector.tensor_mul(out=c_fin[:], in0=u_coef_scaled[:], in1=o_factor[:])
 
         def emit(r, t, stores, fill_between):
             res = stream.tile([P, N], F32, name="res")
@@ -594,7 +570,7 @@ def tile_paralleldirectpoincaredynamics_kernel(
             if k % ratio == 0 and k // ratio < len(for_gpsimd):
                 fill_up_to("vector", vector_sums + (for_gpsimd[k // ratio][0] + 1) * N_TILES)
                 theirs = compute_on_gpsimd(*for_gpsimd[k // ratio])
-            emit(r, t, N_TILES if k == 0 else 2 if k < ratio else 1, 0)
+            emit(r, t, N_TILES if k == 0 else 2 if k < ratio else 1, 1 if k > 0 else 0)
             if k % ratio == ratio - 1:
                 rg, tg = for_gpsimd[k // ratio]
                 nc.sync.dma_start(out=out[rg * P : (rg + 1) * P, tg, :], in_=theirs[:])

@@ -22,6 +22,8 @@ PASSES = K // K_PASS
 N_TILE = 512
 N_TILES = N // N_TILE
 HALF = N // 2
+B_ROWS = 8
+B_WORDS = N // 2 // B_ROWS
 W_LOADS = ((0, 0, 4), (1, 0, 4), (2, 0, 4), (3, 0, 2), (3, 2, 2))
 
 EPS = 1e-7
@@ -68,8 +70,7 @@ def tile_paralleldirectpoincaredynamics_kernel(
         last = N_TILES - 1
 
         w_planes = keep.tile([P, N], U8, align_bytes=64)
-        b_row = keep.tile([P, N], BF16)
-        ones = keep.tile([P, P], BF16)
+        b_rows = keep.tile([P, 2 * B_WORDS], BF16)
         ones_f32 = keep.tile([P, P], F32)
         one_col = per_row("one_col", 1)
         plus_half = per_row("plus_half")
@@ -78,8 +79,7 @@ def tile_paralleldirectpoincaredynamics_kernel(
         b_sq_part = per_row("b_sq_part")
         ident = keep.tile([P, P], F32)
         nc.gpsimd.memset(w_planes[:].bitcast(F32), 0.0)
-        nc.vector.memset(b_row[:].bitcast(I32), 0)
-        nc.vector.memset(ones[:], 1.0)
+        nc.vector.memset(b_rows[:].bitcast(I32), 0)
         nc.vector.memset(ones_f32[:], 1.0)
         nc.gpsimd.memset(one_col[:], 1.0)
         make_identity(nc, ident[:])
@@ -90,7 +90,6 @@ def tile_paralleldirectpoincaredynamics_kernel(
             nc.gpsimd.memset(horizon[:, t : t + 1], float(t + 1))
 
         step_raw = small.tile([P, 1], BF16)
-        b_cols = small.tile([P, N // 16], BF16)
         v_sb = keep.tile([P, ROW_BLOCKS, K], BF16)
         z_sb = keep.tile([P, ROW_BLOCKS, N], BF16)
         w_words = keep.tile([P, PASSES, N], I32, align_bytes=64)
@@ -117,8 +116,7 @@ def tile_paralleldirectpoincaredynamics_kernel(
             )
 
         load_scales()
-        nc.sync.dma_start(out=b_row[0:1, :], in_=b.rearrange("(o n) -> o n", o=1))
-        nc.sync.dma_start(out=b_cols[0:16, :], in_=b.rearrange("(p c) -> p c", p=16))
+        nc.sync.dma_start(out=b_rows[0:B_ROWS, :], in_=b.rearrange("(p c) -> p c", p=B_ROWS))
         nc.sync.dma_start(out=step_raw[0:1, :], in_=step_sizes.rearrange("(o n) -> o n", o=1))
         load_v(0)
         load_z(0)
@@ -254,10 +252,6 @@ def tile_paralleldirectpoincaredynamics_kernel(
         for r in blocks:
             for h in range(2):
                 defer("vector", dot_z_b, r, h)
-        for j in range(N_TILES):
-            for r in blocks:
-                defer("vector", dot_mv_z, j, r)
-        vector_sums = len(lines["vector"])
         for r in blocks:
             for h in range(2):
                 defer("scalar", square_v, r, h)
@@ -269,22 +263,27 @@ def tile_paralleldirectpoincaredynamics_kernel(
 
         warm = per_row("warm", 1)
         nc.scalar.activation(out=warm[:], in_=one_col[:], func=ACT.Ln)
+        b_turned_ps = bank(0, [P, P], F32, "b_turned_ps")
+        nc.tensor.transpose(b_turned_ps[:], b_rows[:].bitcast(F32), ident[:])
+        b_turned = keep.tile([P, B_ROWS], F32)
+        nc.vector.tensor_copy(out=b_turned[:], in_=b_turned_ps[:, 0:B_ROWS])
         for h in range(2):
-            spread = bank(h, [P, HALF], BF16, "spread")
-            for i in range(HALF // N_TILE):
-                nc.tensor.matmul(
-                    out=spread[:, tile_cols(i)], lhsT=ones[:], rhs=b_row[:, tile_cols(2 * h + i)],
-                    start=True, stop=True,
+            spread = bank(6 + h, [P, N_TILE], F32, "spread")
+            for i in range(B_ROWS // 2):
+                m = h * B_ROWS // 2 + i
+                nc.tensor.transpose(
+                    spread[:, i * P : (i + 1) * P], b_turned[:, m : m + 1].to_broadcast([P, P]), ident[:]
                 )
-            nc.vector.tensor_copy(out=b_bc[:, half_cols(h)], in_=spread[:])
+            nc.vector.tensor_copy(out=b_bc[:, half_cols(h)].bitcast(F32), in_=spread[:])
         nc.scalar.activation(
-            out=scrap("scalar", N // 16)[0:16, :], in_=b_cols[0:16, :], func=ACT.Square, accum_out=b_sq_part[0:16, 0:1]
+            out=scrap("scalar", 2 * B_WORDS)[0:B_ROWS, :], in_=b_rows[0:B_ROWS, :], func=ACT.Square,
+            accum_out=b_sq_part[0:B_ROWS, 0:1],
         )
         nc.scalar.copy(out=b_sq_part[0:1, 1:2], in_=step_raw[0:1, :])
         fill("scalar", 1)
         turn_v(0)
         turn_v(1)
-        b_sq_ps = bank(6, [P, ROW_BLOCKS], F32, "b_sq_ps")
+        b_sq_ps = bank(1, [P, ROW_BLOCKS], F32, "b_sq_ps")
         nc.tensor.matmul(out=b_sq_ps[:], lhsT=ones_f32[:], rhs=b_sq_part[:], start=True, stop=True)
         b_sq_and_step = per_row("b_sq_and_step")
         b_sq = b_sq_and_step[:, 0:1]
@@ -330,14 +329,17 @@ def tile_paralleldirectpoincaredynamics_kernel(
         nc.gpsimd.tensor_scalar_min(out=v_clip[:], in0=v_norm[:], scalar1=MAX_NORM)
         nc.gpsimd.tensor_tensor(out=v_rnorm[:], in0=v_sq_c[:], in1=minus_half[:], op=ALU.pow)
 
-        def bank_sums(j, r, vector_fill, scalar_fill):
-            square_mv(j, r)
-            fill("scalar", scalar_fill)
+        def dots(j, r):
             dot_mv_b(j, r)
-            fill("vector", vector_fill)
+            dot_mv_z(j, r)
 
-        for j, r in ((0, 0), (0, 1), (1, 0)):
-            bank_sums(j, r, 1, 1)
+        square_mv(0, 0)
+        dots(0, 0)
+        square_mv(0, 1)
+        dots(0, 1)
+        fill("scalar", 1)
+        square_mv(1, 0)
+        dots(1, 0)
         nc.scalar.activation(out=ln_plus[:], in_=v_clip[:], func=ACT.Ln, bias=one_col[:], scale=1.0)
         nc.scalar.activation(out=ln_minus[:], in_=v_clip[:], func=ACT.Ln, bias=one_col[:], scale=-1.0)
         nc.scalar.activation(out=step[:], in_=b_sq_and_step[:, 1:2], func=ACT.Sigmoid)
@@ -352,8 +354,12 @@ def tile_paralleldirectpoincaredynamics_kernel(
         nc.gpsimd.tensor_scalar_add(out=y2_minus_1[:], in0=y2[:], scalar1=-1.0)
         nc.gpsimd.tensor_scalar_mul(out=minus_beta[:], in0=beta[:], scalar1=-1.0)
         nc.gpsimd.tensor_scalar_mul(out=tau[:], in0=horizon[:], scalar1=step[:])
-        for j, r in ((1, 1), (2, 0), (2, 1)):
-            bank_sums(j, r, 1, 0)
+        dots(1, 1)
+        square_mv(2, 0)
+        square_mv(2, 1)
+        square_mv(1, 1)
+        dots(2, 0)
+        dots(2, 1)
         mv_sq_pair = per_row("mv_sq_pair")
         mv_sq_head = per_row("mv_sq_head")
         mv_dot_b_head = per_row("mv_dot_b_head")
@@ -362,9 +368,11 @@ def tile_paralleldirectpoincaredynamics_kernel(
         nc.gpsimd.tensor_add(out=mv_sq_head[:], in0=mv_sq_pair[:], in1=mv_sq_parts[:, :, 2])
         nc.vector.tensor_reduce(out=mv_dot_b_head[:], in_=mv_dot_b_parts[:, :, 0:last], axis=AX.X, op=ALU.add)
         nc.vector.tensor_scalar_mul(out=head_2bpt[:], in0=mv_dot_b_head[:], scalar1=two_beta[:])
-        bank_sums(last, 0, 1, 0)
-        bank_sums(last, 1, 0, 0)
+        for r in blocks:
+            square_mv(last, r)
+        dot_mv_b(last, 0)
 
+        vec = nc.vector
         mv_sq_c = per_row("mv_sq_c")
         mv_rnorm = per_row("mv_rnorm")
         mv_sq_gain = per_row("mv_sq_gain")
@@ -377,20 +385,19 @@ def tile_paralleldirectpoincaredynamics_kernel(
                 scalar2=EPS_SQ, op0=ALU.add, op1=ALU.max,
             )
         nc.gpsimd.tensor_tensor(out=mv_rnorm[:], in0=mv_sq_c[:], in1=minus_half[:], op=ALU.pow)
-        fill("scalar", 4)
-        fill("vector", 2)
-        nc.vector.scalar_tensor_tensor(
+        vec.tensor_mul(out=mv_sq_gain[:], in0=mv_sq_c[:], in1=gain[:])
+        dot_mv_b(last, 1)
+        vec.scalar_tensor_tensor(
             out=mv_dot_2bpt[:], in0=mv_dot_b_parts[:, :, last], scalar=two_beta[:], in1=head_2bpt[:],
             op0=ALU.mult, op1=ALU.add,
         )
-        nc.vector.tensor_mul(out=mv_sq_gain[:], in0=mv_sq_c[:], in1=gain[:])
+        fill("scalar", 3)
         for r in blocks:
             nc.scalar.activation(
                 out=col(x_norm, r), in_=col(mv_rnorm, r), func=ACT.Tanh, scale=col(mv_sq_gain, r)
             )
+        vec.tensor_mul(out=two_xy_unit[:], in0=mv_rnorm[:], in1=mv_dot_2bpt[:])
         fill_up_to("scalar", scalar_sums)
-        fill("vector", 1)
-        nc.vector.tensor_mul(out=two_xy_unit[:], in0=mv_rnorm[:], in1=mv_dot_2bpt[:])
         one_plus_2xy = per_row("one_plus_2xy")
         x2 = per_row("x2")
         den_raw = per_row("den_raw")
@@ -405,83 +412,78 @@ def tile_paralleldirectpoincaredynamics_kernel(
         mv_coef = per_row("mv_coef")
         b_coef = per_row("b_coef")
         mv_rcoef = per_row("mv_rcoef")
+        vec.tensor_mul(out=x2[:], in0=x_norm[:], in1=x_norm[:])
+        for r in blocks:
+            vec.tensor_scalar(
+                out=col(one_plus_2xy, r), in0=col(x_norm, r), scalar1=col(two_xy_unit, r), scalar2=1.0,
+                op0=ALU.mult, op1=ALU.add,
+            )
+        vec.tensor_mul(out=kappa[:], in0=x_norm[:], in1=mv_rnorm[:])
+        vec.scalar_tensor_tensor(
+            out=sum_sq[:], in0=x2[:], scalar=y2_minus_1[:], in1=one_plus_2xy[:], op0=ALU.add, op1=ALU.add
+        )
+        vec.scalar_tensor_tensor(
+            out=den_raw[:], in0=x2[:], scalar=y2[:], in1=one_plus_2xy[:], op0=ALU.mult, op1=ALU.add
+        )
+        vec.tensor_scalar_add(out=x_coef[:], in0=one_plus_2xy[:], scalar1=y2[:])
+        vec.tensor_scalar(
+            out=b_coef[:], in0=x2[:], scalar1=minus_beta[:], scalar2=beta[:], op0=ALU.mult, op1=ALU.add
+        )
+        vec.scalar_tensor_tensor(
+            out=num_sq[:], in0=sum_sq[:], scalar=TINY, in1=den_raw[:], op0=ALU.max, op1=ALU.mult
+        )
+        nc.gpsimd.tensor_tensor(out=num_norm[:], in0=num_sq[:], in1=plus_half[:], op=ALU.pow)
+        vec.tensor_mul(out=mv_coef[:], in0=x_coef[:], in1=kappa[:])
+        vec.tensor_scalar_max(out=den[:], in0=den_raw[:], scalar1=EPS)
+        dot_mv_z(last, 0)
+        vec.reciprocal(out=mv_rcoef[:], in_=mv_coef[:])
+        vec.reciprocal(out=rden[:], in_=den[:])
+        dot_mv_z(last, 1)
+        vec.tensor_mul(out=rho[:], in0=b_coef[:], in1=mv_rcoef[:])
+
         z_sq = per_row("z_sq")
-        z_dot_b = per_row("z_dot_b")
-        mv_dot_z = per_row("mv_dot_z")
-        z_dot_u_b = per_row("z_dot_u_b")
-        z_dot_u = per_row("z_dot_u")
         one_minus_z2 = per_row("one_minus_z2")
         z2_minus_1 = per_row("z2_minus_1")
         z_gap = per_row("z_gap")
         half_lambda = per_row("half_lambda")
-        tau_lambda = per_horizon("tau_lambda")
-        nc.vector.tensor_mul(out=x2[:], in0=x_norm[:], in1=x_norm[:])
-        for r in blocks:
-            nc.vector.tensor_scalar(
-                out=col(one_plus_2xy, r), in0=col(x_norm, r), scalar1=col(two_xy_unit, r), scalar2=1.0,
-                op0=ALU.mult, op1=ALU.add,
-            )
-        nc.vector.tensor_mul(out=kappa[:], in0=x_norm[:], in1=mv_rnorm[:])
-        nc.vector.scalar_tensor_tensor(
-            out=sum_sq[:], in0=x2[:], scalar=y2_minus_1[:], in1=one_plus_2xy[:], op0=ALU.add, op1=ALU.add
-        )
-        nc.vector.scalar_tensor_tensor(
-            out=den_raw[:], in0=x2[:], scalar=y2[:], in1=one_plus_2xy[:], op0=ALU.mult, op1=ALU.add
-        )
-        nc.vector.tensor_scalar_add(out=x_coef[:], in0=one_plus_2xy[:], scalar1=y2[:])
-        nc.vector.tensor_scalar(
-            out=b_coef[:], in0=x2[:], scalar1=minus_beta[:], scalar2=beta[:], op0=ALU.mult, op1=ALU.add
-        )
-        nc.vector.scalar_tensor_tensor(
-            out=num_sq[:], in0=sum_sq[:], scalar=TINY, in1=den_raw[:], op0=ALU.max, op1=ALU.mult
-        )
-        nc.gpsimd.tensor_tensor(out=num_norm[:], in0=num_sq[:], in1=plus_half[:], op=ALU.pow)
-        nc.vector.tensor_mul(out=mv_coef[:], in0=x_coef[:], in1=kappa[:])
-        nc.vector.tensor_scalar_max(out=den[:], in0=den_raw[:], scalar1=EPS)
-        nc.vector.tensor_reduce(out=z_sq[:], in_=z_sq_parts[:], axis=AX.X, op=ALU.add)
-        nc.vector.reciprocal(out=mv_rcoef[:], in_=mv_coef[:])
-        nc.vector.reciprocal(out=rden[:], in_=den[:])
-        nc.vector.tensor_scalar(
-            out=one_minus_z2[:], in0=z_sq[:], scalar1=-1.0, scalar2=1.0, op0=ALU.mult, op1=ALU.add
-        )
-        nc.vector.tensor_mul(out=rho[:], in0=b_coef[:], in1=mv_rcoef[:])
-        nc.vector.tensor_scalar_max(out=z_gap[:], in0=one_minus_z2[:], scalar1=EPS)
-        for r in blocks:
-            for j in range(N_TILES):
-                defer("vector", make_u, r, j)
-        fill_up_to("vector", vector_sums)
-        nc.vector.reciprocal(out=half_lambda[:], in_=z_gap[:])
-        nc.vector.tensor_reduce(out=z_dot_b[:], in_=z_dot_b_parts[:], axis=AX.X, op=ALU.add)
-        nc.vector.tensor_reduce(out=mv_dot_z[:], in_=mv_dot_z_parts[:], axis=AX.X, op=ALU.add)
-        for r in blocks:
-            nc.vector.tensor_scalar_mul(out=tau_lambda[:, r, :], in0=tau[:], scalar1=col(half_lambda, r))
-        nc.vector.tensor_mul(out=z_dot_u_b[:], in0=rho[:], in1=z_dot_b[:])
-        nc.vector.tensor_scalar_add(out=z2_minus_1[:], in0=z_sq[:], scalar1=-1.0)
-        fill("vector", 1)
-        nc.vector.tensor_add(out=z_dot_u[:], in0=z_dot_u_b[:], in1=mv_dot_z[:])
-
         v0_norm = per_row("v0_norm")
+        v0_lambda = per_row("v0_lambda")
         vt_tanh = per_horizon("vt_tanh")
-        for r in blocks:
-            nc.vector.tensor_scalar(
-                out=col(v0_norm, r), in0=col(num_norm, r), scalar1=col(rden, r), scalar2=MAX_NORM,
-                op0=ALU.mult, op1=ALU.min,
-            )
-            nc.scalar.activation(
-                out=vt_tanh[:, r, :], in_=tau_lambda[:, r, :], func=ACT.Tanh, scale=col(v0_norm, r)
-            )
+        z_dot_b = per_row("z_dot_b")
+        mv_dot_z = per_row("mv_dot_z")
+        z_dot_u_b = per_row("z_dot_u_b")
+        z_dot_u = per_row("z_dot_u")
         u_unit = per_row("u_unit")
         two_z_dot_unit = per_row("two_z_dot_unit")
         unit_gain = per_row("unit_gain")
-        nc.vector.reciprocal(out=num_rnorm[:], in_=num_norm[:])
-        fill("vector", 1)
-        nc.vector.tensor_mul(out=u_unit[:], in0=mv_coef[:], in1=num_rnorm[:])
-        nc.vector.scalar_tensor_tensor(
-            out=two_z_dot_unit[:], in0=z_dot_u[:], scalar=2.0, in1=u_unit[:], op0=ALU.mult, op1=ALU.mult
+        vec.tensor_reduce(out=z_sq[:], in_=z_sq_parts[:], axis=AX.X, op=ALU.add)
+        vec.tensor_reduce(out=z_dot_b[:], in_=z_dot_b_parts[:], axis=AX.X, op=ALU.add)
+        for r in blocks:
+            vec.tensor_scalar(
+                out=col(v0_norm, r), in0=col(num_norm, r), scalar1=col(rden, r), scalar2=MAX_NORM,
+                op0=ALU.mult, op1=ALU.min,
+            )
+        vec.tensor_scalar(
+            out=one_minus_z2[:], in0=z_sq[:], scalar1=-1.0, scalar2=1.0, op0=ALU.mult, op1=ALU.add
         )
-        nc.vector.scalar_tensor_tensor(
+        vec.tensor_reduce(out=mv_dot_z[:], in_=mv_dot_z_parts[:], axis=AX.X, op=ALU.add)
+        vec.reciprocal(out=num_rnorm[:], in_=num_norm[:])
+        vec.tensor_mul(out=z_dot_u_b[:], in0=rho[:], in1=z_dot_b[:])
+        vec.tensor_scalar_max(out=z_gap[:], in0=one_minus_z2[:], scalar1=EPS)
+        vec.tensor_scalar_add(out=z2_minus_1[:], in0=z_sq[:], scalar1=-1.0)
+        vec.tensor_mul(out=u_unit[:], in0=mv_coef[:], in1=num_rnorm[:])
+        vec.tensor_add(out=z_dot_u[:], in0=z_dot_u_b[:], in1=mv_dot_z[:])
+        vec.reciprocal(out=half_lambda[:], in_=z_gap[:])
+        vec.scalar_tensor_tensor(
             out=unit_gain[:], in0=u_unit[:], scalar=ROOT_SLOPE, in1=one_minus_z2[:], op0=ALU.mult, op1=ALU.mult
         )
+        vec.scalar_tensor_tensor(
+            out=two_z_dot_unit[:], in0=z_dot_u[:], scalar=2.0, in1=u_unit[:], op0=ALU.mult, op1=ALU.mult
+        )
+        vec.tensor_mul(out=v0_lambda[:], in0=v0_norm[:], in1=half_lambda[:])
+        for r in blocks:
+            nc.scalar.activation(out=vt_tanh[:, r, :], in_=tau[:], func=ACT.Tanh, scale=col(v0_lambda, r))
+        make_u(0, 0)
 
         two_zs = per_horizon("two_zs")
         s2 = per_horizon("s2")
@@ -495,7 +497,8 @@ def tile_paralleldirectpoincaredynamics_kernel(
         rden2 = per_horizon("rden2")
         out_sq = per_horizon("out_sq")
         newton = per_horizon("newton")
-        o_factor = per_horizon("o_factor")
+        z_part = per_horizon("z_part")
+        u_part = per_horizon("u_part")
         a_fin = per_horizon("a_fin")
         c_fin = per_horizon("c_fin")
 
@@ -503,33 +506,36 @@ def tile_paralleldirectpoincaredynamics_kernel(
             return scalars[:].unsqueeze(2).to_broadcast([P, ROW_BLOCKS, T])
 
         for r in blocks:
-            nc.vector.scalar_tensor_tensor(
+            vec.scalar_tensor_tensor(
                 out=z2_s2[:, r, :], in0=vt_tanh[:, r, :], scalar=col(z_sq, r), in1=vt_tanh[:, r, :],
                 op0=ALU.mult, op1=ALU.mult,
             )
-        nc.vector.tensor_mul(out=two_zs[:], in0=vt_tanh[:], in1=each_horizon(two_z_dot_unit))
-        nc.vector.tensor_mul(out=s2[:], in0=vt_tanh[:], in1=vt_tanh[:])
-        nc.vector.tensor_mul(out=u_coef_scaled[:], in0=vt_tanh[:], in1=each_horizon(unit_gain))
-        nc.vector.scalar_tensor_tensor(
+        vec.tensor_mul(out=s2[:], in0=vt_tanh[:], in1=vt_tanh[:])
+        vec.tensor_mul(out=two_zs[:], in0=vt_tanh[:], in1=each_horizon(two_z_dot_unit))
+        vec.tensor_mul(out=u_coef_scaled[:], in0=vt_tanh[:], in1=each_horizon(unit_gain))
+        vec.scalar_tensor_tensor(
             out=den2_raw[:], in0=two_zs[:], scalar=1.0, in1=z2_s2[:], op0=ALU.add, op1=ALU.add
         )
-        nc.vector.scalar_tensor_tensor(
+        vec.scalar_tensor_tensor(
             out=z_coef[:], in0=two_zs[:], scalar=1.0, in1=s2[:], op0=ALU.add, op1=ALU.add
         )
-        nc.vector.tensor_scalar_max(out=den2[:], in0=den2_raw[:], scalar1=EPS)
-        nc.vector.tensor_add(out=sum2_sq[:], in0=z_coef[:], in1=each_horizon(z2_minus_1))
-        nc.vector.reciprocal(out=rden2[:], in_=den2[:])
-        nc.vector.tensor_scalar_mul(out=z_coef_scaled[:], in0=z_coef[:], scalar1=ROOT_SLOPE)
-        nc.vector.tensor_mul(out=out_sq[:], in0=sum2_sq[:], in1=rden2[:])
-        nc.vector.tensor_scalar(
+        make_u(0, 1)
+        vec.tensor_scalar_max(out=den2[:], in0=den2_raw[:], scalar1=EPS)
+        vec.tensor_add(out=sum2_sq[:], in0=z_coef[:], in1=each_horizon(z2_minus_1))
+        vec.reciprocal(out=rden2[:], in_=den2[:])
+        vec.tensor_scalar_mul(out=z_coef_scaled[:], in0=z_coef[:], scalar1=ROOT_SLOPE)
+        make_u(0, 2)
+        vec.tensor_mul(out=out_sq[:], in0=sum2_sq[:], in1=rden2[:])
+        vec.tensor_mul(out=z_part[:], in0=z_coef_scaled[:], in1=rden2[:])
+        vec.tensor_mul(out=u_part[:], in0=u_coef_scaled[:], in1=rden2[:])
+        vec.tensor_scalar(
             out=newton[:], in0=out_sq[:], scalar1=MAX_SQ, scalar2=-3.0 * MAX_SQ, op0=ALU.max, op1=ALU.add
         )
-        fill("vector", 1)
-        nc.vector.tensor_mul(out=o_factor[:], in0=newton[:], in1=rden2[:])
-        nc.vector.tensor_mul(out=a_fin[:], in0=z_coef_scaled[:], in1=o_factor[:])
-        nc.vector.tensor_mul(out=c_fin[:], in0=u_coef_scaled[:], in1=o_factor[:])
+        vec.tensor_mul(out=a_fin[:], in0=z_part[:], in1=newton[:])
+        vec.tensor_mul(out=c_fin[:], in0=u_part[:], in1=newton[:])
+        make_u(0, last)
 
-        def emit(r, t, stores, fill_between):
+        def emit(r, t, stores):
             res = stream.tile([P, N], F32, name="res")
             width = N // stores
             for i in range(stores):
@@ -538,7 +544,6 @@ def tile_paralleldirectpoincaredynamics_kernel(
                     out=res[:, cols], in_=z_sb[:, r, cols], func=ACT.Copy, scale=a_fin[:, r, t : t + 1]
                 )
             for j in range(N_TILES):
-                fill_up_to("vector", vector_sums + r * N_TILES + j + 1)
                 nc.vector.scalar_tensor_tensor(
                     out=res[:, tile_cols(j)], in0=u_ps[r][j][:], scalar=c_fin[:, r, t : t + 1],
                     in1=res[:, tile_cols(j)], op0=ALU.mult, op1=ALU.add,
@@ -546,7 +551,6 @@ def tile_paralleldirectpoincaredynamics_kernel(
                 if (j + 1) % (N_TILES // stores) == 0:
                     cols = slice((j + 1) * N_TILE - width, (j + 1) * N_TILE)
                     nc.sync.dma_start(out=out[r * P : (r + 1) * P, t, cols], in_=res[:, cols])
-            fill("vector", fill_between)
 
         def compute_on_gpsimd(r, t):
             z_part = own.tile([P, N], F32, name="z_part")
@@ -568,9 +572,10 @@ def tile_paralleldirectpoincaredynamics_kernel(
         for k in range(len(for_vector)):
             r, t = for_vector[k]
             if k % ratio == 0 and k // ratio < len(for_gpsimd):
-                fill_up_to("vector", vector_sums + (for_gpsimd[k // ratio][0] + 1) * N_TILES)
                 theirs = compute_on_gpsimd(*for_gpsimd[k // ratio])
-            emit(r, t, N_TILES if k == 0 else 2 if k < ratio else 1, 1 if k > 0 else 0)
+            emit(r, t, N_TILES if k == 0 else 2 if k < ratio else 1)
+            for j in {2: (0,), 3: (1,), 4: (2,), 5: (3,)}.get(k, ()):
+                make_u(1, j)
             if k % ratio == ratio - 1:
                 rg, tg = for_gpsimd[k // ratio]
                 nc.sync.dma_start(out=out[rg * P : (rg + 1) * P, tg, :], in_=theirs[:])

@@ -115,10 +115,10 @@ def tile_paralleldirectpoincaredynamics_kernel(
                 in_=w_bytes[:, g0 : g0 + count, j * N_TILE * PACK : (j + 1) * N_TILE * PACK].bitcast(I32),
             )
 
-        load_scales()
+        load_v(0)
         nc.sync.dma_start(out=b_rows[0:B_ROWS, :], in_=b.rearrange("(p c) -> p c", p=B_ROWS))
         nc.sync.dma_start(out=step_raw[0:1, :], in_=step_sizes.rearrange("(o n) -> o n", o=1))
-        load_v(0)
+        load_scales()
         load_z(0)
         load_v(1)
         load_w(0)
@@ -130,11 +130,11 @@ def tile_paralleldirectpoincaredynamics_kernel(
 
         squares = keep.tile([P, 2 * N], BF16)
         products = keep.tile([P, 2 * N], F32)
-        turns = {"scalar": 0, "vector": 0}
+        ends = {"scalar": 0, "vector": 0}
 
         def scrap(engine, width):
-            turns[engine] = (turns[engine] + 1) % (2 * N // width)
-            at = turns[engine] * width
+            at = ends[engine] if ends[engine] + width <= 2 * N else 0
+            ends[engine] = at + width
             return {"scalar": squares, "vector": products}[engine][:, at : at + width]
 
         b_bc = keep.tile([P, N], BF16)
@@ -544,6 +544,8 @@ def tile_paralleldirectpoincaredynamics_kernel(
                     out=res[:, cols], in_=z_sb[:, r, cols], func=ACT.Copy, scale=a_fin[:, r, t : t + 1]
                 )
             for j in range(N_TILES):
+                if stores == N_TILES and j == last:
+                    make_u(1, 0)
                 nc.vector.scalar_tensor_tensor(
                     out=res[:, tile_cols(j)], in0=u_ps[r][j][:], scalar=c_fin[:, r, t : t + 1],
                     in1=res[:, tile_cols(j)], op0=ALU.mult, op1=ALU.add,
@@ -552,30 +554,35 @@ def tile_paralleldirectpoincaredynamics_kernel(
                     cols = slice((j + 1) * N_TILE - width, (j + 1) * N_TILE)
                     nc.sync.dma_start(out=out[r * P : (r + 1) * P, t, cols], in_=res[:, cols])
 
-        def compute_on_gpsimd(r, t):
+        def compute_on_gpsimd(r, t, pieces):
             z_part = own.tile([P, N], F32, name="z_part")
             u_part = own.tile([P, N], F32, name="u_part")
-            nc.gpsimd.tensor_scalar(
-                out=z_part[:], in0=z_sb[:, r, :], scalar1=a_fin[:, r, t : t + 1], scalar2=0.0,
-                op0=ALU.mult, op1=ALU.add,
-            )
-            nc.gpsimd.tensor_scalar(
-                out=u_part[:], in0=u_sb[:, r, :], scalar1=c_fin[:, r, t : t + 1], scalar2=0.0,
-                op0=ALU.mult, op1=ALU.add,
-            )
-            nc.gpsimd.tensor_add(out=z_part[:], in0=z_part[:], in1=u_part[:])
+            width = N // pieces
+            for i in range(pieces):
+                cols = slice(i * width, (i + 1) * width)
+                nc.gpsimd.tensor_scalar(
+                    out=z_part[:, cols], in0=z_sb[:, r, cols], scalar1=a_fin[:, r, t : t + 1], scalar2=0.0,
+                    op0=ALU.mult, op1=ALU.add,
+                )
+                nc.gpsimd.tensor_scalar(
+                    out=u_part[:, cols], in0=u_sb[:, r, cols], scalar1=c_fin[:, r, t : t + 1], scalar2=0.0,
+                    op0=ALU.mult, op1=ALU.add,
+                )
+                nc.gpsimd.tensor_add(out=z_part[:, cols], in0=z_part[:, cols], in1=u_part[:, cols])
             return z_part
 
         for_gpsimd = [(0, T - 2), (0, T - 1), (1, T - 1)]
         for_vector = [(r, t) for r in blocks for t in range(T) if (r, t) not in for_gpsimd]
         ratio = 4
+        theirs = {}
         for k in range(len(for_vector)):
             r, t = for_vector[k]
             if k % ratio == 0 and k // ratio < len(for_gpsimd):
-                theirs = compute_on_gpsimd(*for_gpsimd[k // ratio])
-            emit(r, t, N_TILES if k == 0 else 2 if k < ratio else 1)
-            for j in {2: (0,), 3: (1,), 4: (2,), 5: (3,)}.get(k, ()):
+                g = k // ratio
+                theirs[g] = compute_on_gpsimd(*for_gpsimd[g], 2 if g == 0 else 1)
+            emit(r, t, N_TILES if k == 0 else 2 if k < 4 else 1)
+            for j in {1: (1,), 2: (2,), 3: (3,)}.get(k, ()):
                 make_u(1, j)
-            if k % ratio == ratio - 1:
-                rg, tg = for_gpsimd[k // ratio]
-                nc.sync.dma_start(out=out[rg * P : (rg + 1) * P, tg, :], in_=theirs[:])
+            for g, cols in {1: ((0, half_cols(0)),), 2: ((0, half_cols(1)),), 6: ((1, slice(0, N)),), 10: ((2, slice(0, N)),)}.get(k, ()):
+                rg, tg = for_gpsimd[g]
+                nc.sync.dma_start(out=out[rg * P : (rg + 1) * P, tg, cols], in_=theirs[g][:, cols])

@@ -24,7 +24,7 @@ N_TILES = N // N_TILE
 HALF = N // 2
 B_ROWS = 8
 B_WORDS = N // 2 // B_ROWS
-W_LOADS = ((0, 0, 4), (1, 0, 4), (2, 0, 4), (3, 0, 2), (3, 2, 2))
+W_LOADS = ((0, 0, 4), (1, 0, 4), (2, 0, 2), (2, 2, 2), (3, 0, 2), (3, 2, 2))
 
 EPS = 1e-7
 EPS_SQ = 1e-14
@@ -115,10 +115,10 @@ def tile_paralleldirectpoincaredynamics_kernel(
                 in_=w_bytes[:, g0 : g0 + count, j * N_TILE * PACK : (j + 1) * N_TILE * PACK].bitcast(I32),
             )
 
-        load_v(0)
+        load_scales()
         nc.sync.dma_start(out=b_rows[0:B_ROWS, :], in_=b.rearrange("(p c) -> p c", p=B_ROWS))
         nc.sync.dma_start(out=step_raw[0:1, :], in_=step_sizes.rearrange("(o n) -> o n", o=1))
-        load_scales()
+        load_v(0)
         load_z(0)
         load_v(1)
         load_w(0)
@@ -127,6 +127,7 @@ def tile_paralleldirectpoincaredynamics_kernel(
         load_w(2)
         load_w(3)
         load_w(4)
+        load_w(5)
 
         squares = keep.tile([P, 2 * N], BF16)
         products = keep.tile([P, 2 * N], F32)
@@ -139,6 +140,7 @@ def tile_paralleldirectpoincaredynamics_kernel(
 
         b_bc = keep.tile([P, N], BF16)
         v_sq_parts = small.tile([P, ROW_BLOCKS, 2], F32)
+        nc.vector.memset(v_sq_parts[:], 0.0)
         z_sq_parts = small.tile([P, ROW_BLOCKS, N_TILES], F32)
         z_dot_b_parts = small.tile([P, ROW_BLOCKS, 2], F32)
         grouped = keep.tile([P, ROW_BLOCKS, PASSES * P * PACK], BF16, align_bytes=64)
@@ -252,9 +254,8 @@ def tile_paralleldirectpoincaredynamics_kernel(
         for r in blocks:
             for h in range(2):
                 defer("vector", dot_z_b, r, h)
-        for r in blocks:
-            for h in range(2):
-                defer("scalar", square_v, r, h)
+        for h in range(2):
+            defer("scalar", square_v, 1, h)
         scalar_v_sums = len(lines["scalar"])
         for r in blocks:
             for j in range(N_TILES):
@@ -267,6 +268,16 @@ def tile_paralleldirectpoincaredynamics_kernel(
         nc.tensor.transpose(b_turned_ps[:], b_rows[:].bitcast(F32), ident[:])
         b_turned = keep.tile([P, B_ROWS], F32)
         nc.vector.tensor_copy(out=b_turned[:], in_=b_turned_ps[:, 0:B_ROWS])
+        nc.scalar.activation(
+            out=scrap("scalar", 2 * B_WORDS)[0:B_ROWS, :], in_=b_rows[0:B_ROWS, :], func=ACT.Square,
+            accum_out=b_sq_part[0:B_ROWS, 0:1],
+        )
+        nc.scalar.copy(out=b_sq_part[0:1, 1:2], in_=step_raw[0:1, :])
+        b_sq_ps = bank(1, [P, ROW_BLOCKS], F32, "b_sq_ps")
+        nc.tensor.matmul(out=b_sq_ps[:], lhsT=ones_f32[:], rhs=b_sq_part[:], start=True, stop=True)
+        b_sq_and_step = per_row("b_sq_and_step")
+        b_sq = b_sq_and_step[:, 0:1]
+        nc.vector.tensor_copy(out=b_sq_and_step[:], in_=b_sq_ps[:])
         for h in range(2):
             spread = bank(6 + h, [P, N_TILE], F32, "spread")
             for i in range(B_ROWS // 2):
@@ -274,24 +285,23 @@ def tile_paralleldirectpoincaredynamics_kernel(
                 nc.tensor.transpose(
                     spread[:, i * P : (i + 1) * P], b_turned[:, m : m + 1].to_broadcast([P, P]), ident[:]
                 )
-            nc.vector.tensor_copy(out=b_bc[:, half_cols(h)].bitcast(F32), in_=spread[:])
-        nc.scalar.activation(
-            out=scrap("scalar", 2 * B_WORDS)[0:B_ROWS, :], in_=b_rows[0:B_ROWS, :], func=ACT.Square,
-            accum_out=b_sq_part[0:B_ROWS, 0:1],
-        )
-        nc.scalar.copy(out=b_sq_part[0:1, 1:2], in_=step_raw[0:1, :])
-        fill("scalar", 1)
+            nc.scalar.copy(out=b_bc[:, half_cols(h)].bitcast(F32), in_=spread[:])
         turn_v(0)
         turn_v(1)
-        b_sq_ps = bank(1, [P, ROW_BLOCKS], F32, "b_sq_ps")
-        nc.tensor.matmul(out=b_sq_ps[:], lhsT=ones_f32[:], rhs=b_sq_part[:], start=True, stop=True)
-        b_sq_and_step = per_row("b_sq_and_step")
-        b_sq = b_sq_and_step[:, 0:1]
-        fill("vector", 1)
+        gram = bank(6, [P, P], F32, "gram")
+        steps = [(g, t) for g in range(PASSES) for t in range(PACK)]
+        for g, t in steps:
+            k_rows = grouped[:, 0, g * P * PACK + t : (g + 1) * P * PACK : PACK]
+            nc.tensor.matmul(
+                out=gram[:], lhsT=k_rows, rhs=k_rows, start=((g, t) == steps[0]), stop=((g, t) == steps[-1])
+            )
+        fill("vector", 2)
         quantise_v(0)
-        fill("vector", 1)
         quantise_v(1)
-        nc.vector.tensor_copy(out=b_sq_and_step[:], in_=b_sq_ps[:])
+        nc.vector.scalar_tensor_tensor(
+            out=scrap("vector", P), in0=gram[:], scalar=1.0, in1=ident[:], op0=ALU.mult, op1=ALU.mult,
+            accum_out=v_sq_parts[:, 0, 0:1],
+        )
         fill("vector", 2)
         fill_up_to("scalar", scalar_v_sums)
         for i in range(len(W_LOADS)):
@@ -335,6 +345,7 @@ def tile_paralleldirectpoincaredynamics_kernel(
 
         square_mv(0, 0)
         dots(0, 0)
+        fill("scalar", 1)
         square_mv(0, 1)
         dots(0, 1)
         fill("scalar", 1)

from contextlib import ExitStack

import concourse.mybir as mybir
from concourse.masks import make_identity

F32 = mybir.dt.float32
BF16 = mybir.dt.bfloat16
I32 = mybir.dt.int32
U32 = mybir.dt.uint32
U8 = mybir.dt.uint8
FP8X4 = mybir.dt.float8_e4m3fn_x4
ALU = mybir.AluOpType
ACT = mybir.ActivationFunctionType
AX = mybir.AxisListType

P = 128
B, K, N, T = 256, 2048, 2048, 8
ROW_BLOCKS = B // P
PACK = 4
K_PASS = P * PACK
PASSES = K // K_PASS
N_TILE = 512
N_TILES = N // N_TILE
HALF = N // 2
B_ROWS = 8
B_WORDS = N // 2 // B_ROWS
W_LOADS = ((0, 0, 4), (1, 0, 4), (2, 0, 2), (2, 2, 2), (3, 0, 2), (3, 2, 2))

EPS = 1e-7
EPS_SQ = 1e-14
TINY = 1e-24
MAX_NORM = 1.0 - 1e-5
MAX_SQ = MAX_NORM * MAX_NORM
ROOT_SLOPE = -0.5 / MAX_SQ

FLOPS = 2 * B * K * N


def tile_paralleldirectpoincaredynamics_kernel(
    tc, z_0, v_init, W_words, W_scales, b, step_sizes, out
):
    nc = tc.nc
    with ExitStack() as ctx:
        keep = ctx.enter_context(tc.tile_pool(name="keep", bufs=1))
        small = ctx.enter_context(tc.tile_pool(name="small", bufs=1))
        stream = ctx.enter_context(tc.tile_pool(name="stream", bufs=6))
        own = ctx.enter_context(tc.tile_pool(name="own", bufs=2))
        psum = ctx.enter_context(tc.psum_pool(name="psum", bufs=1))
        ctx.enter_context(tc.manual_schedule())

        def per_row(name, width=ROW_BLOCKS):
            return small.tile([P, width], F32, name=name)

        def per_horizon(name):
            return small.tile([P, ROW_BLOCKS, T], F32, name=name)

        def col(scalars, r):
            return scalars[:, r : r + 1]

        def bank(index, shape, dtype, name):
            return psum.tile(shape, dtype, tag="bank%d" % index, name=name)

        def tile_cols(j):
            return slice(j * N_TILE, (j + 1) * N_TILE)

        def half_cols(h):
            return slice(h * HALF, (h + 1) * HALF)

        blocks = range(ROW_BLOCKS)
        last = N_TILES - 1

        w_planes = keep.tile([P, N], U8, align_bytes=64)
        b_rows = keep.tile([P, 2 * B_WORDS], BF16)
        ones_f32 = keep.tile([P, P], F32)
        one_col = per_row("one_col", 1)
        plus_half = per_row("plus_half")
        minus_half = per_row("minus_half")
        horizon = per_row("horizon", T)
        b_sq_part = per_row("b_sq_part")
        ident = keep.tile([P, P], F32)
        nc.gpsimd.memset(w_planes[:].bitcast(F32), 0.0)
        nc.vector.memset(b_rows[:].bitcast(I32), 0)
        nc.vector.memset(ones_f32[:], 1.0)
        nc.gpsimd.memset(one_col[:], 1.0)
        make_identity(nc, ident[:])
        nc.gpsimd.memset(b_sq_part[:], 0.0)
        nc.gpsimd.memset(plus_half[:], 0.5)
        nc.gpsimd.memset(minus_half[:], -0.5)
        for t in range(T):
            nc.gpsimd.memset(horizon[:, t : t + 1], float(t + 1))

        step_raw = small.tile([P, 1], BF16)
        v_sb = keep.tile([P, ROW_BLOCKS, K], BF16)
        z_sb = keep.tile([P, ROW_BLOCKS, N], BF16)
        w_words = keep.tile([P, PASSES, N], I32, align_bytes=64)
        w_bytes = W_words.rearrange("g p n t -> p g (n t)")

        def load_v(r):
            nc.sync.dma_start(out=v_sb[:, r, :], in_=v_init[r * P : (r + 1) * P, :])

        def load_z(r):
            nc.sync.dma_start(out=z_sb[:, r, :], in_=z_0[r * P : (r + 1) * P, :])

        def load_scales():
            for quad in range(4):
                nc.sync.dma_start(
                    out=w_planes[32 * quad : 32 * quad + 16, :].bitcast(I32),
                    in_=W_scales[:, 4 * quad : 4 * quad + 4, :].bitcast(I32),
                )

        def load_w(i):
            j, g0, count = W_LOADS[i]
            nc.sync.dma_start(
                out=w_words[:, g0 : g0 + count, tile_cols(j)],
                in_=w_bytes[:, g0 : g0 + count, j * N_TILE * PACK : (j + 1) * N_TILE * PACK].bitcast(I32),
            )

        load_scales()
        nc.sync.dma_start(out=b_rows[0:B_ROWS, :], in_=b.rearrange("(p c) -> p c", p=B_ROWS))
        nc.sync.dma_start(out=step_raw[0:1, :], in_=step_sizes.rearrange("(o n) -> o n", o=1))
        load_v(0)
        load_z(0)
        load_v(1)
        load_w(0)
        load_z(1)
        load_w(1)
        load_w(2)
        load_w(3)
        load_w(4)
        load_w(5)

        squares = keep.tile([P, 2 * N], BF16)
        products = keep.tile([P, 2 * N], F32)
        ends = {"scalar": 0, "vector": 0}

        def scrap(engine, width):
            at = ends[engine] if ends[engine] + width <= 2 * N else 0
            ends[engine] = at + width
            return {"scalar": squares, "vector": products}[engine][:, at : at + width]

        b_bc = keep.tile([P, N], BF16)
        v_sq_parts = small.tile([P, ROW_BLOCKS, 2], F32)
        nc.vector.memset(v_sq_parts[:], 0.0)
        z_sq_parts = small.tile([P, ROW_BLOCKS, N_TILES], F32)
        z_dot_b_parts = small.tile([P, ROW_BLOCKS, 2], F32)
        grouped = keep.tile([P, ROW_BLOCKS, PASSES * P * PACK], BF16, align_bytes=64)
        v_codes = keep.tile([P, ROW_BLOCKS, PASSES * P], U32, align_bytes=64)
        v_planes = keep.tile([P, ROW_BLOCKS, PASSES * P], U8, align_bytes=64)
        mv = [[None] * N_TILES for r in blocks]
        u_ps = [[None] * N_TILES for r in blocks]
        mv_sq_parts = small.tile([P, ROW_BLOCKS, N_TILES], F32)
        mv_dot_b_parts = small.tile([P, ROW_BLOCKS, N_TILES], F32)
        mv_dot_z_parts = small.tile([P, ROW_BLOCKS, N_TILES], F32)
        u_sb = keep.tile([P, ROW_BLOCKS, N], F32)
        rho = per_row("rho")

        def square_v(r, h):
            nc.scalar.activation(
                out=scrap("scalar", HALF), in_=v_sb[:, r, half_cols(h)], func=ACT.Square,
                accum_out=v_sq_parts[:, r, h : h + 1],
            )

        def square_z(r, j):
            nc.scalar.activation(
                out=scrap("scalar", N_TILE), in_=z_sb[:, r, tile_cols(j)], func=ACT.Square,
                accum_out=z_sq_parts[:, r, j : j + 1],
            )

        def dot_z_b(r, h):
            nc.vector.scalar_tensor_tensor(
                out=scrap("vector", HALF), in0=z_sb[:, r, half_cols(h)], scalar=1.0, in1=b_bc[:, half_cols(h)],
                op0=ALU.mult, op1=ALU.mult, accum_out=z_dot_b_parts[:, r, h : h + 1],
            )

        def turn_v(r):
            v_pairs = v_sb[:, r, :].bitcast(F32)
            for h in range(2):
                turned = bank(2 + 2 * r + h, [P, 2, 2, P], F32, "turned")
                for i in range(2):
                    g = 2 * h + i
                    for u in range(2):
                        nc.tensor.transpose(
                            turned[:, i, u, :], v_pairs[:, 256 * g + u : 256 * (g + 1) : 2], ident[:]
                        )
                side_by_side = (
                    grouped[:, r, h * 1024 : (h + 1) * 1024]
                    .bitcast(F32)
                    .rearrange("p (i b u) -> p i b u", i=2, u=2)
                )
                nc.scalar.copy(out=side_by_side, in_=turned[:].rearrange("p i u b -> p i b u"))

        def quantise_v(r):
            nc.vector.quantize_mx(
                out=v_codes[:, r, :].bitcast(FP8X4), scales=v_planes[:, r, :], in_=grouped[:, r, :]
            )

        def multiply(i, r):
            j, g0, count = W_LOADS[i]
            if mv[r][j] is None:
                mv[r][j] = bank(ROW_BLOCKS * j + r, [P, N_TILE], F32, "mv_%d_%d" % (r, j))
            for g in range(g0, g0 + count):
                rows = slice(g * P, (g + 1) * P)
                nc.tensor.matmul_mx(
                    out=mv[r][j][:],
                    lhsT=v_codes[:, r, rows].bitcast(FP8X4),
                    lhsT_scale=v_planes[:, r, rows],
                    rhs=w_words[:, g, tile_cols(j)].bitcast(FP8X4),
                    rhs_scale=w_planes[4 * g : P, tile_cols(j)],
                    start=(g == 0),
                    stop=(g == PASSES - 1),
                )

        def square_mv(j, r):
            nc.scalar.activation(
                out=scrap("scalar", N_TILE), in_=mv[r][j][:], func=ACT.Square,
                accum_out=mv_sq_parts[:, r, j : j + 1],
            )

        def dot_mv(j, r, other, parts):
            nc.vector.scalar_tensor_tensor(
                out=scrap("vector", N_TILE), in0=mv[r][j][:], scalar=1.0, in1=other,
                op0=ALU.mult, op1=ALU.mult, accum_out=parts[:, r, j : j + 1],
            )

        def dot_mv_b(j, r):
            dot_mv(j, r, b_bc[:, tile_cols(j)], mv_dot_b_parts)

        def dot_mv_z(j, r):
            dot_mv(j, r, z_sb[:, r, tile_cols(j)], mv_dot_z_parts)

        def make_u(r, j):
            nc.vector.scalar_tensor_tensor(
                out=u_sb[:, r, tile_cols(j)], in0=b_bc[:, tile_cols(j)], scalar=col(rho, r),
                in1=mv[r][j][:], op0=ALU.mult, op1=ALU.add,
            )
            u_ps[r][j] = bank(ROW_BLOCKS * j + r, [P, N_TILE], F32, "u_%d_%d" % (r, j))
            nc.tensor.matmul(out=u_ps[r][j][:], lhsT=ident[:], rhs=u_sb[:, r, tile_cols(j)], start=True, stop=True)

        lines = {"vector": [], "scalar": []}
        issued = {"vector": 0, "scalar": 0}

        def defer(engine, action, *args):
            lines[engine].append(lambda: action(*args))

        def fill(engine, n):
            for i in range(n):
                if issued[engine] < len(lines[engine]):
                    lines[engine][issued[engine]]()
                    issued[engine] += 1

        def fill_up_to(engine, count):
            fill(engine, max(0, count - issued[engine]))

        for r in blocks:
            for h in range(2):
                defer("vector", dot_z_b, r, h)
        for h in range(2):
            defer("scalar", square_v, 1, h)
        scalar_v_sums = len(lines["scalar"])
        for r in blocks:
            for j in range(N_TILES):
                defer("scalar", square_z, r, j)
        scalar_sums = len(lines["scalar"])

        warm = per_row("warm", 1)
        nc.scalar.activation(out=warm[:], in_=one_col[:], func=ACT.Ln)
        b_turned_ps = bank(0, [P, P], F32, "b_turned_ps")
        nc.tensor.transpose(b_turned_ps[:], b_rows[:].bitcast(F32), ident[:])
        b_turned = keep.tile([P, B_ROWS], F32)
        nc.vector.tensor_copy(out=b_turned[:], in_=b_turned_ps[:, 0:B_ROWS])
        nc.scalar.activation(
            out=scrap("scalar", 2 * B_WORDS)[0:B_ROWS, :], in_=b_rows[0:B_ROWS, :], func=ACT.Square,
            accum_out=b_sq_part[0:B_ROWS, 0:1],
        )
        nc.scalar.copy(out=b_sq_part[0:1, 1:2], in_=step_raw[0:1, :])
        b_sq_ps = bank(1, [P, ROW_BLOCKS], F32, "b_sq_ps")
        nc.tensor.matmul(out=b_sq_ps[:], lhsT=ones_f32[:], rhs=b_sq_part[:], start=True, stop=True)
        b_sq_and_step = per_row("b_sq_and_step")
        b_sq = b_sq_and_step[:, 0:1]
        nc.vector.tensor_copy(out=b_sq_and_step[:], in_=b_sq_ps[:])
        for h in range(2):
            spread = bank(6 + h, [P, N_TILE], F32, "spread")
            for i in range(B_ROWS // 2):
                m = h * B_ROWS // 2 + i
                nc.tensor.transpose(
                    spread[:, i * P : (i + 1) * P], b_turned[:, m : m + 1].to_broadcast([P, P]), ident[:]
                )
            nc.scalar.copy(out=b_bc[:, half_cols(h)].bitcast(F32), in_=spread[:])
        turn_v(0)
        turn_v(1)
        gram = bank(6, [P, P], F32, "gram")
        steps = [(g, t) for g in range(PASSES) for t in range(PACK)]
        for g, t in steps:
            k_rows = grouped[:, 0, g * P * PACK + t : (g + 1) * P * PACK : PACK]
            nc.tensor.matmul(
                out=gram[:], lhsT=k_rows, rhs=k_rows, start=((g, t) == steps[0]), stop=((g, t) == steps[-1])
            )
        fill("vector", 2)
        quantise_v(0)
        quantise_v(1)
        nc.vector.scalar_tensor_tensor(
            out=scrap("vector", P), in0=gram[:], scalar=1.0, in1=ident[:], op0=ALU.mult, op1=ALU.mult,
            accum_out=v_sq_parts[:, 0, 0:1],
        )
        fill("vector", 2)
        fill_up_to("scalar", scalar_v_sums)
        for i in range(len(W_LOADS)):
            for r in blocks:
                multiply(i, r)

        b_sq_c = per_row("b_sq_c", 1)
        b_norm = per_row("b_norm", 1)
        b_tanh = per_row("b_tanh", 1)
        b_rnorm = per_row("b_rnorm", 1)
        beta = per_row("beta", 1)
        minus_beta = per_row("minus_beta", 1)
        two_beta = per_row("two_beta", 1)
        y2 = per_row("y2", 1)
        y2_minus_1 = per_row("y2_minus_1", 1)
        v_sq = per_row("v_sq")
        v_sq_c = per_row("v_sq_c")
        v_norm = per_row("v_norm")
        v_clip = per_row("v_clip")
        ln_plus = per_row("ln_plus")
        ln_minus = per_row("ln_minus")
        ln_diff = per_row("ln_diff")
        v_rnorm = per_row("v_rnorm")
        two_gain = per_row("two_gain")
        gain = per_row("gain")
        beta_sq = per_row("beta_sq", 1)
        step = per_row("step", 1)
        tau = per_row("tau", T)
        nc.gpsimd.tensor_scalar_max(out=b_sq_c[:], in0=b_sq, scalar1=EPS_SQ)
        nc.gpsimd.tensor_tensor(out=b_norm[:], in0=b_sq_c[:], in1=plus_half[:, 0:1], op=ALU.pow)
        nc.gpsimd.tensor_tensor(out=b_rnorm[:], in0=b_sq_c[:], in1=minus_half[:, 0:1], op=ALU.pow)
        nc.gpsimd.tensor_add(out=v_sq[:], in0=v_sq_parts[:, :, 0], in1=v_sq_parts[:, :, 1])
        nc.gpsimd.tensor_scalar_max(out=v_sq_c[:], in0=v_sq[:], scalar1=EPS_SQ)
        nc.gpsimd.tensor_tensor(out=v_norm[:], in0=v_sq_c[:], in1=plus_half[:], op=ALU.pow)
        nc.gpsimd.tensor_scalar_min(out=v_clip[:], in0=v_norm[:], scalar1=MAX_NORM)
        nc.gpsimd.tensor_tensor(out=v_rnorm[:], in0=v_sq_c[:], in1=minus_half[:], op=ALU.pow)

        def dots(j, r):
            dot_mv_b(j, r)
            dot_mv_z(j, r)

        square_mv(0, 0)
        dots(0, 0)
        fill("scalar", 1)
        square_mv(0, 1)
        dots(0, 1)
        fill("scalar", 1)
        square_mv(1, 0)
        dots(1, 0)
        nc.scalar.activation(out=ln_plus[:], in_=v_clip[:], func=ACT.Ln, bias=one_col[:], scale=1.0)
        nc.scalar.activation(out=ln_minus[:], in_=v_clip[:], func=ACT.Ln, bias=one_col[:], scale=-1.0)
        nc.scalar.activation(out=step[:], in_=b_sq_and_step[:, 1:2], func=ACT.Sigmoid)
        nc.scalar.activation(out=b_tanh[:], in_=b_norm[:], func=ACT.Tanh)
        nc.gpsimd.tensor_sub(out=ln_diff[:], in0=ln_plus[:], in1=ln_minus[:])
        nc.gpsimd.tensor_mul(out=two_gain[:], in0=ln_diff[:], in1=v_rnorm[:])
        nc.gpsimd.tensor_scalar_mul(out=gain[:], in0=two_gain[:], scalar1=0.5)
        nc.gpsimd.tensor_mul(out=beta[:], in0=b_tanh[:], in1=b_rnorm[:])
        nc.gpsimd.tensor_scalar_mul(out=two_beta[:], in0=beta[:], scalar1=2.0)
        nc.gpsimd.tensor_mul(out=beta_sq[:], in0=beta[:], in1=beta[:])
        nc.gpsimd.tensor_mul(out=y2[:], in0=beta_sq[:], in1=b_sq)
        nc.gpsimd.tensor_scalar_add(out=y2_minus_1[:], in0=y2[:], scalar1=-1.0)
        nc.gpsimd.tensor_scalar_mul(out=minus_beta[:], in0=beta[:], scalar1=-1.0)
        nc.gpsimd.tensor_scalar_mul(out=tau[:], in0=horizon[:], scalar1=step[:])
        dots(1, 1)
        square_mv(2, 0)
        square_mv(2, 1)
        square_mv(1, 1)
        dots(2, 0)
        dots(2, 1)
        mv_sq_pair = per_row("mv_sq_pair")
        mv_sq_head = per_row("mv_sq_head")
        mv_dot_b_head = per_row("mv_dot_b_head")
        head_2bpt = per_row("head_2bpt")
        nc.gpsimd.tensor_add(out=mv_sq_pair[:], in0=mv_sq_parts[:, :, 0], in1=mv_sq_parts[:, :, 1])
        nc.gpsimd.tensor_add(out=mv_sq_head[:], in0=mv_sq_pair[:], in1=mv_sq_parts[:, :, 2])
        nc.vector.tensor_reduce(out=mv_dot_b_head[:], in_=mv_dot_b_parts[:, :, 0:last], axis=AX.X, op=ALU.add)
        nc.vector.tensor_scalar_mul(out=head_2bpt[:], in0=mv_dot_b_head[:], scalar1=two_beta[:])
        for r in blocks:
            square_mv(last, r)
        dot_mv_b(last, 0)

        vec = nc.vector
        mv_sq_c = per_row("mv_sq_c")
        mv_rnorm = per_row("mv_rnorm")
        mv_sq_gain = per_row("mv_sq_gain")
        mv_dot_2bpt = per_row("mv_dot_2bpt")
        two_xy_unit = per_row("two_xy_unit")
        x_norm = per_row("x_norm")
        for r in blocks:
            nc.gpsimd.tensor_scalar(
                out=col(mv_sq_c, r), in0=mv_sq_parts[:, r, last : last + 1], scalar1=col(mv_sq_head, r),
                scalar2=EPS_SQ, op0=ALU.add, op1=ALU.max,
            )
        nc.gpsimd.tensor_tensor(out=mv_rnorm[:], in0=mv_sq_c[:], in1=minus_half[:], op=ALU.pow)
        vec.tensor_mul(out=mv_sq_gain[:], in0=mv_sq_c[:], in1=gain[:])
        dot_mv_b(last, 1)
        vec.scalar_tensor_tensor(
            out=mv_dot_2bpt[:], in0=mv_dot_b_parts[:, :, last], scalar=two_beta[:], in1=head_2bpt[:],
            op0=ALU.mult, op1=ALU.add,
        )
        fill("scalar", 3)
        for r in blocks:
            nc.scalar.activation(
                out=col(x_norm, r), in_=col(mv_rnorm, r), func=ACT.Tanh, scale=col(mv_sq_gain, r)
            )
        vec.tensor_mul(out=two_xy_unit[:], in0=mv_rnorm[:], in1=mv_dot_2bpt[:])
        fill_up_to("scalar", scalar_sums)
        one_plus_2xy = per_row("one_plus_2xy")
        x2 = per_row("x2")
        den_raw = per_row("den_raw")
        sum_sq = per_row("sum_sq")
        num_sq = per_row("num_sq")
        num_norm = per_row("num_norm")
        num_rnorm = per_row("num_rnorm")
        den = per_row("den")
        rden = per_row("rden")
        x_coef = per_row("x_coef")
        kappa = per_row("kappa")
        mv_coef = per_row("mv_coef")
        b_coef = per_row("b_coef")
        mv_rcoef = per_row("mv_rcoef")
        vec.tensor_mul(out=x2[:], in0=x_norm[:], in1=x_norm[:])
        for r in blocks:
            vec.tensor_scalar(
                out=col(one_plus_2xy, r), in0=col(x_norm, r), scalar1=col(two_xy_unit, r), scalar2=1.0,
                op0=ALU.mult, op1=ALU.add,
            )
        vec.tensor_mul(out=kappa[:], in0=x_norm[:], in1=mv_rnorm[:])
        vec.scalar_tensor_tensor(
            out=sum_sq[:], in0=x2[:], scalar=y2_minus_1[:], in1=one_plus_2xy[:], op0=ALU.add, op1=ALU.add
        )
        vec.scalar_tensor_tensor(
            out=den_raw[:], in0=x2[:], scalar=y2[:], in1=one_plus_2xy[:], op0=ALU.mult, op1=ALU.add
        )
        vec.tensor_scalar_add(out=x_coef[:], in0=one_plus_2xy[:], scalar1=y2[:])
        vec.tensor_scalar(
            out=b_coef[:], in0=x2[:], scalar1=minus_beta[:], scalar2=beta[:], op0=ALU.mult, op1=ALU.add
        )
        vec.scalar_tensor_tensor(
            out=num_sq[:], in0=sum_sq[:], scalar=TINY, in1=den_raw[:], op0=ALU.max, op1=ALU.mult
        )
        nc.gpsimd.tensor_tensor(out=num_norm[:], in0=num_sq[:], in1=plus_half[:], op=ALU.pow)
        vec.tensor_mul(out=mv_coef[:], in0=x_coef[:], in1=kappa[:])
        vec.tensor_scalar_max(out=den[:], in0=den_raw[:], scalar1=EPS)
        dot_mv_z(last, 0)
        vec.reciprocal(out=mv_rcoef[:], in_=mv_coef[:])
        vec.reciprocal(out=rden[:], in_=den[:])
        dot_mv_z(last, 1)
        vec.tensor_mul(out=rho[:], in0=b_coef[:], in1=mv_rcoef[:])

        z_sq = per_row("z_sq")
        one_minus_z2 = per_row("one_minus_z2")
        z2_minus_1 = per_row("z2_minus_1")
        z_gap = per_row("z_gap")
        half_lambda = per_row("half_lambda")
        v0_norm = per_row("v0_norm")
        v0_lambda = per_row("v0_lambda")
        vt_tanh = per_horizon("vt_tanh")
        z_dot_b = per_row("z_dot_b")
        mv_dot_z = per_row("mv_dot_z")
        z_dot_u_b = per_row("z_dot_u_b")
        z_dot_u = per_row("z_dot_u")
        u_unit = per_row("u_unit")
        two_z_dot_unit = per_row("two_z_dot_unit")
        unit_gain = per_row("unit_gain")
        vec.tensor_reduce(out=z_sq[:], in_=z_sq_parts[:], axis=AX.X, op=ALU.add)
        vec.tensor_reduce(out=z_dot_b[:], in_=z_dot_b_parts[:], axis=AX.X, op=ALU.add)
        for r in blocks:
            vec.tensor_scalar(
                out=col(v0_norm, r), in0=col(num_norm, r), scalar1=col(rden, r), scalar2=MAX_NORM,
                op0=ALU.mult, op1=ALU.min,
            )
        vec.tensor_scalar(
            out=one_minus_z2[:], in0=z_sq[:], scalar1=-1.0, scalar2=1.0, op0=ALU.mult, op1=ALU.add
        )
        vec.tensor_reduce(out=mv_dot_z[:], in_=mv_dot_z_parts[:], axis=AX.X, op=ALU.add)
        vec.reciprocal(out=num_rnorm[:], in_=num_norm[:])
        vec.tensor_mul(out=z_dot_u_b[:], in0=rho[:], in1=z_dot_b[:])
        vec.tensor_scalar_max(out=z_gap[:], in0=one_minus_z2[:], scalar1=EPS)
        vec.tensor_scalar_add(out=z2_minus_1[:], in0=z_sq[:], scalar1=-1.0)
        vec.tensor_mul(out=u_unit[:], in0=mv_coef[:], in1=num_rnorm[:])
        vec.tensor_add(out=z_dot_u[:], in0=z_dot_u_b[:], in1=mv_dot_z[:])
        vec.reciprocal(out=half_lambda[:], in_=z_gap[:])
        vec.scalar_tensor_tensor(
            out=unit_gain[:], in0=u_unit[:], scalar=ROOT_SLOPE, in1=one_minus_z2[:], op0=ALU.mult, op1=ALU.mult
        )
        vec.scalar_tensor_tensor(
            out=two_z_dot_unit[:], in0=z_dot_u[:], scalar=2.0, in1=u_unit[:], op0=ALU.mult, op1=ALU.mult
        )
        vec.tensor_mul(out=v0_lambda[:], in0=v0_norm[:], in1=half_lambda[:])
        for r in blocks:
            nc.scalar.activation(out=vt_tanh[:, r, :], in_=tau[:], func=ACT.Tanh, scale=col(v0_lambda, r))
        make_u(0, 0)

        two_zs = per_horizon("two_zs")
        s2 = per_horizon("s2")
        z2_s2 = per_horizon("z2_s2")
        z_coef = per_horizon("z_coef")
        z_coef_scaled = per_horizon("z_coef_scaled")
        u_coef_scaled = per_horizon("u_coef_scaled")
        den2_raw = per_horizon("den2_raw")
        sum2_sq = per_horizon("sum2_sq")
        den2 = per_horizon("den2")
        rden2 = per_horizon("rden2")
        out_sq = per_horizon("out_sq")
        newton = per_horizon("newton")
        z_part = per_horizon("z_part")
        u_part = per_horizon("u_part")
        a_fin = per_horizon("a_fin")
        c_fin = per_horizon("c_fin")

        def each_horizon(scalars):
            return scalars[:].unsqueeze(2).to_broadcast([P, ROW_BLOCKS, T])

        for r in blocks:
            vec.scalar_tensor_tensor(
                out=z2_s2[:, r, :], in0=vt_tanh[:, r, :], scalar=col(z_sq, r), in1=vt_tanh[:, r, :],
                op0=ALU.mult, op1=ALU.mult,
            )
        vec.tensor_mul(out=s2[:], in0=vt_tanh[:], in1=vt_tanh[:])
        vec.tensor_mul(out=two_zs[:], in0=vt_tanh[:], in1=each_horizon(two_z_dot_unit))
        vec.tensor_mul(out=u_coef_scaled[:], in0=vt_tanh[:], in1=each_horizon(unit_gain))
        vec.scalar_tensor_tensor(
            out=den2_raw[:], in0=two_zs[:], scalar=1.0, in1=z2_s2[:], op0=ALU.add, op1=ALU.add
        )
        vec.scalar_tensor_tensor(
            out=z_coef[:], in0=two_zs[:], scalar=1.0, in1=s2[:], op0=ALU.add, op1=ALU.add
        )
        make_u(0, 1)
        vec.tensor_scalar_max(out=den2[:], in0=den2_raw[:], scalar1=EPS)
        vec.tensor_add(out=sum2_sq[:], in0=z_coef[:], in1=each_horizon(z2_minus_1))
        vec.reciprocal(out=rden2[:], in_=den2[:])
        vec.tensor_scalar_mul(out=z_coef_scaled[:], in0=z_coef[:], scalar1=ROOT_SLOPE)
        make_u(0, 2)
        vec.tensor_mul(out=out_sq[:], in0=sum2_sq[:], in1=rden2[:])
        vec.tensor_mul(out=z_part[:], in0=z_coef_scaled[:], in1=rden2[:])
        vec.tensor_mul(out=u_part[:], in0=u_coef_scaled[:], in1=rden2[:])
        vec.tensor_scalar(
            out=newton[:], in0=out_sq[:], scalar1=MAX_SQ, scalar2=-3.0 * MAX_SQ, op0=ALU.max, op1=ALU.add
        )
        vec.tensor_mul(out=a_fin[:], in0=z_part[:], in1=newton[:])
        vec.tensor_mul(out=c_fin[:], in0=u_part[:], in1=newton[:])
        make_u(0, last)

        def emit(r, t, stores):
            res = stream.tile([P, N], F32, name="res")
            width = N // stores
            for i in range(stores):
                cols = slice(i * width, (i + 1) * width)
                nc.scalar.activation(
                    out=res[:, cols], in_=z_sb[:, r, cols], func=ACT.Copy, scale=a_fin[:, r, t : t + 1]
                )
            for j in range(N_TILES):
                if stores == N_TILES and j == last:
                    make_u(1, 0)
                nc.vector.scalar_tensor_tensor(
                    out=res[:, tile_cols(j)], in0=u_ps[r][j][:], scalar=c_fin[:, r, t : t + 1],
                    in1=res[:, tile_cols(j)], op0=ALU.mult, op1=ALU.add,
                )
                if (j + 1) % (N_TILES // stores) == 0:
                    cols = slice((j + 1) * N_TILE - width, (j + 1) * N_TILE)
                    nc.sync.dma_start(out=out[r * P : (r + 1) * P, t, cols], in_=res[:, cols])

        def compute_on_gpsimd(r, t, pieces):
            z_part = own.tile([P, N], F32, name="z_part")
            u_part = own.tile([P, N], F32, name="u_part")
            width = N // pieces
            for i in range(pieces):
                cols = slice(i * width, (i + 1) * width)
                nc.gpsimd.tensor_scalar(
                    out=z_part[:, cols], in0=z_sb[:, r, cols], scalar1=a_fin[:, r, t : t + 1], scalar2=0.0,
                    op0=ALU.mult, op1=ALU.add,
                )
                nc.gpsimd.tensor_scalar(
                    out=u_part[:, cols], in0=u_sb[:, r, cols], scalar1=c_fin[:, r, t : t + 1], scalar2=0.0,
                    op0=ALU.mult, op1=ALU.add,
                )
                nc.gpsimd.tensor_add(out=z_part[:, cols], in0=z_part[:, cols], in1=u_part[:, cols])
            return z_part

        for_gpsimd = [(0, T - 2), (0, T - 1), (1, T - 1)]
        for_vector = [(r, t) for r in blocks for t in range(T) if (r, t) not in for_gpsimd]
        ratio = 4
        theirs = {}
        for k in range(len(for_vector)):
            r, t = for_vector[k]
            if k % ratio == 0 and k // ratio < len(for_gpsimd):
                g = k // ratio
                theirs[g] = compute_on_gpsimd(*for_gpsimd[g], 2 if g == 0 else 1)
            emit(r, t, N_TILES if k == 0 else 2 if k < 4 else 1)
            for j in {1: (1,), 2: (2,), 3: (3,)}.get(k, ()):
                make_u(1, j)
            for g, cols in {1: ((0, half_cols(0)),), 2: ((0, half_cols(1)),), 6: ((1, slice(0, N)),), 10: ((2, slice(0, N)),)}.get(k, ()):
                rg, tg = for_gpsimd[g]
                nc.sync.dma_start(out=out[rg * P : (rg + 1) * P, tg, cols], in_=theirs[g][:, cols])
